import numpy as np
import ml_dtypes


def mxq(x, axis, fmt="e4m3"):
    dtype, down = {"e4m3": (ml_dtypes.float8_e4m3fn, 7), "e5m2": (ml_dtypes.float8_e5m2, 14)}[fmt]
    v = np.moveaxis(np.asarray(x, np.float32).astype(ml_dtypes.bfloat16).astype(np.float64), axis, -1)
    blocks = v.reshape(v.shape[:-1] + (-1, 32))
    amax = np.abs(blocks).max(-1, keepdims=True)
    byte = np.maximum(np.where(amax > 0, np.frexp(amax)[1] - 1 + 127, 0) - down, 1)
    scale = np.exp2(byte - 127.0)
    codes = (blocks / scale).astype(np.float32).astype(dtype).astype(np.float64)
    return np.moveaxis((codes * scale).reshape(v.shape), -1, axis)


WIDE = False


def mx_kscale(k):
    if not WIDE:
        return np.ones(k)
    levels = np.array([18, -18])
    if k % 512:
        return np.exp2(np.random.permutation(np.resize(levels, k // 32))).repeat(32)
    a = np.empty((k // 512, 16))
    for p in range(k // 512):
        a[p, :8] = np.random.permutation(np.resize(levels, 8))
        for g in range(8):
            far = levels[np.abs(levels - a[p, g]) >= 10]
            a[p, g + 8] = far[np.random.randint(len(far))]
    return np.exp2(a.ravel()).repeat(32)


BF16 = ml_dtypes.bfloat16


def bf(x):
    return np.asarray(x, np.float32).astype(BF16)


def f64(x):
    return np.asarray(x).astype(np.float64)


B, N, G, KT = 1, 1024, 512, 4


def preactivation(x_taps, h_taps, S, weight_A, weight_B, bias_A, bias_B):
    pre = f64(bias_A) + f64(bias_B)
    for taps, w in ((f64(x_taps), f64(weight_A)), (f64(h_taps), f64(weight_B))):
        last = taps[:, KT - 2] @ f64(S)
        z = np.concatenate([taps, last[:, None]], axis=1).reshape(B, KT * G, N)
        pre = pre + w.reshape(G, KT * G) @ z
    return pre


def setup_inputs():
    s = mx_kscale(2 * G)
    sa, sb = s[:G], s[G:]
    u = mx_kscale(G)
    v = mx_kscale(N)
    c = np.ones(KT)
    c[:KT - 1] = 1.0 / np.max(v)
    x0 = bf(np.random.standard_normal((B, KT - 1, G, N)))
    h0 = bf(np.random.standard_normal((B, KT - 1, G, N)))
    S0 = bf(np.random.standard_normal((B, N, N)) / np.sqrt(N))
    wa0 = bf(np.random.standard_normal((G, KT, G)) / np.sqrt(KT * G))
    wb0 = bf(np.random.standard_normal((G, KT, G)) / np.sqrt(KT * G))
    bias_A = bf(np.random.standard_normal(G) * 0.3)[:, None]
    bias_B = bf(np.random.standard_normal(G) * 0.3)[:, None]
    pre = preactivation(x0, h0, S0, wa0, wb0, bias_A, bias_B)
    g = np.random.standard_normal((B, G, N)) * np.exp2(np.random.randint(-6, 1, (B, 1, N))) * 8.0
    g = g * (np.abs(pre) > 1e-4)
    return {"x_taps": bf(f64(x0) * sa[None, None, :, None]),
            "h_taps": bf(f64(h0) * sb[None, None, :, None]),
            "S": bf(f64(S0) / v[None, None, :]),
            "weight_A": bf(f64(wa0) * c[None, :, None] / sa[None, None, :] / u[:, None, None]),
            "weight_B": bf(f64(wb0) / sb[None, None, :] / u[:, None, None]),
            "bias_A": bias_A,
            "bias_B": bias_B,
            "pre": np.asarray(pre, np.float32),
            "grad_out": bf(g * u[None, :, None] * v[None, None, :])}


def reference(x_taps, h_taps, S, weight_A, weight_B, bias_A, bias_B, pre, grad_out):
    dpre = f64(grad_out) * (f64(pre) > 0.0)
    w = np.concatenate([f64(weight_A).reshape(G, KT * G), f64(weight_B)[:, KT - 1]], axis=1)
    d = mxq(w, 0, "e4m3").T @ mxq(dpre, 1, "e5m2")
    d3 = d[:, (KT - 1) * G:]
    back = mxq(d3[:, :G], 2, "e5m2") @ mxq(f64(S), 2, "e4m3").transpose(0, 2, 1)
    xh = np.concatenate([f64(x_taps)[:, KT - 2], f64(h_taps)[:, KT - 2]], axis=1)
    dS = mxq(xh, 1, "e4m3").transpose(0, 2, 1) @ mxq(d3, 1, "e5m2")
    dx = np.array(d[:, :(KT - 1) * G]).reshape(B, KT - 1, G, N)
    dx[:, KT - 2] = dx[:, KT - 2] + back
    return dx, dS

@@ -1,0 +1,354 @@
+from contextlib import ExitStack
+
+import concourse.mybir as mybir
+from concourse.masks import make_identity
+
+F32 = mybir.dt.float32
+BF16 = mybir.dt.bfloat16
+U32 = mybir.dt.uint32
+U8 = mybir.dt.uint8
+E4M3 = mybir.dt.float8_e4m3fn_x4
+E5M2 = mybir.dt.float8_e5m2_x4
+IS_GT = mybir.AluOpType.is_gt
+MULT = mybir.AluOpType.mult
+
+P = 128
+PACK = 4
+FEATURES = 512
+NODES = 1024
+HALF = 512
+QUARTER = 256
+TAPS = 4
+LAST_TAP = 3
+X, H = 0, 1
+
+FLOPS = 2 * ((TAPS + 1) * FEATURES * FEATURES * NODES + FEATURES * NODES * NODES + 2 * FEATURES * NODES * NODES)
+BYTES = (
+    2 * (2 * FEATURES * NODES + NODES * NODES + (TAPS + 1) * FEATURES * FEATURES + FEATURES * NODES)
+    + 4 * FEATURES * NODES
+    + 4 * (3 * FEATURES * NODES + NODES * NODES)
+)
+
+
+def tile_graphfilterrnnbatch_pb_v_kernel(
+    tc, x_taps, h_taps, S, weight_A, weight_B, bias_A, bias_B, pre, grad_out, out_0, out_1
+):
+    nc = tc.nc
+
+    def on_vector(out, in_):
+        nc.vector.tensor_copy(out=out, in_=in_)
+
+    def on_scalar(out, in_):
+        nc.scalar.copy(out=out, in_=in_)
+
+    V, A = on_vector, on_scalar
+
+    with ExitStack() as ctx:
+        keep = ctx.enter_context(tc.tile_pool(name="keep", bufs=1))
+        groups = ctx.enter_context(tc.tile_pool(name="groups", bufs=8))
+        rows = ctx.enter_context(tc.tile_pool(name="rows", bufs=14))
+        psum = ctx.enter_context(tc.psum_pool(name="psum", bufs=8))
+
+        def half(h):
+            return slice(h * HALF, (h + 1) * HALF)
+
+        def block(i):
+            return slice(i * P, (i + 1) * P)
+
+        def by_four(ap):
+            return ap.rearrange("(p j) n -> p j n", j=PACK)
+
+        pre_sb = [keep.tile([P, PACK, HALF], F32, name="pre_%d" % h, align_bytes=64) for h in range(2)]
+        grad_sb = [keep.tile([P, PACK, HALF], BF16, name="grad_%d" % h, align_bytes=64) for h in range(2)]
+        w_sb = [keep.tile([P, PACK, FEATURES], BF16, name="w_%d" % k, align_bytes=64) for k in range(TAPS + 1)]
+        xh_sb = [keep.tile([P, PACK, NODES], BF16, name="xh_%d" % s, align_bytes=64) for s in (X, H)]
+        s_sb = [keep.tile([P, 2, NODES], BF16, name="s_%d" % c, align_bytes=64) for c in range(4)]
+
+        def load_pre(h, lo, hi):
+            nc.sync.dma_start(out=pre_sb[h][:, :, lo:hi], in_=by_four(pre[0, :, h * HALF + lo : h * HALF + hi]))
+
+        def load_grad(h, lo, hi):
+            nc.sync.dma_start(out=grad_sb[h][:, :, lo:hi], in_=by_four(grad_out[0, :, h * HALF + lo : h * HALF + hi]))
+
+        def load_w(k):
+            source = weight_A[:, k, :] if k < TAPS else weight_B[:, LAST_TAP, :]
+            nc.sync.dma_start(out=w_sb[k][:], in_=by_four(source))
+
+        def load_xh(s):
+            source = x_taps if s == X else h_taps
+            nc.sync.dma_start(out=xh_sb[s][:], in_=by_four(source[0, 2, :, :]))
+
+        def load_s(c):
+            nc.sync.dma_start(
+                out=s_sb[c][:], in_=S[0, 2 * P * c : 2 * P * (c + 1), :].rearrange("(r p) n -> p r n", p=P)
+            )
+
+        load_w(1)
+        load_w(3)
+        load_grad(0, 0, QUARTER)
+        load_pre(0, 0, QUARTER)
+        load_pre(0, QUARTER, HALF)
+        load_grad(0, QUARTER, HALF)
+        load_w(0)
+        load_w(4)
+        load_pre(1, 0, HALF)
+        load_grad(1, 0, HALF)
+        load_s(2)
+        load_s(3)
+        load_xh(X)
+        load_w(2)
+        load_xh(H)
+        load_s(0)
+        load_s(1)
+
+        identity = keep.tile([P, P], F32, name="identity", align_bytes=64)
+        make_identity(nc, identity[:])
+        first = keep.tile([P, 2], F32, name="first", align_bytes=64)
+        nc.vector.memset(first[:, 0:1], 0.0)
+        nc.scalar.copy(out=first[:, 1:2], in_=first[:, 0:1])
+
+        def operand(name):
+            codes = keep.tile([P, HALF], U32, name=name + "_codes", align_bytes=64)
+            scales = keep.tile([P, HALF], U8, name=name + "_scales", align_bytes=64)
+            return codes, scales
+
+        w_q = [operand("wq_%d" % k) for k in range(TAPS + 1)]
+        dpre_q = [operand("dpre_%d" % h) for h in range(2)]
+        xh_q = [[operand("xhq_%d%d" % (s, h)) for h in range(2)] for s in (X, H)]
+        d3_q = [[operand("d3q_%d%d" % (s, h)) for h in range(2)] for s in (X, H)]
+        dx3t_q = [operand("dx3t_%d" % g) for g in range(2)]
+        st_q = [[operand("st_%d%d" % (g, h)) for h in range(2)] for g in range(2)]
+
+        def new_group():
+            group = groups.tile([P, HALF, PACK], BF16, name="group", align_bytes=64)
+            return group
+
+        def quantise(target, group, dtype):
+            nc.vector.quantize_mx(
+                out=target[0][:].bitcast(dtype), scales=target[1][:], in_=group[:].rearrange("p c j -> p (c j)")
+            )
+
+        def matmul(bank, left, columns, left_dtype, right, right_dtype, start, stop):
+            nc.tensor.matmul_mx(
+                out=bank[:],
+                lhsT=left[0][:, columns].bitcast(left_dtype),
+                lhsT_scale=left[1][:, columns],
+                rhs=right[0][:].bitcast(right_dtype),
+                rhs_scale=right[1][:],
+                start=start,
+                stop=stop,
+            )
+
+        def new_bank():
+            bank = psum.tile([P, HALF], F32, name="bank")
+            return bank
+
+        def interleave(engine, group, source):
+            engine(group.rearrange("p (c i) j -> p c j i", i=4), source.rearrange("p j (c i) -> p c j i", i=4))
+
+        def mask(group, h, lo, hi):
+            nc.vector.scalar_tensor_tensor(
+                out=group[:, lo:hi, :],
+                in0=pre_sb[h][:, :, lo:hi].rearrange("p j c -> p c j"),
+                scalar=0.0,
+                in1=grad_sb[h][:, :, lo:hi].rearrange("p j c -> p c j"),
+                op0=IS_GT,
+                op1=MULT,
+            )
+
+        def mix_w(k, engine):
+            group = new_group()
+            if k < 2:
+                interleave(engine, group[:], w_sb[k][:])
+            else:
+                engine(
+                    group[:].rearrange("p (t m) j -> p t m j", t=4), w_sb[k][:].rearrange("p j (m t) -> p t m j", t=4)
+                )
+            return lambda: quantise(w_q[k], group, E4M3)
+
+        def mix_xh(s, h, engine):
+            group = new_group()
+            interleave(engine, group[:], xh_sb[s][:, :, half(h)])
+            return lambda: quantise(xh_q[s][h], group, E4M3)
+
+        d3_sb = [
+            [keep.tile([P, PACK, HALF], BF16, name="d3_%d%d" % (s, h), align_bytes=64) for h in range(2)] for s in (X, H)
+        ]
+
+        def make_d3(s, h, engines):
+            for t in range(PACK):
+                bank = new_bank()
+                matmul(bank, w_q[LAST_TAP + s], block(t), E4M3, dpre_q[h], E5M2, True, True)
+                engines[t](
+                    d3_sb[s][h][:, t, :].rearrange("p (u q e) -> p u q e", u=2, e=2),
+                    bank[:].rearrange("p (q u e) -> p u q e", u=2, e=2),
+                )
+
+        def mix_d3(s, h, engine):
+            group = new_group()
+            interleave(engine, group[:], d3_sb[s][h][:])
+            return lambda: quantise(d3_q[s][h], group, E5M2)
+
+        def words_of(tile):
+            return tile[:].rearrange("p a b -> p (a b)").bitcast(F32)
+
+        def transpose_dx3(h, engines):
+            words = words_of(d3_sb[X][h])
+            group = new_group()
+            pairs = words_of(group).rearrange("p (c u) -> p c u", u=2)
+            for b in range(2):
+                bank = psum.tile([P, 2, 2, P], F32, name="bank")
+                for i in range(2):
+                    for u in range(2):
+                        nc.tensor.transpose(bank[:, i, u, :], words[:, block(4 * b + 2 * i + u)], identity[:])
+                engines[b](
+                    pairs[:, 2 * P * b : 2 * P * (b + 1), :].rearrange("p (i c) u -> p i c u", i=2),
+                    bank[:].rearrange("p i u c -> p i c u"),
+                )
+            return lambda: quantise(dx3t_q[h], group, E5M2)
+
+        def transpose_s(g, h, engines):
+            group = new_group()
+            pairs = words_of(group).rearrange("p (c u) -> p c u", u=2)
+            for b in range(2):
+                words = words_of(s_sb[2 * h + b])
+                bank = psum.tile([P, 2, 2, P], F32, name="bank")
+                for r in range(2):
+                    for u in range(2):
+                        low = (r * NODES + g * HALF) // 2
+                        nc.tensor.transpose(bank[:, r, u, :], words[:, low + u : low + 2 * P : 2], identity[:])
+                engines[b](
+                    pairs[:, 2 * P * b : 2 * P * (b + 1), :].rearrange("p (r c) u -> p r c u", r=2),
+                    bank[:].rearrange("p r u c -> p r c u"),
+                )
+            return lambda: quantise(st_q[g][h], group, E4M3)
+
+        open_rows = {}
+
+        def emit(key, h, engine, bank, target, pair_order=False, by_halves=False):
+            first_half = key not in open_rows
+            if first_half:
+                open_rows[key] = rows.tile([P, NODES], F32, name="row", align_bytes=64)
+            row = open_rows[key]
+            if pair_order:
+                engine(
+                    row[:, half(h)].rearrange("p (q u e) -> p q u e", u=2, e=2),
+                    bank[:].rearrange("p (u q e) -> p q u e", u=2, e=2),
+                )
+            else:
+                engine(row[:, half(h)], bank[:])
+            if by_halves:
+                nc.sync.dma_start(out=target[:, half(h)], in_=row[:, half(h)])
+            elif not first_half:
+                nc.sync.dma_start(out=target, in_=row[:])
+
+        def direct(tap, i, h, engine):
+            bank = new_bank()
+            matmul(bank, w_q[tap], block(i), E4M3, dpre_q[h], E5M2, True, True)
+            emit((tap, i), h, engine, bank, out_0[0, tap, block(i), :])
+
+        tap2_rows = out_0[0, 2, :, :].rearrange("(p t) n -> p t n", t=PACK)
+
+        def tap2(t, h, engine):
+            bank = new_bank()
+            matmul(bank, w_q[2], block(t), E4M3, dpre_q[h], E5M2, True, False)
+            matmul(bank, dx3t_q[0], block(t), E5M2, st_q[0][h], E4M3, False, False)
+            matmul(bank, dx3t_q[1], block(t), E5M2, st_q[1][h], E4M3, False, True)
+            emit((2, t), h, engine, bank, tap2_rows[:, t, :], by_halves=t == PACK - 1)
+
+        def shift(i, h, engine):
+            bank = new_bank()
+            for s in (X, H):
+                matmul(bank, xh_q[s][i // 4], block(i % 4), E4M3, d3_q[s][h], E5M2, s == X, s == H)
+            emit(("shift", i), h, engine, bank, out_1[0, block(i), :], pair_order=True)
+
+        with tc.manual_schedule():
+            quantise_w3 = mix_w(3, A)
+            quantise_w1 = mix_w(1, V)
+            quantise_w1()
+            dpre_0 = new_group()
+            mask(dpre_0, 0, 0, QUARTER)
+            quantise_w3()
+            quantise_w0 = mix_w(0, A)
+            mask(dpre_0, 0, QUARTER, HALF)
+            quantise(dpre_q[0], dpre_0, E5M2)
+            quantise_w4 = mix_w(4, V)
+            make_d3(X, 0, (A, V, A, A))
+            direct(1, 0, 0, A)
+            quantise_w4()
+            quantise_w0()
+            direct(1, 1, 0, A)
+            direct(1, 2, 0, V)
+            make_d3(H, 0, (A, A, A, A))
+            quantise_dx0 = transpose_dx3(0, (A, A))
+            dpre_1 = new_group()
+            mask(dpre_1, 1, 0, HALF)
+            quantise_st01 = transpose_s(0, 1, (V, A))
+            quantise(dpre_q[1], dpre_1, E5M2)
+            direct(1, 3, 0, A)
+            direct(1, 0, 1, A)
+            quantise_d3h0 = mix_d3(H, 0, V)
+            direct(1, 1, 1, A)
+            quantise_d3x0 = mix_d3(X, 0, V)
+            quantise_d3h0()
+            quantise_x0 = mix_xh(X, 0, V)
+            direct(1, 2, 1, A)
+            make_d3(X, 1, (A, A, A, A))
+            quantise_d3x0()
+            quantise_h0 = mix_xh(H, 0, V)
+            quantise_d3x1 = mix_d3(X, 1, V)
+            quantise_st11 = transpose_s(1, 1, (A, A))
+            quantise_x0()
+            make_d3(H, 1, (A, V, A, A))
+            quantise_h0()
+            quantise_d3h1 = mix_d3(H, 1, V)
+            direct(1, 3, 1, A)
+            quantise_d3x1()
+            quantise_dx1 = transpose_dx3(1, (A, A))
+            direct(0, 0, 0, A)
+            quantise_d3h1()
+            quantise_h1 = mix_xh(H, 1, V)
+            quantise_st00 = transpose_s(0, 0, (A, V))
+            quantise_x1 = mix_xh(X, 1, V)
+            direct(0, 1, 0, A)
+            direct(0, 0, 1, A)
+            quantise_h1()
+            direct(0, 1, 1, A)
+            quantise_x1()
+            quantise_st10 = transpose_s(1, 0, (A, V))
+            quantise_w2 = mix_w(2, V)
+            shift(0, 0, A)
+            shift(0, 1, A)
+            shift(1, 0, A)
+            shift(1, 1, A)
+            shift(2, 0, A)
+            shift(2, 1, A)
+            shift(3, 0, A)
+            quantise_dx0()
+            quantise_st10()
+            shift(3, 1, A)
+            direct(0, 2, 0, A)
+            direct(0, 2, 1, A)
+            shift(4, 0, A)
+            quantise_dx1()
+            shift(4, 1, A)
+            shift(5, 0, A)
+            quantise_w2()
+            quantise_st00()
+            quantise_st11()
+            quantise_st01()
+            shift(5, 1, A)
+            shift(6, 0, A)
+            shift(6, 1, A)
+            shift(7, 0, V)
+            shift(7, 1, A)
+            direct(0, 3, 0, V)
+            direct(0, 3, 1, A)
+            tap2(0, 0, A)
+            tap2(0, 1, V)
+            tap2(1, 0, A)
+            tap2(1, 1, V)
+            tap2(2, 0, V)
+            tap2(2, 1, V)
+            tap2(3, 0, V)
+            tap2(3, 1, V)

@@ -20,6 +20,8 @@ HALF = 512
 QUARTER = 256
 TAPS = 4
 LAST_TAP = 3
+GROUP_BUFS = 6
+ROW_BUFS = 7
 X, H = 0, 1
 
 FLOPS = 2 * ((TAPS + 1) * FEATURES * FEATURES * NODES + FEATURES * NODES * NODES + 2 * FEATURES * NODES * NODES)
@@ -45,67 +47,40 @@ def tile_graphfilterrnnbatch_pb_v_kernel(
 
     with ExitStack() as ctx:
         keep = ctx.enter_context(tc.tile_pool(name="keep", bufs=1))
-        groups = ctx.enter_context(tc.tile_pool(name="groups", bufs=8))
-        rows = ctx.enter_context(tc.tile_pool(name="rows", bufs=14))
+        groups = ctx.enter_context(tc.tile_pool(name="groups", bufs=GROUP_BUFS))
+        rows = ctx.enter_context(tc.tile_pool(name="rows", bufs=ROW_BUFS))
         psum = ctx.enter_context(tc.psum_pool(name="psum", bufs=8))
 
         def half(h):
             return slice(h * HALF, (h + 1) * HALF)
 
+        def quarter(q):
+            return slice(q * QUARTER, (q + 1) * QUARTER)
+
         def block(i):
             return slice(i * P, (i + 1) * P)
 
-        def by_four(ap):
-            return ap.rearrange("(p j) n -> p j n", j=PACK)
+        def load(name, source, dtype):
+            tile = keep.tile([P, PACK, source.shape[-1]], dtype, name=name, align_bytes=64)
+            nc.sync.dma_start(out=tile[:], in_=source.rearrange("(p j) n -> p j n", j=PACK))
+            return tile
 
-        pre_sb = [keep.tile([P, PACK, HALF], F32, name="pre_%d" % h, align_bytes=64) for h in range(2)]
-        grad_sb = [keep.tile([P, PACK, HALF], BF16, name="grad_%d" % h, align_bytes=64) for h in range(2)]
-        w_sb = [keep.tile([P, PACK, FEATURES], BF16, name="w_%d" % k, align_bytes=64) for k in range(TAPS + 1)]
-        xh_sb = [keep.tile([P, PACK, NODES], BF16, name="xh_%d" % s, align_bytes=64) for s in (X, H)]
-        s_sb = [keep.tile([P, 2, NODES], BF16, name="s_%d" % c, align_bytes=64) for c in range(4)]
+        taps_a = weight_A.rearrange("k t c -> k (t c)")
 
-        def load_pre(h, lo, hi):
-            nc.sync.dma_start(out=pre_sb[h][:, :, lo:hi], in_=by_four(pre[0, :, h * HALF + lo : h * HALF + hi]))
-
-        def load_grad(h, lo, hi):
-            nc.sync.dma_start(out=grad_sb[h][:, :, lo:hi], in_=by_four(grad_out[0, :, h * HALF + lo : h * HALF + hi]))
-
-        def load_w(k):
-            source = weight_A[:, k, :] if k < TAPS else weight_B[:, LAST_TAP, :]
-            nc.sync.dma_start(out=w_sb[k][:], in_=by_four(source))
-
-        def load_xh(s):
-            source = x_taps if s == X else h_taps
-            nc.sync.dma_start(out=xh_sb[s][:], in_=by_four(source[0, 2, :, :]))
-
-        def load_s(c):
-            nc.sync.dma_start(
-                out=s_sb[c][:], in_=S[0, 2 * P * c : 2 * P * (c + 1), :].rearrange("(r p) n -> p r n", p=P)
-            )
-
-        load_w(1)
-        load_w(3)
-        load_grad(0, 0, QUARTER)
-        load_pre(0, 0, QUARTER)
-        load_pre(0, QUARTER, HALF)
-        load_grad(0, QUARTER, HALF)
-        load_w(0)
-        load_w(4)
-        load_pre(1, 0, HALF)
-        load_grad(1, 0, HALF)
-        load_s(2)
-        load_s(3)
-        load_xh(X)
-        load_w(2)
-        load_xh(H)
-        load_s(0)
-        load_s(1)
+        pre_0 = [load("pre_00", pre[0, :, quarter(0)], F32)]
+        grad_sb = [load("grad_0", grad_out[0, :, half(0)], BF16)]
+        pre_0.append(load("pre_01", pre[0, :, quarter(1)], F32))
+        w_3 = load("w_3", weight_A[:, LAST_TAP, :], BF16)
+        w_b = load("w_b", weight_B[:, LAST_TAP, :], BF16)
+        grad_sb.append(load("grad_1", grad_out[0, :, half(1)], BF16))
+        pre_1 = load("pre_1", pre[0, :, half(1)], F32)
+        w_012 = load("w_012", taps_a[:, 0 : LAST_TAP * FEATURES], BF16)
+        s_sb = [load("s_%d" % h, S[0, half(h), :], BF16) for h in range(2)]
+        xh_sb = [load("x", x_taps[0, 2, :, :], BF16), load("h", h_taps[0, 2, :, :], BF16)]
+        w_sb = [w_012[:, :, k * FEATURES : (k + 1) * FEATURES] for k in range(LAST_TAP)] + [w_3[:], w_b[:]]
 
         identity = keep.tile([P, P], F32, name="identity", align_bytes=64)
         make_identity(nc, identity[:])
-        first = keep.tile([P, 2], F32, name="first", align_bytes=64)
-        nc.vector.memset(first[:, 0:1], 0.0)
-        nc.scalar.copy(out=first[:, 1:2], in_=first[:, 0:1])
 
         def operand(name):
             codes = keep.tile([P, HALF], U32, name=name + "_codes", align_bytes=64)
@@ -114,7 +89,7 @@ def tile_graphfilterrnnbatch_pb_v_kernel(
 
         w_q = [operand("wq_%d" % k) for k in range(TAPS + 1)]
         dpre_q = [operand("dpre_%d" % h) for h in range(2)]
-        xh_q = [[operand("xhq_%d%d" % (s, h)) for h in range(2)] for s in (X, H)]
+        xh_q = [operand("xhq_%d" % g) for g in range(4)]
         d3_q = [[operand("d3q_%d%d" % (s, h)) for h in range(2)] for s in (X, H)]
         dx3t_q = [operand("dx3t_%d" % g) for g in range(2)]
         st_q = [[operand("st_%d%d" % (g, h)) for h in range(2)] for g in range(2)]
@@ -146,30 +121,38 @@ def tile_graphfilterrnnbatch_pb_v_kernel(
         def interleave(engine, group, source):
             engine(group.rearrange("p (c i) j -> p c j i", i=4), source.rearrange("p j (c i) -> p c j i", i=4))
 
-        def mask(group, h, lo, hi):
-            nc.vector.scalar_tensor_tensor(
-                out=group[:, lo:hi, :],
-                in0=pre_sb[h][:, :, lo:hi].rearrange("p j c -> p c j"),
-                scalar=0.0,
-                in1=grad_sb[h][:, :, lo:hi].rearrange("p j c -> p c j"),
-                op0=IS_GT,
-                op1=MULT,
+        def interleave_by_two(engine, group, source):
+            engine(
+                group.rearrange("p (t c i) j -> p c j i t", t=2, i=2),
+                source.rearrange("p j (c i t) -> p c j i t", t=2, i=2),
             )
+
+        def interleave_by_four(engine, group, source, part=slice(0, 4)):
+            engine(
+                group.rearrange("p (t m) j -> p t m j", t=4)[:, part],
+                source.rearrange("p j (m t) -> p t m j", t=4)[:, part],
+            )
+
+        def mask(pre_part, grad_part, name):
+            masked = keep.tile([P, PACK, pre_part.shape[-1]], BF16, name=name, align_bytes=64)
+            nc.vector.scalar_tensor_tensor(
+                out=masked[:], in0=pre_part, scalar=0.0, in1=grad_part, op0=IS_GT, op1=MULT
+            )
+            return masked
 
         def mix_w(k, engine):
             group = new_group()
             if k < 2:
-                interleave(engine, group[:], w_sb[k][:])
+                interleave_by_two(engine, group[:], w_sb[k])
             else:
-                engine(
-                    group[:].rearrange("p (t m) j -> p t m j", t=4), w_sb[k][:].rearrange("p j (m t) -> p t m j", t=4)
-                )
+                interleave_by_four(engine, group[:], w_sb[k])
             return lambda: quantise(w_q[k], group, E4M3)
 
-        def mix_xh(s, h, engine):
+        def mix_xh(g, engines):
             group = new_group()
-            interleave(engine, group[:], xh_sb[s][:, :, half(h)])
-            return lambda: quantise(xh_q[s][h], group, E4M3)
+            for s in (X, H):
+                interleave_by_two(engines[s], group[:, quarter(s), :], xh_sb[s][:, :, quarter(g)])
+            return lambda: quantise(xh_q[g], group, E4M3)
 
         d3_sb = [
             [keep.tile([P, PACK, HALF], BF16, name="d3_%d%d" % (s, h), align_bytes=64) for h in range(2)] for s in (X, H)
@@ -208,147 +191,135 @@ def tile_graphfilterrnnbatch_pb_v_kernel(
             return lambda: quantise(dx3t_q[h], group, E5M2)
 
         def transpose_s(g, h, engines):
+            words = words_of(s_sb[h])
             group = new_group()
-            pairs = words_of(group).rearrange("p (c u) -> p c u", u=2)
+            pairs = words_of(group).rearrange("p (c r u) -> p c r u", r=PACK, u=2)
             for b in range(2):
-                words = words_of(s_sb[2 * h + b])
                 bank = psum.tile([P, 2, 2, P], F32, name="bank")
-                for r in range(2):
+                for i in range(2):
                     for u in range(2):
-                        low = (r * NODES + g * HALF) // 2
-                        nc.tensor.transpose(bank[:, r, u, :], words[:, low + u : low + 2 * P : 2], identity[:])
-                engines[b](
-                    pairs[:, 2 * P * b : 2 * P * (b + 1), :].rearrange("p (r c) u -> p r c u", r=2),
-                    bank[:].rearrange("p r u c -> p r c u"),
-                )
+                        low = ((2 * b + i) * NODES + g * HALF) // 2
+                        nc.tensor.transpose(bank[:, i, u, :], words[:, low + u : low + 2 * P : 2], identity[:])
+                engines[b](pairs[:, :, 2 * b : 2 * b + 2, :], bank[:].rearrange("p i u c -> p c i u"))
             return lambda: quantise(st_q[g][h], group, E4M3)
 
         open_rows = {}
 
-        def emit(key, h, engine, bank, target, pair_order=False, by_halves=False):
-            first_half = key not in open_rows
-            if first_half:
-                open_rows[key] = rows.tile([P, NODES], F32, name="row", align_bytes=64)
-            row = open_rows[key]
+        def emit(key, t, h, engine, bank, target, pair_order=False, pieces=False):
+            if key not in open_rows:
+                open_rows[key] = [rows.tile([P, 2, NODES], F32, name="row", align_bytes=64), 0]
+            row = open_rows[key][0]
+            open_rows[key][1] = open_rows[key][1] + 1
             if pair_order:
                 engine(
-                    row[:, half(h)].rearrange("p (q u e) -> p q u e", u=2, e=2),
+                    row[:, t, half(h)].rearrange("p (q u e) -> p q u e", u=2, e=2),
                     bank[:].rearrange("p (u q e) -> p q u e", u=2, e=2),
                 )
             else:
-                engine(row[:, half(h)], bank[:])
-            if by_halves:
-                nc.sync.dma_start(out=target[:, half(h)], in_=row[:, half(h)])
-            elif not first_half:
+                engine(row[:, t, half(h)], bank[:])
+            if pieces:
+                if open_rows[key][1] % 2 == 0:
+                    nc.sync.dma_start(out=target[:, t, :], in_=row[:, t, :])
+            elif open_rows[key][1] == 4:
                 nc.sync.dma_start(out=target, in_=row[:])
 
-        def direct(tap, i, h, engine):
+        def by_two(rows_256):
+            return rows_256.rearrange("(p t) n -> p t n", t=2)
+
+        def direct(tap, g, t, h, engine, pieces=False):
             bank = new_bank()
-            matmul(bank, w_q[tap], block(i), E4M3, dpre_q[h], E5M2, True, True)
-            emit((tap, i), h, engine, bank, out_0[0, tap, block(i), :])
+            matmul(bank, w_q[tap], block(2 * t + g), E4M3, dpre_q[h], E5M2, True, True)
+            emit((tap, g), t, h, engine, bank, by_two(out_0[0, tap, 2 * P * g : 2 * P * (g + 1), :]), pieces=pieces)
 
         tap2_rows = out_0[0, 2, :, :].rearrange("(p t) n -> p t n", t=PACK)
 
-        def tap2(t, h, engine):
+        def tap2(g, t, h, engine, pieces=False):
             bank = new_bank()
-            matmul(bank, w_q[2], block(t), E4M3, dpre_q[h], E5M2, True, False)
-            matmul(bank, dx3t_q[0], block(t), E5M2, st_q[0][h], E4M3, False, False)
-            matmul(bank, dx3t_q[1], block(t), E5M2, st_q[1][h], E4M3, False, True)
-            emit((2, t), h, engine, bank, tap2_rows[:, t, :], by_halves=t == PACK - 1)
+            matmul(bank, w_q[2], block(2 * g + t), E4M3, dpre_q[h], E5M2, True, False)
+            matmul(bank, dx3t_q[0], block(2 * g + t), E5M2, st_q[0][h], E4M3, False, False)
+            matmul(bank, dx3t_q[1], block(2 * g + t), E5M2, st_q[1][h], E4M3, False, True)
+            emit((2, g), t, h, engine, bank, tap2_rows[:, 2 * g : 2 * g + 2, :], pieces=pieces)
 
-        def shift(i, h, engine):
+        def shift(g, t, h, engine, pieces=False):
             bank = new_bank()
             for s in (X, H):
-                matmul(bank, xh_q[s][i // 4], block(i % 4), E4M3, d3_q[s][h], E5M2, s == X, s == H)
-            emit(("shift", i), h, engine, bank, out_1[0, block(i), :], pair_order=True)
+                matmul(bank, xh_q[g], block(2 * s + t), E4M3, d3_q[s][h], E5M2, s == X, s == H)
+            target = by_two(out_1[0, 2 * P * g : 2 * P * (g + 1), :])
+            emit(("shift", g), t, h, engine, bank, target, pair_order=True, pieces=pieces)
 
         with tc.manual_schedule():
-            quantise_w3 = mix_w(3, A)
-            quantise_w1 = mix_w(1, V)
-            quantise_w1()
+            all_scalar = (A, A, A, A)
+
+            def tap_rows(tap, g):
+                for h in range(2):
+                    for t in range(2):
+                        direct(tap, g, t, h, A)
+
+            def shared(k):
+                group = new_group()
+                interleave_by_four(A, group[:], w_sb[k], slice(0, 2))
+                interleave_by_four(V, group[:], w_sb[k], slice(2, 4))
+                return lambda: quantise(w_q[k], group, E4M3)
+
             dpre_0 = new_group()
-            mask(dpre_0, 0, 0, QUARTER)
-            quantise_w3()
-            quantise_w0 = mix_w(0, A)
-            mask(dpre_0, 0, QUARTER, HALF)
+            for q in range(2):
+                masked = mask(pre_0[q][:], grad_sb[0][:, :, quarter(q)], "masked_0%d" % q)
+                interleave((A, V)[q], dpre_0[:, quarter(q), :], masked[:])
+            quantise_w3 = shared(3)
             quantise(dpre_q[0], dpre_0, E5M2)
+            quantise_w3()
             quantise_w4 = mix_w(4, V)
-            make_d3(X, 0, (A, V, A, A))
-            direct(1, 0, 0, A)
+            make_d3(X, 0, all_scalar)
             quantise_w4()
-            quantise_w0()
-            direct(1, 1, 0, A)
-            direct(1, 2, 0, V)
-            make_d3(H, 0, (A, A, A, A))
+            make_d3(H, 0, all_scalar)
+            masked = mask(pre_1[:], grad_sb[1][:], "masked_1")
             quantise_dx0 = transpose_dx3(0, (A, A))
             dpre_1 = new_group()
-            mask(dpre_1, 1, 0, HALF)
-            quantise_st01 = transpose_s(0, 1, (V, A))
-            quantise(dpre_q[1], dpre_1, E5M2)
-            direct(1, 3, 0, A)
-            direct(1, 0, 1, A)
-            quantise_d3h0 = mix_d3(H, 0, V)
-            direct(1, 1, 1, A)
-            quantise_d3x0 = mix_d3(X, 0, V)
-            quantise_d3h0()
-            quantise_x0 = mix_xh(X, 0, V)
-            direct(1, 2, 1, A)
-            make_d3(X, 1, (A, A, A, A))
-            quantise_d3x0()
-            quantise_h0 = mix_xh(H, 0, V)
-            quantise_d3x1 = mix_d3(X, 1, V)
-            quantise_st11 = transpose_s(1, 1, (A, A))
-            quantise_x0()
-            make_d3(H, 1, (A, V, A, A))
-            quantise_h0()
-            quantise_d3h1 = mix_d3(H, 1, V)
-            direct(1, 3, 1, A)
-            quantise_d3x1()
-            quantise_dx1 = transpose_dx3(1, (A, A))
-            direct(0, 0, 0, A)
-            quantise_d3h1()
-            quantise_h1 = mix_xh(H, 1, V)
-            quantise_st00 = transpose_s(0, 0, (A, V))
-            quantise_x1 = mix_xh(X, 1, V)
-            direct(0, 1, 0, A)
-            direct(0, 0, 1, A)
-            quantise_h1()
-            direct(0, 1, 1, A)
-            quantise_x1()
-            quantise_st10 = transpose_s(1, 0, (A, V))
-            quantise_w2 = mix_w(2, V)
-            shift(0, 0, A)
-            shift(0, 1, A)
-            shift(1, 0, A)
-            shift(1, 1, A)
-            shift(2, 0, A)
-            shift(2, 1, A)
-            shift(3, 0, A)
+            interleave(V, dpre_1[:], masked[:])
             quantise_dx0()
-            quantise_st10()
-            shift(3, 1, A)
-            direct(0, 2, 0, A)
-            direct(0, 2, 1, A)
-            shift(4, 0, A)
-            quantise_dx1()
-            shift(4, 1, A)
-            shift(5, 0, A)
+            quantise(dpre_q[1], dpre_1, E5M2)
+            quantise_w1 = mix_w(1, A)
+            quantise_w0 = mix_w(0, V)
+            make_d3(X, 1, all_scalar)
+            quantise_w1()
+            quantise_w2 = mix_w(2, V)
+            quantise_w0()
+            quantise_s = [transpose_s(0, 0, (V, V))]
             quantise_w2()
-            quantise_st00()
-            quantise_st11()
-            quantise_st01()
-            shift(5, 1, A)
-            shift(6, 0, A)
-            shift(6, 1, A)
-            shift(7, 0, V)
-            shift(7, 1, A)
-            direct(0, 3, 0, V)
-            direct(0, 3, 1, A)
-            tap2(0, 0, A)
-            tap2(0, 1, V)
-            tap2(1, 0, A)
-            tap2(1, 1, V)
-            tap2(2, 0, V)
-            tap2(2, 1, V)
-            tap2(3, 0, V)
-            tap2(3, 1, V)
+            tap_rows(1, 0)
+            quantise_s.append(transpose_s(1, 0, (V, V)))
+            quantise_s[0]()
+            tap_rows(1, 1)
+            quantise_s.append(transpose_s(0, 1, (V, V)))
+            quantise_s[1]()
+            quantise_dx1 = transpose_dx3(1, (A, A))
+            quantise_d3 = [mix_d3(X, 0, V)]
+            quantise_s[2]()
+            tap_rows(0, 0)
+            quantise_dx1()
+            quantise_s.append(transpose_s(1, 1, (A, A)))
+            quantise_d3.append(mix_d3(H, 0, V))
+            quantise_d3[0]()
+            tap_rows(0, 1)
+            quantise_s[3]()
+            quantise_d3.append(mix_d3(X, 1, V))
+            quantise_d3[1]()
+            make_d3(H, 1, all_scalar)
+            quantise_xh = mix_xh(0, (V, V))
+            quantise_d3[2]()
+            quantise_d3.append(mix_d3(H, 1, V))
+            quantise_xh()
+            for g in range(2):
+                for h in range(2):
+                    for t in range(2):
+                        tap2(g, t, h, A)
+            quantise_xh = mix_xh(1, (V, V))
+            quantise_d3[3]()
+            for g in range(4):
+                if g > 0:
+                    quantise_xh()
+                if 0 < g < 3:
+                    quantise_xh = mix_xh(g + 1, (V, V))
+                for t in range(2):
+                    for h in range(2):
+                        shift(g, t, h, A if g < 3 else (A, V)[h], pieces=g == 3)

@@ -21,7 +21,7 @@ QUARTER = 256
 TAPS = 4
 LAST_TAP = 3
 GROUP_BUFS = 6
-ROW_BUFS = 7
+ROW_BUFS = 14
 X, H = 0, 1
 
 FLOPS = 2 * ((TAPS + 1) * FEATURES * FEATURES * NODES + FEATURES * NODES * NODES + 2 * FEATURES * NODES * NODES)
@@ -67,17 +67,24 @@ def tile_graphfilterrnnbatch_pb_v_kernel(
 
         taps_a = weight_A.rearrange("k t c -> k (t c)")
 
-        pre_0 = [load("pre_00", pre[0, :, quarter(0)], F32)]
-        grad_sb = [load("grad_0", grad_out[0, :, half(0)], BF16)]
-        pre_0.append(load("pre_01", pre[0, :, quarter(1)], F32))
+        pre_0a = load("pre_0a", pre[0, :, quarter(0)], F32)
+        grad_0 = load("grad_0", grad_out[0, :, half(0)], BF16)
+        pre_0b = load("pre_0b", pre[0, :, quarter(1)], F32)
         w_3 = load("w_3", weight_A[:, LAST_TAP, :], BF16)
         w_b = load("w_b", weight_B[:, LAST_TAP, :], BF16)
-        grad_sb.append(load("grad_1", grad_out[0, :, half(1)], BF16))
-        pre_1 = load("pre_1", pre[0, :, half(1)], F32)
+        grad_1 = load("grad_1", grad_out[0, :, half(1)], BF16)
+        pre_1a = load("pre_1a", pre[0, :, quarter(2)], F32)
+        pre_1b = load("pre_1b", pre[0, :, quarter(3)], F32)
         w_012 = load("w_012", taps_a[:, 0 : LAST_TAP * FEATURES], BF16)
-        s_sb = [load("s_%d" % h, S[0, half(h), :], BF16) for h in range(2)]
-        xh_sb = [load("x", x_taps[0, 2, :, :], BF16), load("h", h_taps[0, 2, :, :], BF16)]
-        w_sb = [w_012[:, :, k * FEATURES : (k + 1) * FEATURES] for k in range(LAST_TAP)] + [w_3[:], w_b[:]]
+        s_0 = load("s_0", S[0, half(0), :], BF16)
+        s_1 = load("s_1", S[0, half(1), :], BF16)
+        x_sb = load("x", x_taps[0, 2, :, :], BF16)
+        h_sb = load("h", h_taps[0, 2, :, :], BF16)
+        pre_parts = [pre_0a[:], pre_0b[:], pre_1a[:], pre_1b[:]]
+        grad_parts = [(grad_0, grad_1)[q // 2][:, :, quarter(q % 2)] for q in range(4)]
+        s_sb = [s_0, s_1]
+        xh_sb = [x_sb, h_sb]
+        w_sb = [w_012[:, :, half(k)] for k in range(LAST_TAP)] + [w_3[:], w_b[:]]
 
         identity = keep.tile([P, P], F32, name="identity", align_bytes=64)
         make_identity(nc, identity[:])
@@ -121,12 +128,6 @@ def tile_graphfilterrnnbatch_pb_v_kernel(
         def interleave(engine, group, source):
             engine(group.rearrange("p (c i) j -> p c j i", i=4), source.rearrange("p j (c i) -> p c j i", i=4))
 
-        def interleave_by_two(engine, group, source):
-            engine(
-                group.rearrange("p (t c i) j -> p c j i t", t=2, i=2),
-                source.rearrange("p j (c i t) -> p c j i t", t=2, i=2),
-            )
-
         def interleave_by_four(engine, group, source, part=slice(0, 4)):
             engine(
                 group.rearrange("p (t m) j -> p t m j", t=4)[:, part],
@@ -143,7 +144,7 @@ def tile_graphfilterrnnbatch_pb_v_kernel(
         def mix_w(k, engine):
             group = new_group()
             if k < 2:
-                interleave_by_two(engine, group[:], w_sb[k])
+                interleave(engine, group[:], w_sb[k])
             else:
                 interleave_by_four(engine, group[:], w_sb[k])
             return lambda: quantise(w_q[k], group, E4M3)
@@ -151,7 +152,7 @@ def tile_graphfilterrnnbatch_pb_v_kernel(
         def mix_xh(g, engines):
             group = new_group()
             for s in (X, H):
-                interleave_by_two(engines[s], group[:, quarter(s), :], xh_sb[s][:, :, quarter(g)])
+                interleave(engines[s], group[:, quarter(s), :], xh_sb[s][:, :, quarter(g)])
             return lambda: quantise(xh_q[g], group, E4M3)
 
         d3_sb = [
@@ -203,123 +204,117 @@ def tile_graphfilterrnnbatch_pb_v_kernel(
                 engines[b](pairs[:, :, 2 * b : 2 * b + 2, :], bank[:].rearrange("p i u c -> p c i u"))
             return lambda: quantise(st_q[g][h], group, E4M3)
 
-        open_rows = {}
+        def emit(make_bank, engines, target, pair_order=False):
+            row = rows.tile([P, NODES], F32, name="row", align_bytes=64)
+            for h in range(2):
+                bank = make_bank(h)
+                if pair_order:
+                    engines[h](
+                        row[:, half(h)].rearrange("p (q u e) -> p q u e", u=2, e=2),
+                        bank[:].rearrange("p (u q e) -> p q u e", u=2, e=2),
+                    )
+                else:
+                    engines[h](row[:, half(h)], bank[:])
+            nc.sync.dma_start(out=target, in_=row[:])
 
-        def emit(key, t, h, engine, bank, target, pair_order=False, pieces=False):
-            if key not in open_rows:
-                open_rows[key] = [rows.tile([P, 2, NODES], F32, name="row", align_bytes=64), 0]
-            row = open_rows[key][0]
-            open_rows[key][1] = open_rows[key][1] + 1
-            if pair_order:
-                engine(
-                    row[:, t, half(h)].rearrange("p (q u e) -> p q u e", u=2, e=2),
-                    bank[:].rearrange("p (u q e) -> p q u e", u=2, e=2),
-                )
-            else:
-                engine(row[:, t, half(h)], bank[:])
-            if pieces:
-                if open_rows[key][1] % 2 == 0:
-                    nc.sync.dma_start(out=target[:, t, :], in_=row[:, t, :])
-            elif open_rows[key][1] == 4:
-                nc.sync.dma_start(out=target, in_=row[:])
+        def direct(tap, i, engines):
+            def make_bank(h):
+                bank = new_bank()
+                matmul(bank, w_q[tap], block(i), E4M3, dpre_q[h], E5M2, True, True)
+                return bank
 
-        def by_two(rows_256):
-            return rows_256.rearrange("(p t) n -> p t n", t=2)
-
-        def direct(tap, g, t, h, engine, pieces=False):
-            bank = new_bank()
-            matmul(bank, w_q[tap], block(2 * t + g), E4M3, dpre_q[h], E5M2, True, True)
-            emit((tap, g), t, h, engine, bank, by_two(out_0[0, tap, 2 * P * g : 2 * P * (g + 1), :]), pieces=pieces)
+            emit(make_bank, engines, out_0[0, tap, block(i), :])
 
         tap2_rows = out_0[0, 2, :, :].rearrange("(p t) n -> p t n", t=PACK)
 
-        def tap2(g, t, h, engine, pieces=False):
-            bank = new_bank()
-            matmul(bank, w_q[2], block(2 * g + t), E4M3, dpre_q[h], E5M2, True, False)
-            matmul(bank, dx3t_q[0], block(2 * g + t), E5M2, st_q[0][h], E4M3, False, False)
-            matmul(bank, dx3t_q[1], block(2 * g + t), E5M2, st_q[1][h], E4M3, False, True)
-            emit((2, g), t, h, engine, bank, tap2_rows[:, 2 * g : 2 * g + 2, :], pieces=pieces)
+        def tap2(t, engines):
+            def make_bank(h):
+                bank = new_bank()
+                matmul(bank, w_q[2], block(t), E4M3, dpre_q[h], E5M2, True, False)
+                matmul(bank, dx3t_q[0], block(t), E5M2, st_q[0][h], E4M3, False, False)
+                matmul(bank, dx3t_q[1], block(t), E5M2, st_q[1][h], E4M3, False, True)
+                return bank
 
-        def shift(g, t, h, engine, pieces=False):
-            bank = new_bank()
-            for s in (X, H):
-                matmul(bank, xh_q[g], block(2 * s + t), E4M3, d3_q[s][h], E5M2, s == X, s == H)
-            target = by_two(out_1[0, 2 * P * g : 2 * P * (g + 1), :])
-            emit(("shift", g), t, h, engine, bank, target, pair_order=True, pieces=pieces)
+            emit(make_bank, engines, tap2_rows[:, t, :])
+
+        def shift(i, engines):
+            def make_bank(h):
+                bank = new_bank()
+                for s in (X, H):
+                    matmul(bank, xh_q[i // 2], block(2 * s + i % 2), E4M3, d3_q[s][h], E5M2, s == X, s == H)
+                return bank
+
+            emit(make_bank, engines, out_1[0, block(i), :], pair_order=True)
 
         with tc.manual_schedule():
             all_scalar = (A, A, A, A)
 
             def tap_rows(tap, g):
-                for h in range(2):
-                    for t in range(2):
-                        direct(tap, g, t, h, A)
+                for i in (2 * g, 2 * g + 1):
+                    direct(tap, i, (A, A))
 
-            def shared(k):
-                group = new_group()
-                interleave_by_four(A, group[:], w_sb[k], slice(0, 2))
-                interleave_by_four(V, group[:], w_sb[k], slice(2, 4))
-                return lambda: quantise(w_q[k], group, E4M3)
-
-            dpre_0 = new_group()
+            dpre = new_group()
+            masked = [mask(pre_parts[q], grad_parts[q], "masked_%d" % q) for q in range(2)]
             for q in range(2):
-                masked = mask(pre_0[q][:], grad_sb[0][:, :, quarter(q)], "masked_0%d" % q)
-                interleave((A, V)[q], dpre_0[:, quarter(q), :], masked[:])
-            quantise_w3 = shared(3)
-            quantise(dpre_q[0], dpre_0, E5M2)
-            quantise_w3()
-            quantise_w4 = mix_w(4, V)
+                interleave((A, V)[q], dpre[:, quarter(q), :], masked[q][:])
+            w_group = new_group()
+            interleave_by_four(A, w_group[:], w_sb[3], slice(0, 2))
+            interleave_by_four(V, w_group[:], w_sb[3], slice(2, 4))
+            quantise(dpre_q[0], dpre, E5M2)
+            quantise(w_q[3], w_group, E4M3)
+            quantise_w4 = mix_w(4, A)
             make_d3(X, 0, all_scalar)
             quantise_w4()
+            dpre = new_group()
+            masked = [mask(pre_parts[2 + q], grad_parts[2 + q], "masked_%d" % q) for q in range(2)]
+            for q in range(2):
+                interleave(V, dpre[:, quarter(q), :], masked[q][:])
+            quantise_dx = transpose_dx3(0, (A, A))
             make_d3(H, 0, all_scalar)
-            masked = mask(pre_1[:], grad_sb[1][:], "masked_1")
-            quantise_dx0 = transpose_dx3(0, (A, A))
-            dpre_1 = new_group()
-            interleave(V, dpre_1[:], masked[:])
-            quantise_dx0()
-            quantise(dpre_q[1], dpre_1, E5M2)
-            quantise_w1 = mix_w(1, A)
-            quantise_w0 = mix_w(0, V)
+            quantise(dpre_q[1], dpre, E5M2)
+
+            quantise_dx()
             make_d3(X, 1, all_scalar)
-            quantise_w1()
-            quantise_w2 = mix_w(2, V)
-            quantise_w0()
-            quantise_s = [transpose_s(0, 0, (V, V))]
-            quantise_w2()
-            tap_rows(1, 0)
-            quantise_s.append(transpose_s(1, 0, (V, V)))
-            quantise_s[0]()
-            tap_rows(1, 1)
-            quantise_s.append(transpose_s(0, 1, (V, V)))
-            quantise_s[1]()
-            quantise_dx1 = transpose_dx3(1, (A, A))
-            quantise_d3 = [mix_d3(X, 0, V)]
-            quantise_s[2]()
-            tap_rows(0, 0)
-            quantise_dx1()
-            quantise_s.append(transpose_s(1, 1, (A, A)))
-            quantise_d3.append(mix_d3(H, 0, V))
-            quantise_d3[0]()
-            tap_rows(0, 1)
-            quantise_s[3]()
-            quantise_d3.append(mix_d3(X, 1, V))
-            quantise_d3[1]()
             make_d3(H, 1, all_scalar)
-            quantise_xh = mix_xh(0, (V, V))
-            quantise_d3[2]()
-            quantise_d3.append(mix_d3(H, 1, V))
+            quantise_w1 = mix_w(1, V)
+            quantise_w0 = mix_w(0, V)
+            quantise_w1()
+            quantise_w0()
+            quantise_s = transpose_s(0, 0, (V, V))
+            quantise_w2 = mix_w(2, V)
+            tap_rows(1, 0)
+            quantise_s()
+            quantise_w2()
+            quantise_s = transpose_s(1, 0, (V, V))
+            quantise_dx = transpose_dx3(1, (A, A))
+            quantise_d3 = mix_d3(H, 0, V)
+            tap_rows(1, 1)
+            quantise_s()
+            quantise_dx()
+            quantise_s = transpose_s(0, 1, (V, V))
+            quantise_d3()
+            tap_rows(0, 0)
+            quantise_s()
+            quantise_d3 = mix_d3(X, 0, V)
+            quantise_s = transpose_s(1, 1, (A, A))
+            quantise_s()
+            quantise_d3x = mix_d3(X, 1, V)
+            quantise_d3()
+            tap_rows(0, 1)
+            quantise_d3 = mix_d3(H, 1, V)
+            quantise_d3x()
+            for t in range(PACK):
+                if t == 2:
+                    quantise_xh = mix_xh(0, (V, A))
+                    quantise_d3()
+                tap2(t, (A, A))
             quantise_xh()
-            for g in range(2):
-                for h in range(2):
-                    for t in range(2):
-                        tap2(g, t, h, A)
             quantise_xh = mix_xh(1, (V, V))
-            quantise_d3[3]()
+
             for g in range(4):
                 if g > 0:
                     quantise_xh()
                 if 0 < g < 3:
                     quantise_xh = mix_xh(g + 1, (V, V))
-                for t in range(2):
-                    for h in range(2):
-                        shift(g, t, h, A if g < 3 else (A, V)[h], pieces=g == 3)
+                for i in (2 * g, 2 * g + 1):
+                    shift(i, (A, A) if g < 3 else (A, V))

@@ -128,10 +128,10 @@ def tile_graphfilterrnnbatch_pb_v_kernel(
         def interleave(engine, group, source):
             engine(group.rearrange("p (c i) j -> p c j i", i=4), source.rearrange("p j (c i) -> p c j i", i=4))
 
-        def interleave_by_four(engine, group, source, part=slice(0, 4)):
+        def interleave_by_four(engine, group, source, part=slice(0, 64)):
             engine(
-                group.rearrange("p (t m) j -> p t m j", t=4)[:, part],
-                source.rearrange("p j (m t) -> p t m j", t=4)[:, part],
+                group.rearrange("p (t a b) j -> p a j b t", t=4, b=2)[:, part],
+                source.rearrange("p j (a b t) -> p a j b t", t=4, b=2)[:, part],
             )
 
         def mask(pre_part, grad_part, name):
@@ -258,8 +258,8 @@ def tile_graphfilterrnnbatch_pb_v_kernel(
             for q in range(2):
                 interleave((A, V)[q], dpre[:, quarter(q), :], masked[q][:])
             w_group = new_group()
-            interleave_by_four(A, w_group[:], w_sb[3], slice(0, 2))
-            interleave_by_four(V, w_group[:], w_sb[3], slice(2, 4))
+            interleave_by_four(A, w_group[:], w_sb[3], slice(0, 32))
+            interleave_by_four(V, w_group[:], w_sb[3], slice(32, 64))
             quantise(dpre_q[0], dpre, E5M2)
             quantise(w_q[3], w_group, E4M3)
             quantise_w4 = mix_w(4, A)

@@ -130,8 +130,8 @@ def tile_graphfilterrnnbatch_pb_v_kernel(
 
         def interleave_by_four(engine, group, source, part=slice(0, 64)):
             engine(
-                group.rearrange("p (t a b) j -> p a j b t", t=4, b=2)[:, part],
-                source.rearrange("p j (a b t) -> p a j b t", t=4, b=2)[:, part],
+                group.rearrange("p (t a b) j -> p a j t b", t=4, b=2)[:, part],
+                source.rearrange("p j (a b t) -> p a j t b", t=4, b=2)[:, part],
             )
 
         def mask(pre_part, grad_part, name):

@@ -75,16 +75,17 @@ def tile_graphfilterrnnbatch_pb_v_kernel(
         grad_1 = load("grad_1", grad_out[0, :, half(1)], BF16)
         pre_1a = load("pre_1a", pre[0, :, quarter(2)], F32)
         pre_1b = load("pre_1b", pre[0, :, quarter(3)], F32)
-        w_012 = load("w_012", taps_a[:, 0 : LAST_TAP * FEATURES], BF16)
+        w_01 = load("w_01", taps_a[:, 0 : 2 * FEATURES], BF16)
         s_0 = load("s_0", S[0, half(0), :], BF16)
         s_1 = load("s_1", S[0, half(1), :], BF16)
+        w_2 = load("w_2", weight_A[:, 2, :], BF16)
         x_sb = load("x", x_taps[0, 2, :, :], BF16)
         h_sb = load("h", h_taps[0, 2, :, :], BF16)
         pre_parts = [pre_0a[:], pre_0b[:], pre_1a[:], pre_1b[:]]
         grad_parts = [(grad_0, grad_1)[q // 2][:, :, quarter(q % 2)] for q in range(4)]
         s_sb = [s_0, s_1]
         xh_sb = [x_sb, h_sb]
-        w_sb = [w_012[:, :, half(k)] for k in range(LAST_TAP)] + [w_3[:], w_b[:]]
+        w_sb = [w_01[:, :, half(0)], w_01[:, :, half(1)], w_2[:], w_3[:], w_b[:]]
 
         identity = keep.tile([P, P], F32, name="identity", align_bytes=64)
         make_identity(nc, identity[:])
@@ -134,12 +135,15 @@ def tile_graphfilterrnnbatch_pb_v_kernel(
                 source.rearrange("p j (a b t) -> p a j t b", t=4, b=2)[:, part],
             )
 
-        def mask(pre_part, grad_part, name):
-            masked = keep.tile([P, PACK, pre_part.shape[-1]], BF16, name=name, align_bytes=64)
+        def mask(group, part):
             nc.vector.scalar_tensor_tensor(
-                out=masked[:], in0=pre_part, scalar=0.0, in1=grad_part, op0=IS_GT, op1=MULT
+                out=group[:, quarter(part % 2), :],
+                in0=pre_parts[part].rearrange("p j c -> p c j"),
+                scalar=0.0,
+                in1=grad_parts[part].rearrange("p j c -> p c j"),
+                op0=IS_GT,
+                op1=MULT,
             )
-            return masked
 
         def mix_w(k, engine):
             group = new_group()
@@ -254,26 +258,24 @@ def tile_graphfilterrnnbatch_pb_v_kernel(
                     direct(tap, i, (A, A))
 
             dpre = new_group()
-            masked = [mask(pre_parts[q], grad_parts[q], "masked_%d" % q) for q in range(2)]
-            for q in range(2):
-                interleave((A, V)[q], dpre[:, quarter(q), :], masked[q][:])
+            for part in (0, 1):
+                mask(dpre, part)
             w_group = new_group()
             interleave_by_four(A, w_group[:], w_sb[3], slice(0, 32))
             interleave_by_four(V, w_group[:], w_sb[3], slice(32, 64))
             quantise(dpre_q[0], dpre, E5M2)
             quantise(w_q[3], w_group, E4M3)
-            quantise_w4 = mix_w(4, A)
+            quantise_w4 = mix_w(4, V)
             make_d3(X, 0, all_scalar)
             quantise_w4()
             dpre = new_group()
-            masked = [mask(pre_parts[2 + q], grad_parts[2 + q], "masked_%d" % q) for q in range(2)]
-            for q in range(2):
-                interleave(V, dpre[:, quarter(q), :], masked[q][:])
+            for part in (2, 3):
+                mask(dpre, part)
             quantise_dx = transpose_dx3(0, (A, A))
             make_d3(H, 0, all_scalar)
+            quantise_dx()
             quantise(dpre_q[1], dpre, E5M2)
 
-            quantise_dx()
             make_d3(X, 1, all_scalar)
             make_d3(H, 1, all_scalar)
             quantise_w1 = mix_w(1, V)
@@ -281,32 +283,33 @@ def tile_graphfilterrnnbatch_pb_v_kernel(
             quantise_w1()
             quantise_w0()
             quantise_s = transpose_s(0, 0, (V, V))
-            quantise_w2 = mix_w(2, V)
+            quantise_d3 = mix_d3(X, 0, V)
             tap_rows(1, 0)
             quantise_s()
-            quantise_w2()
             quantise_s = transpose_s(1, 0, (V, V))
+            quantise_d3()
             quantise_dx = transpose_dx3(1, (A, A))
-            quantise_d3 = mix_d3(H, 0, V)
+            quantise_w2 = mix_w(2, V)
             tap_rows(1, 1)
             quantise_s()
-            quantise_dx()
             quantise_s = transpose_s(0, 1, (V, V))
-            quantise_d3()
+            quantise_w2()
+            quantise_dx()
             tap_rows(0, 0)
             quantise_s()
-            quantise_d3 = mix_d3(X, 0, V)
             quantise_s = transpose_s(1, 1, (A, A))
+            quantise_d3 = mix_d3(H, 0, V)
             quantise_s()
+            tap_rows(0, 1)
+
             quantise_d3x = mix_d3(X, 1, V)
             quantise_d3()
-            tap_rows(0, 1)
-            quantise_d3 = mix_d3(H, 1, V)
+            quantise_d3h = mix_d3(H, 1, V)
             quantise_d3x()
             for t in range(PACK):
                 if t == 2:
                     quantise_xh = mix_xh(0, (V, A))
-                    quantise_d3()
+                    quantise_d3h()
                 tap2(t, (A, A))
             quantise_xh()
             quantise_xh = mix_xh(1, (V, V))

@@ -20,8 +20,8 @@ HALF = 512
 QUARTER = 256
 TAPS = 4
 LAST_TAP = 3
-GROUP_BUFS = 6
-ROW_BUFS = 14
+GROUP_BUFS = 4
+ROW_BUFS = 12
 X, H = 0, 1
 
 FLOPS = 2 * ((TAPS + 1) * FEATURES * FEATURES * NODES + FEATURES * NODES * NODES + 2 * FEATURES * NODES * NODES)
@@ -77,22 +77,22 @@ def tile_graphfilterrnnbatch_pb_v_kernel(
         pre_1b = load("pre_1b", pre[0, :, quarter(3)], F32)
         w_01 = load("w_01", taps_a[:, 0 : 2 * FEATURES], BF16)
         s_0 = load("s_0", S[0, half(0), :], BF16)
-        s_1 = load("s_1", S[0, half(1), :], BF16)
         w_2 = load("w_2", weight_A[:, 2, :], BF16)
-        x_sb = load("x", x_taps[0, 2, :, :], BF16)
-        h_sb = load("h", h_taps[0, 2, :, :], BF16)
+        s_1 = load("s_1", S[0, half(1), :], BF16)
+        xh_sb = keep.tile([P, 2, PACK, NODES], BF16, name="xh", align_bytes=64)
+        nc.sync.dma_start(out=xh_sb[:, X], in_=x_taps[0, 2, :, :].rearrange("(p j) n -> p j n", j=PACK))
+        nc.sync.dma_start(out=xh_sb[:, H], in_=h_taps[0, 2, :, :].rearrange("(p j) n -> p j n", j=PACK))
         pre_parts = [pre_0a[:], pre_0b[:], pre_1a[:], pre_1b[:]]
         grad_parts = [(grad_0, grad_1)[q // 2][:, :, quarter(q % 2)] for q in range(4)]
         s_sb = [s_0, s_1]
-        xh_sb = [x_sb, h_sb]
         w_sb = [w_01[:, :, half(0)], w_01[:, :, half(1)], w_2[:], w_3[:], w_b[:]]
 
         identity = keep.tile([P, P], F32, name="identity", align_bytes=64)
         make_identity(nc, identity[:])
 
-        def operand(name):
-            codes = keep.tile([P, HALF], U32, name=name + "_codes", align_bytes=64)
-            scales = keep.tile([P, HALF], U8, name=name + "_scales", align_bytes=64)
+        def operand(name, columns=HALF):
+            codes = keep.tile([P, columns], U32, name=name + "_codes", align_bytes=64)
+            scales = keep.tile([P, columns], U8, name=name + "_scales", align_bytes=64)
             return codes, scales
 
         w_q = [operand("wq_%d" % k) for k in range(TAPS + 1)]
@@ -100,7 +100,7 @@ def tile_graphfilterrnnbatch_pb_v_kernel(
         xh_q = [operand("xhq_%d" % g) for g in range(4)]
         d3_q = [[operand("d3q_%d%d" % (s, h)) for h in range(2)] for s in (X, H)]
         dx3t_q = [operand("dx3t_%d" % g) for g in range(2)]
-        st_q = [[operand("st_%d%d" % (g, h)) for h in range(2)] for g in range(2)]
+        st_q = [operand("st_%d" % h, NODES) for h in range(2)]
 
         def new_group():
             group = groups.tile([P, HALF, PACK], BF16, name="group", align_bytes=64)
@@ -111,13 +111,20 @@ def tile_graphfilterrnnbatch_pb_v_kernel(
                 out=target[0][:].bitcast(dtype), scales=target[1][:], in_=group[:].rearrange("p c j -> p (c j)")
             )
 
-        def matmul(bank, left, columns, left_dtype, right, right_dtype, start, stop):
+        def quantise_s(g, h):
+            nc.vector.quantize_mx(
+                out=st_q[h][0][:, half(g)].bitcast(E4M3),
+                scales=st_q[h][1][:, half(g)],
+                in_=st_group[h][:, half(g), :].rearrange("p c j -> p (c j)"),
+            )
+
+        def matmul(bank, left, columns, left_dtype, right, part, right_dtype, start, stop):
             nc.tensor.matmul_mx(
                 out=bank[:],
                 lhsT=left[0][:, columns].bitcast(left_dtype),
                 lhsT_scale=left[1][:, columns],
-                rhs=right[0][:].bitcast(right_dtype),
-                rhs_scale=right[1][:],
+                rhs=right[0][:, half(part)].bitcast(right_dtype),
+                rhs_scale=right[1][:, half(part)],
                 start=start,
                 stop=stop,
             )
@@ -155,22 +162,30 @@ def tile_graphfilterrnnbatch_pb_v_kernel(
 
         def mix_xh(g, engines):
             group = new_group()
-            for s in (X, H):
-                interleave(engines[s], group[:, quarter(s), :], xh_sb[s][:, :, quarter(g)])
+            if engines[X] == engines[H]:
+                engines[X](
+                    group[:].rearrange("p (s c i) j -> p s c j i", s=2, i=4),
+                    xh_sb[:, :, :, quarter(g)].rearrange("p s j (c i) -> p s c j i", i=4),
+                )
+            else:
+                for s in (X, H):
+                    interleave(engines[s], group[:, quarter(s), :], xh_sb[:, s, :, quarter(g)])
             return lambda: quantise(xh_q[g], group, E4M3)
 
         d3_sb = [
             [keep.tile([P, PACK, HALF], BF16, name="d3_%d%d" % (s, h), align_bytes=64) for h in range(2)] for s in (X, H)
         ]
 
-        def make_d3(s, h, engines):
-            for t in range(PACK):
-                bank = new_bank()
-                matmul(bank, w_q[LAST_TAP + s], block(t), E4M3, dpre_q[h], E5M2, True, True)
-                engines[t](
-                    d3_sb[s][h][:, t, :].rearrange("p (u q e) -> p u q e", u=2, e=2),
-                    bank[:].rearrange("p (q u e) -> p u q e", u=2, e=2),
-                )
+        def make_d3(s, h):
+            for first in (0, 2):
+                banks = [new_bank(), new_bank()]
+                for i in range(2):
+                    matmul(banks[i], w_q[LAST_TAP + s], block(first + i), E4M3, dpre_q[h], 0, E5M2, True, True)
+                for i in (0, 1):
+                    A(
+                        d3_sb[s][h][:, first + i, :].rearrange("p (u q e) -> p u q e", u=2, e=2),
+                        banks[i][:].rearrange("p (q u e) -> p u q e", u=2, e=2),
+                    )
 
         def mix_d3(s, h, engine):
             group = new_group()
@@ -184,78 +199,81 @@ def tile_graphfilterrnnbatch_pb_v_kernel(
             words = words_of(d3_sb[X][h])
             group = new_group()
             pairs = words_of(group).rearrange("p (c u) -> p c u", u=2)
+            banks = [psum.tile([P, 2, 2, P], F32, name="bank") for b in range(2)]
             for b in range(2):
-                bank = psum.tile([P, 2, 2, P], F32, name="bank")
                 for i in range(2):
                     for u in range(2):
-                        nc.tensor.transpose(bank[:, i, u, :], words[:, block(4 * b + 2 * i + u)], identity[:])
+                        nc.tensor.transpose(banks[b][:, i, u, :], words[:, block(4 * b + 2 * i + u)], identity[:])
+            for b in (0, 1):
                 engines[b](
                     pairs[:, 2 * P * b : 2 * P * (b + 1), :].rearrange("p (i c) u -> p i c u", i=2),
-                    bank[:].rearrange("p i u c -> p i c u"),
+                    banks[b][:].rearrange("p i u c -> p i c u"),
                 )
             return lambda: quantise(dx3t_q[h], group, E5M2)
 
+        st_group = [keep.tile([P, NODES, PACK], BF16, name="st_group_%d" % h, align_bytes=64) for h in range(2)]
+
         def transpose_s(g, h, engines):
             words = words_of(s_sb[h])
-            group = new_group()
-            pairs = words_of(group).rearrange("p (c r u) -> p c r u", r=PACK, u=2)
+            pairs = words_of(st_group[h]).rearrange("p (g c r u) -> p g c r u", g=2, r=PACK, u=2)[:, g]
+            banks = [psum.tile([P, 2, 2, P], F32, name="bank") for b in range(2)]
             for b in range(2):
-                bank = psum.tile([P, 2, 2, P], F32, name="bank")
                 for i in range(2):
                     for u in range(2):
                         low = ((2 * b + i) * NODES + g * HALF) // 2
-                        nc.tensor.transpose(bank[:, i, u, :], words[:, low + u : low + 2 * P : 2], identity[:])
-                engines[b](pairs[:, :, 2 * b : 2 * b + 2, :], bank[:].rearrange("p i u c -> p c i u"))
-            return lambda: quantise(st_q[g][h], group, E4M3)
+                        nc.tensor.transpose(banks[b][:, i, u, :], words[:, low + u : low + 2 * P : 2], identity[:])
+            for b in (0, 1):
+                engines[b](pairs[:, :, 2 * b : 2 * b + 2, :], banks[b][:].rearrange("p i u c -> p c i u"))
 
-        def emit(make_bank, engines, target, pair_order=False):
+        def emit(make_bank, i, target, engines, order, pair_order=False, by_halves=False):
             row = rows.tile([P, NODES], F32, name="row", align_bytes=64)
-            for h in range(2):
-                bank = make_bank(h)
+            banks = [make_bank(i, h) for h in range(2)]
+            for h in order:
                 if pair_order:
                     engines[h](
                         row[:, half(h)].rearrange("p (q u e) -> p q u e", u=2, e=2),
-                        bank[:].rearrange("p (u q e) -> p q u e", u=2, e=2),
+                        banks[h][:].rearrange("p (u q e) -> p q u e", u=2, e=2),
                     )
                 else:
-                    engines[h](row[:, half(h)], bank[:])
-            nc.sync.dma_start(out=target, in_=row[:])
+                    engines[h](row[:, half(h)], banks[h][:])
+                if by_halves:
+                    nc.sync.dma_start(out=target[:, half(h)], in_=row[:, half(h)])
+            if not by_halves:
+                nc.sync.dma_start(out=target, in_=row[:])
 
-        def direct(tap, i, engines):
-            def make_bank(h):
+        def direct(tap, i):
+            def make_bank(i, h):
                 bank = new_bank()
-                matmul(bank, w_q[tap], block(i), E4M3, dpre_q[h], E5M2, True, True)
+                matmul(bank, w_q[tap], block(i), E4M3, dpre_q[h], 0, E5M2, True, True)
                 return bank
 
-            emit(make_bank, engines, out_0[0, tap, block(i), :])
+            emit(make_bank, i, out_0[0, tap, block(i), :], (A, A), (1, 0))
 
         tap2_rows = out_0[0, 2, :, :].rearrange("(p t) n -> p t n", t=PACK)
 
-        def tap2(t, engines):
-            def make_bank(h):
+        def tap2(t, order):
+            def make_bank(t, h):
                 bank = new_bank()
-                matmul(bank, w_q[2], block(t), E4M3, dpre_q[h], E5M2, True, False)
-                matmul(bank, dx3t_q[0], block(t), E5M2, st_q[0][h], E4M3, False, False)
-                matmul(bank, dx3t_q[1], block(t), E5M2, st_q[1][h], E4M3, False, True)
+                matmul(bank, w_q[2], block(t), E4M3, dpre_q[h], 0, E5M2, True, False)
+                matmul(bank, dx3t_q[0], block(t), E5M2, st_q[h], 0, E4M3, False, False)
+                matmul(bank, dx3t_q[1], block(t), E5M2, st_q[h], 1, E4M3, False, True)
                 return bank
 
-            emit(make_bank, engines, tap2_rows[:, t, :])
+            emit(make_bank, t, tap2_rows[:, t, :], (A, A), order)
 
-        def shift(i, engines):
-            def make_bank(h):
+        def shift(i, engines, order):
+            def make_bank(i, h):
                 bank = new_bank()
                 for s in (X, H):
-                    matmul(bank, xh_q[i // 2], block(2 * s + i % 2), E4M3, d3_q[s][h], E5M2, s == X, s == H)
+                    matmul(bank, xh_q[i // 2], block(2 * s + i % 2), E4M3, d3_q[s][h], 0, E5M2, s == X, s == H)
                 return bank
 
-            emit(make_bank, engines, out_1[0, block(i), :], pair_order=True)
+            emit(make_bank, i, out_1[0, block(i), :], engines, order, pair_order=True, by_halves=False)
 
         with tc.manual_schedule():
-            all_scalar = (A, A, A, A)
-
             def tap_rows(tap, g):
                 for i in (2 * g, 2 * g + 1):
-                    direct(tap, i, (A, A))
+                    direct(tap, i)
 
             dpre = new_group()
             for part in (0, 1):
@@ -266,42 +284,41 @@ def tile_graphfilterrnnbatch_pb_v_kernel(
             quantise(dpre_q[0], dpre, E5M2)
             quantise(w_q[3], w_group, E4M3)
             quantise_w4 = mix_w(4, V)
-            make_d3(X, 0, all_scalar)
+            make_d3(X, 0)
             quantise_w4()
             dpre = new_group()
             for part in (2, 3):
                 mask(dpre, part)
             quantise_dx = transpose_dx3(0, (A, A))
-            make_d3(H, 0, all_scalar)
-            quantise_dx()
+            make_d3(H, 0)
             quantise(dpre_q[1], dpre, E5M2)
+            quantise_dx()
 
-            make_d3(X, 1, all_scalar)
-            make_d3(H, 1, all_scalar)
+            make_d3(X, 1)
+            make_d3(H, 1)
             quantise_w1 = mix_w(1, V)
             quantise_w0 = mix_w(0, V)
             quantise_w1()
             quantise_w0()
-            quantise_s = transpose_s(0, 0, (V, V))
             quantise_d3 = mix_d3(X, 0, V)
-            tap_rows(1, 0)
-            quantise_s()
-            quantise_s = transpose_s(1, 0, (V, V))
+            transpose_s(0, 0, (V, V))
             quantise_d3()
-            quantise_dx = transpose_dx3(1, (A, A))
+            tap_rows(1, 0)
+
+            transpose_s(1, 0, (V, V))
             quantise_w2 = mix_w(2, V)
+            quantise_dx = transpose_dx3(1, (A, A))
             tap_rows(1, 1)
-            quantise_s()
-            quantise_s = transpose_s(0, 1, (V, V))
+            quantise(st_q[0], st_group[0], E4M3)
             quantise_w2()
+            transpose_s(0, 1, (V, V))
             quantise_dx()
             tap_rows(0, 0)
-            quantise_s()
-            quantise_s = transpose_s(1, 1, (A, A))
+            quantise_s(0, 1)
+            transpose_s(1, 1, (A, A))
             quantise_d3 = mix_d3(H, 0, V)
-            quantise_s()
+            quantise_s(1, 1)
             tap_rows(0, 1)
-
             quantise_d3x = mix_d3(X, 1, V)
             quantise_d3()
             quantise_d3h = mix_d3(H, 1, V)
@@ -310,14 +327,11 @@ def tile_graphfilterrnnbatch_pb_v_kernel(
                 if t == 2:
                     quantise_xh = mix_xh(0, (V, A))
                     quantise_d3h()
-                tap2(t, (A, A))
-            quantise_xh()
-            quantise_xh = mix_xh(1, (V, V))
-
-            for g in range(4):
-                if g > 0:
                     quantise_xh()
-                if 0 < g < 3:
+                tap2(t, (0, 1))
+            for g in range(4):
+                if g < 3:
                     quantise_xh = mix_xh(g + 1, (V, V))
+                    quantise_xh()
                 for i in (2 * g, 2 * g + 1):
-                    shift(i, (A, A) if g < 3 else (A, V))
+                    shift(i, (A, A) if i < 4 else (A, V), (0, 1))

@@ -20,8 +20,10 @@ HALF = 512
 QUARTER = 256
 TAPS = 4
 LAST_TAP = 3
-GROUP_BUFS = 4
-ROW_BUFS = 12
+GROUP_BUFS = 7
+ROW_BUFS = 14
+S_ON_VECTOR = 3
+SHARED_FROM = 4
 X, H = 0, 1
 
 FLOPS = 2 * ((TAPS + 1) * FEATURES * FEATURES * NODES + FEATURES * NODES * NODES + 2 * FEATURES * NODES * NODES)
@@ -60,39 +62,36 @@ def tile_graphfilterrnnbatch_pb_v_kernel(
         def block(i):
             return slice(i * P, (i + 1) * P)
 
+        def by_four(source):
+            return source.rearrange("(p j) n -> p j n", j=PACK)
+
         def load(name, source, dtype):
             tile = keep.tile([P, PACK, source.shape[-1]], dtype, name=name, align_bytes=64)
-            nc.sync.dma_start(out=tile[:], in_=source.rearrange("(p j) n -> p j n", j=PACK))
+            nc.sync.dma_start(out=tile[:], in_=by_four(source))
             return tile
 
-        taps_a = weight_A.rearrange("k t c -> k (t c)")
-
-        pre_0a = load("pre_0a", pre[0, :, quarter(0)], F32)
-        grad_0 = load("grad_0", grad_out[0, :, half(0)], BF16)
-        pre_0b = load("pre_0b", pre[0, :, quarter(1)], F32)
-        w_3 = load("w_3", weight_A[:, LAST_TAP, :], BF16)
+        pre_sb = [load("pre_0", pre[0, :, quarter(0)], F32)]
+        grad_sb = [load("grad_0", grad_out[0, :, half(0)], BF16)]
+        pre_sb.append(load("pre_1", pre[0, :, quarter(1)], F32))
+        w_last = load("w_last", weight_A[:, LAST_TAP, :], BF16)
         w_b = load("w_b", weight_B[:, LAST_TAP, :], BF16)
-        grad_1 = load("grad_1", grad_out[0, :, half(1)], BF16)
-        pre_1a = load("pre_1a", pre[0, :, quarter(2)], F32)
-        pre_1b = load("pre_1b", pre[0, :, quarter(3)], F32)
-        w_01 = load("w_01", taps_a[:, 0 : 2 * FEATURES], BF16)
-        s_0 = load("s_0", S[0, half(0), :], BF16)
+        grad_sb.append(load("grad_1", grad_out[0, :, half(1)], BF16))
+        pre_sb.extend(load("pre_%d" % q, pre[0, :, quarter(q)], F32) for q in (2, 3))
+        w_01 = load("w_01", weight_A.rearrange("k t c -> k (t c)")[:, 0 : 2 * FEATURES], BF16)
+        s_sb = [load("s_0", S[0, half(0), :], BF16)]
         w_2 = load("w_2", weight_A[:, 2, :], BF16)
-        s_1 = load("s_1", S[0, half(1), :], BF16)
+        s_sb.append(load("s_1", S[0, half(1), :], BF16))
         xh_sb = keep.tile([P, 2, PACK, NODES], BF16, name="xh", align_bytes=64)
-        nc.sync.dma_start(out=xh_sb[:, X], in_=x_taps[0, 2, :, :].rearrange("(p j) n -> p j n", j=PACK))
-        nc.sync.dma_start(out=xh_sb[:, H], in_=h_taps[0, 2, :, :].rearrange("(p j) n -> p j n", j=PACK))
-        pre_parts = [pre_0a[:], pre_0b[:], pre_1a[:], pre_1b[:]]
-        grad_parts = [(grad_0, grad_1)[q // 2][:, :, quarter(q % 2)] for q in range(4)]
-        s_sb = [s_0, s_1]
-        w_sb = [w_01[:, :, half(0)], w_01[:, :, half(1)], w_2[:], w_3[:], w_b[:]]
+        for s, taps in ((X, x_taps), (H, h_taps)):
+            nc.sync.dma_start(out=xh_sb[:, s], in_=by_four(taps[0, 2, :, :]))
+        w_sb = [w_01[:, :, 0:FEATURES], w_01[:, :, FEATURES : 2 * FEATURES], w_2[:], w_last[:], w_b[:]]
 
         identity = keep.tile([P, P], F32, name="identity", align_bytes=64)
         make_identity(nc, identity[:])
 
-        def operand(name, columns=HALF):
-            codes = keep.tile([P, columns], U32, name=name + "_codes", align_bytes=64)
-            scales = keep.tile([P, columns], U8, name=name + "_scales", align_bytes=64)
+        def operand(name):
+            codes = keep.tile([P, HALF], U32, name=name + "_codes", align_bytes=64)
+            scales = keep.tile([P, HALF], U8, name=name + "_scales", align_bytes=64)
             return codes, scales
 
         w_q = [operand("wq_%d" % k) for k in range(TAPS + 1)]
@@ -100,31 +99,27 @@ def tile_graphfilterrnnbatch_pb_v_kernel(
         xh_q = [operand("xhq_%d" % g) for g in range(4)]
         d3_q = [[operand("d3q_%d%d" % (s, h)) for h in range(2)] for s in (X, H)]
         dx3t_q = [operand("dx3t_%d" % g) for g in range(2)]
-        st_q = [operand("st_%d" % h, NODES) for h in range(2)]
+        st_q = [[operand("st_%d%d" % (g, h)) for h in range(2)] for g in range(2)]
 
         def new_group():
             group = groups.tile([P, HALF, PACK], BF16, name="group", align_bytes=64)
             return group
 
-        def quantise(target, group, dtype):
-            nc.vector.quantize_mx(
-                out=target[0][:].bitcast(dtype), scales=target[1][:], in_=group[:].rearrange("p c j -> p (c j)")
-            )
+        def quantiser(target, group, dtype):
+            def quantise():
+                nc.vector.quantize_mx(
+                    out=target[0][:].bitcast(dtype), scales=target[1][:], in_=group[:].rearrange("p c j -> p (c j)")
+                )
 
-        def quantise_s(g, h):
-            nc.vector.quantize_mx(
-                out=st_q[h][0][:, half(g)].bitcast(E4M3),
-                scales=st_q[h][1][:, half(g)],
-                in_=st_group[h][:, half(g), :].rearrange("p c j -> p (c j)"),
-            )
+            return quantise
 
-        def matmul(bank, left, columns, left_dtype, right, part, right_dtype, start, stop):
+        def matmul(bank, left, columns, left_dtype, right, right_dtype, start, stop):
             nc.tensor.matmul_mx(
                 out=bank[:],
                 lhsT=left[0][:, columns].bitcast(left_dtype),
                 lhsT_scale=left[1][:, columns],
-                rhs=right[0][:, half(part)].bitcast(right_dtype),
-                rhs_scale=right[1][:, half(part)],
+                rhs=right[0][:].bitcast(right_dtype),
+                rhs_scale=right[1][:],
                 start=start,
                 stop=stop,
             )
@@ -133,101 +128,102 @@ def tile_graphfilterrnnbatch_pb_v_kernel(
             bank = psum.tile([P, HALF], F32, name="bank")
             return bank
 
+        def mix_dpre(h):
+            group = new_group()
+            for q in range(2):
+                nc.vector.scalar_tensor_tensor(
+                    out=group[:, quarter(q), :],
+                    in0=pre_sb[2 * h + q][:].rearrange("p j c -> p c j"),
+                    scalar=0.0,
+                    in1=grad_sb[h][:, :, quarter(q)].rearrange("p j c -> p c j"),
+                    op0=IS_GT,
+                    op1=MULT,
+                )
+            return quantiser(dpre_q[h], group, E5M2)
+
         def interleave(engine, group, source):
             engine(group.rearrange("p (c i) j -> p c j i", i=4), source.rearrange("p j (c i) -> p c j i", i=4))
 
-        def interleave_by_four(engine, group, source, part=slice(0, 64)):
+        def interleave_by_four(engine, group, source, part):
             engine(
                 group.rearrange("p (t a b) j -> p a j t b", t=4, b=2)[:, part],
                 source.rearrange("p j (a b t) -> p a j t b", t=4, b=2)[:, part],
             )
 
-        def mask(group, part):
-            nc.vector.scalar_tensor_tensor(
-                out=group[:, quarter(part % 2), :],
-                in0=pre_parts[part].rearrange("p j c -> p c j"),
-                scalar=0.0,
-                in1=grad_parts[part].rearrange("p j c -> p c j"),
-                op0=IS_GT,
-                op1=MULT,
-            )
-
-        def mix_w(k, engine):
+        def mix_w(k, engines):
             group = new_group()
             if k < 2:
-                interleave(engine, group[:], w_sb[k])
+                interleave(engines[0], group[:], w_sb[k])
             else:
-                interleave_by_four(engine, group[:], w_sb[k])
-            return lambda: quantise(w_q[k], group, E4M3)
+                share = P // 2 // len(engines)
+                for n, engine in enumerate(engines):
+                    interleave_by_four(engine, group[:], w_sb[k], slice(n * share, (n + 1) * share))
+            return quantiser(w_q[k], group, E4M3)
 
-        def mix_xh(g, engines):
+        def mix_xh(g):
             group = new_group()
-            if engines[X] == engines[H]:
-                engines[X](
+            if g == 0:
+                for s, engine in ((X, V), (H, A)):
+                    interleave(engine, group[:, quarter(s), :], xh_sb[:, s, :, quarter(g)])
+            else:
+                V(
                     group[:].rearrange("p (s c i) j -> p s c j i", s=2, i=4),
                     xh_sb[:, :, :, quarter(g)].rearrange("p s j (c i) -> p s c j i", i=4),
                 )
-            else:
-                for s in (X, H):
-                    interleave(engines[s], group[:, quarter(s), :], xh_sb[:, s, :, quarter(g)])
-            return lambda: quantise(xh_q[g], group, E4M3)
+            return quantiser(xh_q[g], group, E4M3)
 
         d3_sb = [
             [keep.tile([P, PACK, HALF], BF16, name="d3_%d%d" % (s, h), align_bytes=64) for h in range(2)] for s in (X, H)
         ]
 
         def make_d3(s, h):
-            for first in (0, 2):
-                banks = [new_bank(), new_bank()]
-                for i in range(2):
-                    matmul(banks[i], w_q[LAST_TAP + s], block(first + i), E4M3, dpre_q[h], 0, E5M2, True, True)
-                for i in (0, 1):
-                    A(
-                        d3_sb[s][h][:, first + i, :].rearrange("p (u q e) -> p u q e", u=2, e=2),
-                        banks[i][:].rearrange("p (q u e) -> p u q e", u=2, e=2),
-                    )
+            for t in range(PACK):
+                bank = new_bank()
+                matmul(bank, w_q[LAST_TAP + s], block(t), E4M3, dpre_q[h], E5M2, True, True)
+                A(
+                    d3_sb[s][h][:, t, :].rearrange("p (u q e) -> p u q e", u=2, e=2),
+                    bank[:].rearrange("p (q u e) -> p u q e", u=2, e=2),
+                )
 
-        def mix_d3(s, h, engine):
+        def mix_d3(s, h):
             group = new_group()
-            interleave(engine, group[:], d3_sb[s][h][:])
-            return lambda: quantise(d3_q[s][h], group, E5M2)
+            interleave(V, group[:], d3_sb[s][h][:])
+            return quantiser(d3_q[s][h], group, E5M2)
 
         def words_of(tile):
             return tile[:].rearrange("p a b -> p (a b)").bitcast(F32)
 
-        def transpose_dx3(h, engines):
+        def transpose_dx3(h):
             words = words_of(d3_sb[X][h])
             group = new_group()
             pairs = words_of(group).rearrange("p (c u) -> p c u", u=2)
-            banks = [psum.tile([P, 2, 2, P], F32, name="bank") for b in range(2)]
             for b in range(2):
+                bank = psum.tile([P, 2, 2, P], F32, name="bank")
                 for i in range(2):
                     for u in range(2):
-                        nc.tensor.transpose(banks[b][:, i, u, :], words[:, block(4 * b + 2 * i + u)], identity[:])
-            for b in (0, 1):
-                engines[b](
+                        nc.tensor.transpose(bank[:, i, u, :], words[:, block(4 * b + 2 * i + u)], identity[:])
+                A(
                     pairs[:, 2 * P * b : 2 * P * (b + 1), :].rearrange("p (i c) u -> p i c u", i=2),
-                    banks[b][:].rearrange("p i u c -> p i c u"),
+                    bank[:].rearrange("p i u c -> p i c u"),
                 )
-            return lambda: quantise(dx3t_q[h], group, E5M2)
+            return quantiser(dx3t_q[h], group, E5M2)
 
-        st_group = [keep.tile([P, NODES, PACK], BF16, name="st_group_%d" % h, align_bytes=64) for h in range(2)]
-
-        def transpose_s(g, h, engines):
+        def transpose_s(g, h, engine):
             words = words_of(s_sb[h])
-            pairs = words_of(st_group[h]).rearrange("p (g c r u) -> p g c r u", g=2, r=PACK, u=2)[:, g]
-            banks = [psum.tile([P, 2, 2, P], F32, name="bank") for b in range(2)]
+            group = new_group()
+            pairs = words_of(group).rearrange("p (c r u) -> p c r u", r=PACK, u=2)
             for b in range(2):
+                bank = psum.tile([P, 2, 2, P], F32, name="bank")
                 for i in range(2):
                     for u in range(2):
                         low = ((2 * b + i) * NODES + g * HALF) // 2
-                        nc.tensor.transpose(banks[b][:, i, u, :], words[:, low + u : low + 2 * P : 2], identity[:])
-            for b in (0, 1):
-                engines[b](pairs[:, :, 2 * b : 2 * b + 2, :], banks[b][:].rearrange("p i u c -> p c i u"))
+                        nc.tensor.transpose(bank[:, i, u, :], words[:, low + u : low + 2 * P : 2], identity[:])
+                engine(pairs[:, :, 2 * b : 2 * b + 2, :], bank[:].rearrange("p i u c -> p c i u"))
+            return quantiser(st_q[g][h], group, E4M3)
 
-        def emit(make_bank, i, target, engines, order, pair_order=False, by_halves=False):
+        def emit(make_bank, target, engines=(A, A), order=(0, 1), pair_order=False):
             row = rows.tile([P, NODES], F32, name="row", align_bytes=64)
-            banks = [make_bank(i, h) for h in range(2)]
+            banks = [make_bank(h) for h in range(2)]
             for h in order:
                 if pair_order:
                     engines[h](
@@ -236,102 +232,74 @@ def tile_graphfilterrnnbatch_pb_v_kernel(
                     )
                 else:
                     engines[h](row[:, half(h)], banks[h][:])
-                if by_halves:
-                    nc.sync.dma_start(out=target[:, half(h)], in_=row[:, half(h)])
-            if not by_halves:
-                nc.sync.dma_start(out=target, in_=row[:])
+            nc.sync.dma_start(out=target, in_=row[:])
 
         def direct(tap, i):
-            def make_bank(i, h):
+            def make_bank(h):
                 bank = new_bank()
-                matmul(bank, w_q[tap], block(i), E4M3, dpre_q[h], 0, E5M2, True, True)
+                matmul(bank, w_q[tap], block(i), E4M3, dpre_q[h], E5M2, True, True)
                 return bank
 
-            emit(make_bank, i, out_0[0, tap, block(i), :], (A, A), (1, 0))
+            emit(make_bank, out_0[0, tap, block(i), :], order=(1, 0))
 
-        tap2_rows = out_0[0, 2, :, :].rearrange("(p t) n -> p t n", t=PACK)
-
-        def tap2(t, order):
-            def make_bank(t, h):
+        def tap2(t):
+            def make_bank(h):
                 bank = new_bank()
-                matmul(bank, w_q[2], block(t), E4M3, dpre_q[h], 0, E5M2, True, False)
-                matmul(bank, dx3t_q[0], block(t), E5M2, st_q[h], 0, E4M3, False, False)
-                matmul(bank, dx3t_q[1], block(t), E5M2, st_q[h], 1, E4M3, False, True)
+                matmul(bank, w_q[2], block(t), E4M3, dpre_q[h], E5M2, True, False)
+                matmul(bank, dx3t_q[0], block(t), E5M2, st_q[0][h], E4M3, False, False)
+                matmul(bank, dx3t_q[1], block(t), E5M2, st_q[1][h], E4M3, False, True)
                 return bank
 
-            emit(make_bank, t, tap2_rows[:, t, :], (A, A), order)
+            emit(make_bank, by_four(out_0[0, 2, :, :])[:, t, :])
 
-        def shift(i, engines, order):
-            def make_bank(i, h):
+        def shift(i):
+            def make_bank(h):
                 bank = new_bank()
                 for s in (X, H):
-                    matmul(bank, xh_q[i // 2], block(2 * s + i % 2), E4M3, d3_q[s][h], 0, E5M2, s == X, s == H)
+                    matmul(bank, xh_q[i // 2], block(2 * s + i % 2), E4M3, d3_q[s][h], E5M2, s == X, s == H)
                 return bank
 
-            emit(make_bank, i, out_1[0, block(i), :], engines, order, pair_order=True, by_halves=False)
+            emit(make_bank, out_1[0, block(i), :], (A, A) if i < SHARED_FROM else (A, V), pair_order=True)
 
         with tc.manual_schedule():
-            def tap_rows(tap, g):
-                for i in (2 * g, 2 * g + 1):
-                    direct(tap, i)
-
-            dpre = new_group()
-            for part in (0, 1):
-                mask(dpre, part)
-            w_group = new_group()
-            interleave_by_four(A, w_group[:], w_sb[3], slice(0, 32))
-            interleave_by_four(V, w_group[:], w_sb[3], slice(32, 64))
-            quantise(dpre_q[0], dpre, E5M2)
-            quantise(w_q[3], w_group, E4M3)
-            quantise_w4 = mix_w(4, V)
+            quantise_dpre = mix_dpre(0)
+            quantise_w = mix_w(LAST_TAP, (A, V))
+            quantise_dpre()
+            quantise_w()
+            mix_w(TAPS, (A, V))()
             make_d3(X, 0)
-            quantise_w4()
-            dpre = new_group()
-            for part in (2, 3):
-                mask(dpre, part)
-            quantise_dx = transpose_dx3(0, (A, A))
+            quantise_dpre = mix_dpre(1)
+            quantise_dx = transpose_dx3(0)
             make_d3(H, 0)
-            quantise(dpre_q[1], dpre, E5M2)
+            quantise_dpre()
             quantise_dx()
-
-            make_d3(X, 1)
-            make_d3(H, 1)
-            quantise_w1 = mix_w(1, V)
-            quantise_w0 = mix_w(0, V)
-            quantise_w1()
-            quantise_w0()
-            quantise_d3 = mix_d3(X, 0, V)
-            transpose_s(0, 0, (V, V))
-            quantise_d3()
-            tap_rows(1, 0)
-
-            transpose_s(1, 0, (V, V))
-            quantise_w2 = mix_w(2, V)
-            quantise_dx = transpose_dx3(1, (A, A))
-            tap_rows(1, 1)
-            quantise(st_q[0], st_group[0], E4M3)
-            quantise_w2()
-            transpose_s(0, 1, (V, V))
-            quantise_dx()
-            tap_rows(0, 0)
-            quantise_s(0, 1)
-            transpose_s(1, 1, (A, A))
-            quantise_d3 = mix_d3(H, 0, V)
-            quantise_s(1, 1)
-            tap_rows(0, 1)
-            quantise_d3x = mix_d3(X, 1, V)
-            quantise_d3()
-            quantise_d3h = mix_d3(H, 1, V)
-            quantise_d3x()
+            for s in (X, H):
+                make_d3(s, 1)
+            for quantise in [mix_w(k, (V,)) for k in (1, 0)]:
+                quantise()
+            extra = (lambda: mix_w(2, (V,)), lambda: transpose_dx3(1), lambda: mix_d3(X, 0), lambda: mix_d3(H, 0))
+            quantise_extra = None
+            for n in range(4):
+                quantise_s = transpose_s(n % 2, n // 2, V if n < S_ON_VECTOR else A)
+                if n > 0:
+                    quantise_extra()
+                quantise_extra = extra[n]()
+                quantise_s()
+                for i in (2 * (n % 2), 2 * (n % 2) + 1):
+                    direct(1 - n // 2, i)
+            quantise_d3 = quantise_extra
+            for s in (X, H):
+                quantise_next = mix_d3(s, 1)
+                quantise_d3()
+                quantise_d3 = quantise_next
             for t in range(PACK):
-                if t == 2:
-                    quantise_xh = mix_xh(0, (V, A))
-                    quantise_d3h()
+                if t == PACK // 2:
+                    quantise_xh = mix_xh(0)
+                    quantise_d3()
                     quantise_xh()
-                tap2(t, (0, 1))
+                tap2(t)
             for g in range(4):
                 if g < 3:
-                    quantise_xh = mix_xh(g + 1, (V, V))
-                    quantise_xh()
+                    mix_xh(g + 1)()
                 for i in (2 * g, 2 * g + 1):
-                    shift(i, (A, A) if i < 4 else (A, V), (0, 1))
+                    shift(i)

@@ -142,12 +142,12 @@ def tile_graphfilterrnnbatch_pb_v_kernel(
             return quantiser(dpre_q[h], group, E5M2)
 
         def interleave(engine, group, source):
-            engine(group.rearrange("p (c i) j -> p c j i", i=4), source.rearrange("p j (c i) -> p c j i", i=4))
+            engine(group.rearrange("p (c i) j -> p c j i", i=2), source.rearrange("p j (c i) -> p c j i", i=2))
 
         def interleave_by_four(engine, group, source, part):
             engine(
-                group.rearrange("p (t a b) j -> p a j t b", t=4, b=2)[:, part],
-                source.rearrange("p j (a b t) -> p a j t b", t=4, b=2)[:, part],
+                group.rearrange("p (t a b) j -> p a t j b", t=4, b=2)[:, part],
+                source.rearrange("p j (a b t) -> p a t j b", t=4, b=2)[:, part],
             )
 
         def mix_w(k, engines):
@@ -167,8 +167,8 @@ def tile_graphfilterrnnbatch_pb_v_kernel(
                     interleave(engine, group[:, quarter(s), :], xh_sb[:, s, :, quarter(g)])
             else:
                 V(
-                    group[:].rearrange("p (s c i) j -> p s c j i", s=2, i=4),
-                    xh_sb[:, :, :, quarter(g)].rearrange("p s j (c i) -> p s c j i", i=4),
+                    group[:].rearrange("p (s c i) j -> p s c j i", s=2, i=2),
+                    xh_sb[:, :, :, quarter(g)].rearrange("p s j (c i) -> p s c j i", i=2),
                 )
             return quantiser(xh_q[g], group, E4M3)
 

@@ -22,8 +22,6 @@ TAPS = 4
 LAST_TAP = 3
 GROUP_BUFS = 7
 ROW_BUFS = 14
-S_ON_VECTOR = 3
-SHARED_FROM = 4
 X, H = 0, 1
 
 FLOPS = 2 * ((TAPS + 1) * FEATURES * FEATURES * NODES + FEATURES * NODES * NODES + 2 * FEATURES * NODES * NODES)
@@ -51,7 +49,8 @@ def tile_graphfilterrnnbatch_pb_v_kernel(
         keep = ctx.enter_context(tc.tile_pool(name="keep", bufs=1))
         groups = ctx.enter_context(tc.tile_pool(name="groups", bufs=GROUP_BUFS))
         rows = ctx.enter_context(tc.tile_pool(name="rows", bufs=ROW_BUFS))
-        psum = ctx.enter_context(tc.psum_pool(name="psum", bufs=8))
+        psum = ctx.enter_context(tc.psum_pool(name="psum", bufs=6))
+        psum_s = ctx.enter_context(tc.psum_pool(name="psum_s", bufs=2))
 
         def half(h):
             return slice(h * HALF, (h + 1) * HALF)
@@ -70,13 +69,15 @@ def tile_graphfilterrnnbatch_pb_v_kernel(
             nc.sync.dma_start(out=tile[:], in_=by_four(source))
             return tile
 
-        pre_sb = [load("pre_0", pre[0, :, quarter(0)], F32)]
-        grad_sb = [load("grad_0", grad_out[0, :, half(0)], BF16)]
-        pre_sb.append(load("pre_1", pre[0, :, quarter(1)], F32))
+        grad_first = load("grad_first", grad_out[0, :, quarter(0)], BF16)
+        pre_sb = [load("pre_0", pre[0, :, quarter(0)], F32)[:]]
         w_last = load("w_last", weight_A[:, LAST_TAP, :], BF16)
         w_b = load("w_b", weight_B[:, LAST_TAP, :], BF16)
-        grad_sb.append(load("grad_1", grad_out[0, :, half(1)], BF16))
-        pre_sb.extend(load("pre_%d" % q, pre[0, :, quarter(q)], F32) for q in (2, 3))
+        grad_second = load("grad_second", grad_out[0, :, quarter(1)], BF16)
+        pre_sb.append(load("pre_1", pre[0, :, quarter(1)], F32)[:])
+        grad_rest = load("grad_rest", grad_out[0, :, half(1)], BF16)
+        pre_sb.extend(load("pre_%d" % q, pre[0, :, quarter(q)], F32)[:] for q in (2, 3))
+        grad_sb = [grad_first[:], grad_second[:]] + [grad_rest[:, :, quarter(q)] for q in range(2)]
         w_01 = load("w_01", weight_A.rearrange("k t c -> k (t c)")[:, 0 : 2 * FEATURES], BF16)
         s_sb = [load("s_0", S[0, half(0), :], BF16)]
         w_2 = load("w_2", weight_A[:, 2, :], BF16)
@@ -89,57 +90,62 @@ def tile_graphfilterrnnbatch_pb_v_kernel(
         identity = keep.tile([P, P], F32, name="identity", align_bytes=64)
         make_identity(nc, identity[:])
 
-        def operand(name):
-            codes = keep.tile([P, HALF], U32, name=name + "_codes", align_bytes=64)
-            scales = keep.tile([P, HALF], U8, name=name + "_scales", align_bytes=64)
+        def operand(name, columns=HALF):
+            codes = keep.tile([P, columns], U32, name=name + "_codes", align_bytes=64)
+            scales = keep.tile([P, columns], U8, name=name + "_scales", align_bytes=64)
             return codes, scales
 
         w_q = [operand("wq_%d" % k) for k in range(TAPS + 1)]
-        dpre_q = [operand("dpre_%d" % h) for h in range(2)]
+        dpre_q = operand("dpre", NODES)
         xh_q = [operand("xhq_%d" % g) for g in range(4)]
         d3_q = [[operand("d3q_%d%d" % (s, h)) for h in range(2)] for s in (X, H)]
         dx3t_q = [operand("dx3t_%d" % g) for g in range(2)]
         st_q = [[operand("st_%d%d" % (g, h)) for h in range(2)] for g in range(2)]
 
-        def new_group():
-            group = groups.tile([P, HALF, PACK], BF16, name="group", align_bytes=64)
+        def new_group(columns=HALF):
+            group = groups.tile([P, columns, PACK], BF16, name="group", align_bytes=64)
             return group
 
-        def quantiser(target, group, dtype):
+        def quantiser(target, group, dtype, columns=slice(0, HALF)):
             def quantise():
                 nc.vector.quantize_mx(
-                    out=target[0][:].bitcast(dtype), scales=target[1][:], in_=group[:].rearrange("p c j -> p (c j)")
+                    out=target[0][:, columns].bitcast(dtype),
+                    scales=target[1][:, columns],
+                    in_=group[:].rearrange("p c j -> p (c j)"),
                 )
 
             return quantise
 
-        def matmul(bank, left, columns, left_dtype, right, right_dtype, start, stop):
+        def matmul(out, left, rows_out, left_dtype, right, columns, right_dtype, start=True, stop=True):
             nc.tensor.matmul_mx(
-                out=bank[:],
-                lhsT=left[0][:, columns].bitcast(left_dtype),
-                lhsT_scale=left[1][:, columns],
-                rhs=right[0][:].bitcast(right_dtype),
-                rhs_scale=right[1][:],
+                out=out,
+                lhsT=left[0][:, rows_out].bitcast(left_dtype),
+                lhsT_scale=left[1][:, rows_out],
+                rhs=right[0][:, columns].bitcast(right_dtype),
+                rhs_scale=right[1][:, columns],
                 start=start,
                 stop=stop,
             )
 
-        def new_bank():
-            bank = psum.tile([P, HALF], F32, name="bank")
+        def new_bank(*shape):
+            bank = psum.tile([P, *shape], F32, name="bank")
             return bank
 
-        def mix_dpre(h):
-            group = new_group()
-            for q in range(2):
-                nc.vector.scalar_tensor_tensor(
-                    out=group[:, quarter(q), :],
-                    in0=pre_sb[2 * h + q][:].rearrange("p j c -> p c j"),
-                    scalar=0.0,
-                    in1=grad_sb[h][:, :, quarter(q)].rearrange("p j c -> p c j"),
-                    op0=IS_GT,
-                    op1=MULT,
-                )
-            return quantiser(dpre_q[h], group, E5M2)
+        def new_s_bank():
+            bank = psum_s.tile([P, 2, 2, P], F32, name="s_bank")
+            return bank
+
+        def mix_dpre(i):
+            group = groups.tile([P, P, PACK], BF16, name="dpre_group", align_bytes=64, bufs=3)
+            nc.vector.scalar_tensor_tensor(
+                out=group[:],
+                in0=pre_sb[i // 2][:, :, block(i % 2)].rearrange("p j c -> p c j"),
+                scalar=0.0,
+                in1=grad_sb[i // 2][:, :, block(i % 2)].rearrange("p j c -> p c j"),
+                op0=IS_GT,
+                op1=MULT,
+            )
+            return quantiser(dpre_q, group, E5M2, block(i))
 
         def interleave(engine, group, source):
             engine(group.rearrange("p (c i) j -> p c j i", i=2), source.rearrange("p j (c i) -> p c j i", i=2))
@@ -150,156 +156,184 @@ def tile_graphfilterrnnbatch_pb_v_kernel(
                 source.rearrange("p j (a b t) -> p a t j b", t=4, b=2)[:, part],
             )
 
-        def mix_w(k, engines):
+        def mix_w(k, on_scalar_eighths=0):
             group = new_group()
+            cut = on_scalar_eighths * P // 16
             if k < 2:
-                interleave(engines[0], group[:], w_sb[k])
+                interleave(V, group[:], w_sb[k])
             else:
-                share = P // 2 // len(engines)
-                for n, engine in enumerate(engines):
-                    interleave_by_four(engine, group[:], w_sb[k], slice(n * share, (n + 1) * share))
+                if cut > 0:
+                    interleave_by_four(A, group[:], w_sb[k], slice(0, cut))
+                interleave_by_four(V, group[:], w_sb[k], slice(cut, P // 2))
             return quantiser(w_q[k], group, E4M3)
 
         def mix_xh(g):
             group = new_group()
-            if g == 0:
-                for s, engine in ((X, V), (H, A)):
-                    interleave(engine, group[:, quarter(s), :], xh_sb[:, s, :, quarter(g)])
-            else:
-                V(
-                    group[:].rearrange("p (s c i) j -> p s c j i", s=2, i=2),
-                    xh_sb[:, :, :, quarter(g)].rearrange("p s j (c i) -> p s c j i", i=2),
-                )
+            V(
+                group[:].rearrange("p (s c i) j -> p s c j i", s=2, i=2),
+                xh_sb[:, :, :, quarter(g)].rearrange("p s j (c i) -> p s c j i", i=2),
+            )
             return quantiser(xh_q[g], group, E4M3)
 
-        d3_sb = [
-            [keep.tile([P, PACK, HALF], BF16, name="d3_%d%d" % (s, h), align_bytes=64) for h in range(2)] for s in (X, H)
-        ]
+        dx3_sb = [keep.tile([P, PACK, HALF], BF16, name="dx3_%d" % h, align_bytes=64) for h in range(2)]
+        dh3_group = [keep.tile([P, HALF, PACK], BF16, name="dh3_%d" % h, align_bytes=64) for h in range(2)]
 
-        def make_d3(s, h):
+        def make_d3(s, i):
+            bank = new_bank(PACK, P)
             for t in range(PACK):
-                bank = new_bank()
-                matmul(bank, w_q[LAST_TAP + s], block(t), E4M3, dpre_q[h], E5M2, True, True)
+                matmul(bank[:, t, :], w_q[LAST_TAP + s], block(t), E4M3, dpre_q, block(i), E5M2)
+            if s == X:
                 A(
-                    d3_sb[s][h][:, t, :].rearrange("p (u q e) -> p u q e", u=2, e=2),
-                    bank[:].rearrange("p (q u e) -> p u q e", u=2, e=2),
+                    dx3_sb[i // 4][:].rearrange("p t (u r q e) -> p r t u q e", u=2, r=4, e=2)[:, i % 4],
+                    bank[:].rearrange("p t (q u e) -> p t u q e", u=2, e=2),
                 )
+            else:
+                A(dh3_group[i // 4][:, block(i % 4), :], bank[:].rearrange("p t n -> p n t"))
 
-        def mix_d3(s, h):
+        def quantise_dh3(h):
+            quantiser(d3_q[H][h], dh3_group[h], E5M2)()
+
+        def mix_dx3(h):
             group = new_group()
-            interleave(V, group[:], d3_sb[s][h][:])
-            return quantiser(d3_q[s][h], group, E5M2)
+            V(
+                group[:].rearrange("p (q u e) t -> p u q t e", u=2, e=2),
+                dx3_sb[h][:].rearrange("p t (u q e) -> p u q t e", u=2, e=2),
+            )
+            return quantiser(d3_q[X][h], group, E5M2)
 
         def words_of(tile):
             return tile[:].rearrange("p a b -> p (a b)").bitcast(F32)
 
-        def transpose_dx3(h):
-            words = words_of(d3_sb[X][h])
+        def transpose_dx3(h, engine=A):
+            words = words_of(dx3_sb[h])
             group = new_group()
             pairs = words_of(group).rearrange("p (c u) -> p c u", u=2)
             for b in range(2):
-                bank = psum.tile([P, 2, 2, P], F32, name="bank")
+                bank = new_bank(2, 2, P)
                 for i in range(2):
                     for u in range(2):
                         nc.tensor.transpose(bank[:, i, u, :], words[:, block(4 * b + 2 * i + u)], identity[:])
-                A(
+                engine(
                     pairs[:, 2 * P * b : 2 * P * (b + 1), :].rearrange("p (i c) u -> p i c u", i=2),
                     bank[:].rearrange("p i u c -> p i c u"),
                 )
             return quantiser(dx3t_q[h], group, E5M2)
 
-        def transpose_s(g, h, engine):
+        def transpose_s(g, h):
             words = words_of(s_sb[h])
-            group = new_group()
-            pairs = words_of(group).rearrange("p (c r u) -> p c r u", r=PACK, u=2)
+            banks = []
             for b in range(2):
-                bank = psum.tile([P, 2, 2, P], F32, name="bank")
+                bank = new_s_bank()
+                banks.append(bank)
                 for i in range(2):
                     for u in range(2):
                         low = ((2 * b + i) * NODES + g * HALF) // 2
                         nc.tensor.transpose(bank[:, i, u, :], words[:, low + u : low + 2 * P : 2], identity[:])
-                engine(pairs[:, :, 2 * b : 2 * b + 2, :], bank[:].rearrange("p i u c -> p c i u"))
-            return quantiser(st_q[g][h], group, E4M3)
 
-        def emit(make_bank, target, engines=(A, A), order=(0, 1), pair_order=False):
+            def empty(engine):
+                group = new_group()
+                pairs = words_of(group).rearrange("p (c r u) -> p c r u", r=PACK, u=2)
+                for b in range(2):
+                    engine(pairs[:, :, 2 * b : 2 * b + 2, :], banks[b][:].rearrange("p i u c -> p c i u"))
+                return quantiser(st_q[g][h], group, E4M3)
+
+            return empty
+
+        def row_tile(target, passes):
             row = rows.tile([P, NODES], F32, name="row", align_bytes=64)
-            banks = [make_bank(h) for h in range(2)]
-            for h in order:
-                if pair_order:
-                    engines[h](
-                        row[:, half(h)].rearrange("p (q u e) -> p q u e", u=2, e=2),
-                        banks[h][:].rearrange("p (u q e) -> p q u e", u=2, e=2),
-                    )
-                else:
-                    engines[h](row[:, half(h)], banks[h][:])
-            nc.sync.dma_start(out=target, in_=row[:])
+
+            def make(h, engine=A):
+                bank = new_bank(HALF)
+                steps = passes(h)
+                for n, step in enumerate(steps):
+                    matmul(bank[:], *step, n == 0, n == len(steps) - 1)
+                engine(row[:, half(h)], bank[:])
+                if h == 1:
+                    nc.sync.dma_start(out=target, in_=row[:])
+
+            return make
+
+        def both(make, second=A):
+            make(0)
+            make(1, second)
 
         def direct(tap, i):
-            def make_bank(h):
-                bank = new_bank()
-                matmul(bank, w_q[tap], block(i), E4M3, dpre_q[h], E5M2, True, True)
-                return bank
-
-            emit(make_bank, out_0[0, tap, block(i), :], order=(1, 0))
+            both(row_tile(out_0[0, tap, block(i), :], lambda h: [(w_q[tap], block(i), E4M3, dpre_q, half(h), E5M2)]))
 
         def tap2(t):
-            def make_bank(h):
-                bank = new_bank()
-                matmul(bank, w_q[2], block(t), E4M3, dpre_q[h], E5M2, True, False)
-                matmul(bank, dx3t_q[0], block(t), E5M2, st_q[0][h], E4M3, False, False)
-                matmul(bank, dx3t_q[1], block(t), E5M2, st_q[1][h], E4M3, False, True)
-                return bank
-
-            emit(make_bank, by_four(out_0[0, 2, :, :])[:, t, :])
+            return row_tile(
+                by_four(out_0[0, 2, :, :])[:, t, :],
+                lambda h: [(w_q[2], block(t), E4M3, dpre_q, half(h), E5M2)]
+                + [(dx3t_q[g], block(t), E5M2, st_q[g][h], half(0), E4M3) for g in range(2)],
+            )
 
         def shift(i):
-            def make_bank(h):
-                bank = new_bank()
-                for s in (X, H):
-                    matmul(bank, xh_q[i // 2], block(2 * s + i % 2), E4M3, d3_q[s][h], E5M2, s == X, s == H)
-                return bank
-
-            emit(make_bank, out_1[0, block(i), :], (A, A) if i < SHARED_FROM else (A, V), pair_order=True)
+            return row_tile(
+                out_1[0, block(i), :],
+                lambda h: [(xh_q[i // 2], block(2 * s + i % 2), E4M3, d3_q[s][h], half(0), E5M2) for s in (X, H)],
+            )
 
         with tc.manual_schedule():
-            quantise_dpre = mix_dpre(0)
-            quantise_w = mix_w(LAST_TAP, (A, V))
-            quantise_dpre()
-            quantise_w()
-            mix_w(TAPS, (A, V))()
-            make_d3(X, 0)
-            quantise_dpre = mix_dpre(1)
-            quantise_dx = transpose_dx3(0)
-            make_d3(H, 0)
-            quantise_dpre()
-            quantise_dx()
+            q_0 = mix_dpre(0)
+            q_1 = mix_dpre(1)
+            q_x = mix_w(LAST_TAP, 3)
+            q_0()
+            q_x()
+            q_h = mix_w(TAPS, 5)
+            q_1()
+            q_h()
+            q_prev = mix_dpre(2)
             for s in (X, H):
-                make_d3(s, 1)
-            for quantise in [mix_w(k, (V,)) for k in (1, 0)]:
-                quantise()
-            extra = (lambda: mix_w(2, (V,)), lambda: transpose_dx3(1), lambda: mix_d3(X, 0), lambda: mix_d3(H, 0))
-            quantise_extra = None
-            for n in range(4):
-                quantise_s = transpose_s(n % 2, n // 2, V if n < S_ON_VECTOR else A)
-                if n > 0:
-                    quantise_extra()
-                quantise_extra = extra[n]()
-                quantise_s()
-                for i in (2 * (n % 2), 2 * (n % 2) + 1):
-                    direct(1 - n // 2, i)
-            quantise_d3 = quantise_extra
-            for s in (X, H):
-                quantise_next = mix_d3(s, 1)
-                quantise_d3()
-                quantise_d3 = quantise_next
-            for t in range(PACK):
-                if t == PACK // 2:
-                    quantise_xh = mix_xh(0)
-                    quantise_d3()
-                    quantise_xh()
-                tap2(t)
-            for g in range(4):
-                if g < 3:
-                    mix_xh(g + 1)()
+                for i in range(2):
+                    make_d3(s, i)
+            for i in range(3, 9):
+                q_next = mix_dpre(i) if i < 8 else mix_w(0)
+                q_prev()
+                q_prev = q_next
+                make_d3(X, i - 1)
+                make_d3(H, i - 1)
+                if i == 5:
+                    q_dx3t0 = transpose_dx3(0)
+            q_prev()
+            q_w1 = mix_w(1)
+            e_s = transpose_s(0, 0)
+            direct(0, 0)
+            direct(0, 1)
+            q_s00 = e_s(V)
+            q_w1()
+            q_w2 = mix_w(2)
+            q_dx3t1 = transpose_dx3(1)
+            q_s10 = transpose_s(1, 0)(V)
+            q_s00()
+            q_w2()
+            q_dx3t0()
+            q_s10()
+            q_dx3t1()
+            direct(0, 2)
+            direct(0, 3)
+            q_s01 = transpose_s(0, 1)(V)
+            direct(1, 0)
+            direct(1, 1)
+            q_a = mix_dx3(0)
+            q_s11 = transpose_s(1, 1)(A)
+            q_s01()
+            direct(1, 2)
+            direct(1, 3)
+            q_a()
+            q_s11()
+            tiles = [tap2(t) for t in range(PACK)]
+            for t, h in ((0, 0), (1, 0), (0, 1), (1, 1), (2, 0), (2, 1), (3, 0), (3, 1)):
+                tiles[t](h)
+            q_x = mix_xh(0)
+            quantise_dh3(0)
+            q_x()
+            q_b = mix_dx3(1)
+            quantise_dh3(1)
+            q_b()
+            tiles = [shift(i) for i in range(2)]
+            for i in range(2):
+                both(tiles[i])
+            for g in range(1, 4):
+                mix_xh(g)()
                 for i in (2 * g, 2 * g + 1):
-                    shift(i)
+                    both(shift(i), A if i < 6 else V)

@@ -73,15 +73,15 @@ def tile_graphfilterrnnbatch_pb_v_kernel(
         pre_sb = [load("pre_0", pre[0, :, quarter(0)], F32)[:]]
         w_last = load("w_last", weight_A[:, LAST_TAP, :], BF16)
         w_b = load("w_b", weight_B[:, LAST_TAP, :], BF16)
+        s_sb = [load("s_0", S[0, half(0), :], BF16)]
         grad_second = load("grad_second", grad_out[0, :, quarter(1)], BF16)
         pre_sb.append(load("pre_1", pre[0, :, quarter(1)], F32)[:])
         grad_rest = load("grad_rest", grad_out[0, :, half(1)], BF16)
         pre_sb.extend(load("pre_%d" % q, pre[0, :, quarter(q)], F32)[:] for q in (2, 3))
         grad_sb = [grad_first[:], grad_second[:]] + [grad_rest[:, :, quarter(q)] for q in range(2)]
         w_01 = load("w_01", weight_A.rearrange("k t c -> k (t c)")[:, 0 : 2 * FEATURES], BF16)
-        s_sb = [load("s_0", S[0, half(0), :], BF16)]
-        w_2 = load("w_2", weight_A[:, 2, :], BF16)
         s_sb.append(load("s_1", S[0, half(1), :], BF16))
+        w_2 = load("w_2", weight_A[:, 2, :], BF16)
         xh_sb = keep.tile([P, 2, PACK, NODES], BF16, name="xh", align_bytes=64)
         for s, taps in ((X, x_taps), (H, h_taps)):
             nc.sync.dma_start(out=xh_sb[:, s], in_=by_four(taps[0, 2, :, :]))
@@ -176,22 +176,30 @@ def tile_graphfilterrnnbatch_pb_v_kernel(
             return quantiser(xh_q[g], group, E4M3)
 
         dx3_sb = [keep.tile([P, PACK, HALF], BF16, name="dx3_%d" % h, align_bytes=64) for h in range(2)]
-        dh3_group = [keep.tile([P, HALF, PACK], BF16, name="dh3_%d" % h, align_bytes=64) for h in range(2)]
+        dh3_sb = [keep.tile([P, 2, HALF, 2], BF16, name="dh3_%d" % h, align_bytes=64) for h in range(2)]
 
-        def make_d3(s, i):
-            bank = new_bank(PACK, P)
-            for t in range(PACK):
-                matmul(bank[:, t, :], w_q[LAST_TAP + s], block(t), E4M3, dpre_q, block(i), E5M2)
-            if s == X:
-                A(
-                    dx3_sb[i // 4][:].rearrange("p t (u r q e) -> p r t u q e", u=2, r=4, e=2)[:, i % 4],
-                    bank[:].rearrange("p t (q u e) -> p t u q e", u=2, e=2),
-                )
-            else:
-                A(dh3_group[i // 4][:, block(i % 4), :], bank[:].rearrange("p t n -> p n t"))
+        def make_d3(s, q):
+            for u in range(2):
+                bank = new_bank(2, QUARTER)
+                for e in range(2):
+                    matmul(bank[:, e, :], w_q[LAST_TAP + s], block(2 * u + e), E4M3, dpre_q, quarter(q), E5M2)
+                if s == X:
+                    A(
+                        dx3_sb[q // 2][:, 2 * u : 2 * u + 2, :].rearrange("p t (v r q e) -> p r t v q e", v=2, r=2, e=2)[
+                            :, q % 2
+                        ],
+                        bank[:].rearrange("p t (q v e) -> p t v q e", v=2, e=2),
+                    )
+                else:
+                    A(dh3_sb[q // 2][:, u, quarter(q % 2), :], bank[:].rearrange("p e n -> p n e"))
 
-        def quantise_dh3(h):
-            quantiser(d3_q[H][h], dh3_group[h], E5M2)()
+        def mix_dh3(h):
+            group = new_group()
+            V(
+                words_of(group).rearrange("p (n u) -> p n u", u=2),
+                dh3_sb[h][:].rearrange("p u n e -> p (u n e)").bitcast(F32).rearrange("p (u n) -> p n u", u=2),
+            )
+            return quantiser(d3_q[H][h], group, E5M2)
 
         def mix_dx3(h):
             group = new_group()
@@ -278,62 +286,74 @@ def tile_graphfilterrnnbatch_pb_v_kernel(
             q_1 = mix_dpre(1)
             q_x = mix_w(LAST_TAP, 3)
             q_0()
-            q_x()
-            q_h = mix_w(TAPS, 5)
             q_1()
+            q_x()
+            q_h = mix_w(TAPS, 4)
+            make_d3(X, 0)
             q_h()
-            q_prev = mix_dpre(2)
-            for s in (X, H):
-                for i in range(2):
-                    make_d3(s, i)
-            for i in range(3, 9):
-                q_next = mix_dpre(i) if i < 8 else mix_w(0)
-                q_prev()
-                q_prev = q_next
-                make_d3(X, i - 1)
-                make_d3(H, i - 1)
-                if i == 5:
-                    q_dx3t0 = transpose_dx3(0)
-            q_prev()
-            q_w1 = mix_w(1)
-            e_s = transpose_s(0, 0)
-            direct(0, 0)
-            direct(0, 1)
-            q_s00 = e_s(V)
-            q_w1()
-            q_w2 = mix_w(2)
-            q_dx3t1 = transpose_dx3(1)
-            q_s10 = transpose_s(1, 0)(V)
+            q_s00 = transpose_s(0, 0)(A)
+            make_d3(H, 0)
+            q_2 = mix_dpre(2)
+            q_3 = mix_dpre(3)
+            q_s10 = transpose_s(1, 0)(A)
+            q_2()
             q_s00()
-            q_w2()
-            q_dx3t0()
+            q_3()
+            make_d3(X, 1)
+            make_d3(H, 1)
+            q_4 = mix_dpre(4)
+            q_5 = mix_dpre(5)
+            q_4()
+            q_6 = mix_dpre(6)
+            q_5()
+            q_dx3t0 = transpose_dx3(0)
+            make_d3(X, 2)
+            make_d3(H, 2)
+            q_7 = mix_dpre(7)
+            q_6()
             q_s10()
+            q_7()
+            make_d3(X, 3)
+            make_d3(H, 3)
+            q_w0 = mix_w(0)
+            q_dx3t0()
+            q_w0()
+            e_s = transpose_s(0, 1)
+            q_w1 = mix_w(1)
+            direct(0, 0)
+            q_s01 = e_s(V)
+            q_w1()
+            direct(0, 1)
+            q_dx3t1 = transpose_dx3(1)
+            e_s = transpose_s(1, 1)
+            q_w2 = mix_w(2)
+            q_s11 = e_s(V)
+            q_w2()
             q_dx3t1()
+            q_s01()
+            q_s11()
             direct(0, 2)
             direct(0, 3)
-            q_s01 = transpose_s(0, 1)(V)
+            tiles = [tap2(t) for t in range(PACK)]
             direct(1, 0)
             direct(1, 1)
+            for t in range(2):
+                both(tiles[t])
+                direct(1, 2 + t)
+            for t in range(2, 4):
+                both(tiles[t])
             q_a = mix_dx3(0)
-            q_s11 = transpose_s(1, 1)(A)
-            q_s01()
-            direct(1, 2)
-            direct(1, 3)
+            q_h = mix_dh3(0)
             q_a()
-            q_s11()
-            tiles = [tap2(t) for t in range(PACK)]
-            for t, h in ((0, 0), (1, 0), (0, 1), (1, 1), (2, 0), (2, 1), (3, 0), (3, 1)):
-                tiles[t](h)
             q_x = mix_xh(0)
-            quantise_dh3(0)
+            q_h()
+            q_h = mix_dh3(1)
             q_x()
             q_b = mix_dx3(1)
-            quantise_dh3(1)
+            q_h()
             q_b()
-            tiles = [shift(i) for i in range(2)]
-            for i in range(2):
-                both(tiles[i])
-            for g in range(1, 4):
-                mix_xh(g)()
+            for g in range(4):
+                if g > 0:
+                    mix_xh(g)()
                 for i in (2 * g, 2 * g + 1):
                     both(shift(i), A if i < 6 else V)

@@ -20,8 +20,11 @@ HALF = 512
 QUARTER = 256
 TAPS = 4
 LAST_TAP = 3
-GROUP_BUFS = 7
-ROW_BUFS = 14
+ROW_BUFS = 6
+BANKS = 6
+S_BANKS = 2
+SCALAR_EIGHTHS = {4: 4}
+GROUP_BUFS = dict(group=4, a_group=3, dpre_group=3, xh_group=3)
 X, H = 0, 1
 
 FLOPS = 2 * ((TAPS + 1) * FEATURES * FEATURES * NODES + FEATURES * NODES * NODES + 2 * FEATURES * NODES * NODES)
@@ -47,10 +50,10 @@ def tile_graphfilterrnnbatch_pb_v_kernel(
 
     with ExitStack() as ctx:
         keep = ctx.enter_context(tc.tile_pool(name="keep", bufs=1))
-        groups = ctx.enter_context(tc.tile_pool(name="groups", bufs=GROUP_BUFS))
+        groups = ctx.enter_context(tc.tile_pool(name="groups", bufs=3))
         rows = ctx.enter_context(tc.tile_pool(name="rows", bufs=ROW_BUFS))
-        psum = ctx.enter_context(tc.psum_pool(name="psum", bufs=6))
-        psum_s = ctx.enter_context(tc.psum_pool(name="psum_s", bufs=2))
+        psum = ctx.enter_context(tc.psum_pool(name="psum", bufs=BANKS))
+        psum_s = ctx.enter_context(tc.psum_pool(name="psum_s", bufs=S_BANKS))
 
         def half(h):
             return slice(h * HALF, (h + 1) * HALF)
@@ -69,23 +72,25 @@ def tile_graphfilterrnnbatch_pb_v_kernel(
             nc.sync.dma_start(out=tile[:], in_=by_four(source))
             return tile
 
-        grad_first = load("grad_first", grad_out[0, :, quarter(0)], BF16)
-        pre_sb = [load("pre_0", pre[0, :, quarter(0)], F32)[:]]
-        w_last = load("w_last", weight_A[:, LAST_TAP, :], BF16)
-        w_b = load("w_b", weight_B[:, LAST_TAP, :], BF16)
-        s_sb = [load("s_0", S[0, half(0), :], BF16)]
-        grad_second = load("grad_second", grad_out[0, :, quarter(1)], BF16)
-        pre_sb.append(load("pre_1", pre[0, :, quarter(1)], F32)[:])
-        grad_rest = load("grad_rest", grad_out[0, :, half(1)], BF16)
-        pre_sb.extend(load("pre_%d" % q, pre[0, :, quarter(q)], F32)[:] for q in (2, 3))
-        grad_sb = [grad_first[:], grad_second[:]] + [grad_rest[:, :, quarter(q)] for q in range(2)]
-        w_01 = load("w_01", weight_A.rearrange("k t c -> k (t c)")[:, 0 : 2 * FEATURES], BF16)
-        s_sb.append(load("s_1", S[0, half(1), :], BF16))
-        w_2 = load("w_2", weight_A[:, 2, :], BF16)
         xh_sb = keep.tile([P, 2, PACK, NODES], BF16, name="xh", align_bytes=64)
-        for s, taps in ((X, x_taps), (H, h_taps)):
-            nc.sync.dma_start(out=xh_sb[:, s], in_=by_four(taps[0, 2, :, :]))
-        w_sb = [w_01[:, :, 0:FEATURES], w_01[:, :, FEATURES : 2 * FEATURES], w_2[:], w_last[:], w_b[:]]
+        w_last = load("w_last", weight_A[:, LAST_TAP, :], BF16)
+        grad_0 = load("grad_0", grad_out[0, :, half(0)], BF16)
+        pre_0 = load("pre_0", pre[0, :, quarter(0)], F32)
+        w_b = load("w_b", weight_B[:, LAST_TAP, :], BF16)
+        pre_1 = load("pre_1", pre[0, :, quarter(1)], F32)
+        grad_1 = load("grad_1", grad_out[0, :, half(1)], BF16)
+        pre_2 = load("pre_2", pre[0, :, quarter(2)], F32)
+        pre_3 = load("pre_3", pre[0, :, quarter(3)], F32)
+        s_0 = load("s_0", S[0, half(0), :], BF16)
+        w_0 = load("w_0", weight_A[:, 0, :], BF16)
+        w_12 = load("w_12", weight_A.rearrange("k t c -> k (t c)")[:, FEATURES : 3 * FEATURES], BF16)
+        s_1 = load("s_1", S[0, half(1), :], BF16)
+        nc.sync.dma_start(out=xh_sb[:, X], in_=by_four(x_taps[0, 2, :, :]))
+        nc.sync.dma_start(out=xh_sb[:, H], in_=by_four(h_taps[0, 2, :, :]))
+        pre_sb = [pre_0[:], pre_1[:], pre_2[:], pre_3[:]]
+        grad_sb = [(grad_0, grad_1)[q // 2][:, :, quarter(q % 2)] for q in range(4)]
+        s_sb = [s_0, s_1]
+        w_sb = [w_0[:], w_12[:, :, 0:FEATURES], w_12[:, :, FEATURES:], w_last[:], w_b[:]]
 
         identity = keep.tile([P, P], F32, name="identity", align_bytes=64)
         make_identity(nc, identity[:])
@@ -97,24 +102,29 @@ def tile_graphfilterrnnbatch_pb_v_kernel(
 
         w_q = [operand("wq_%d" % k) for k in range(TAPS + 1)]
         dpre_q = operand("dpre", NODES)
-        xh_q = [operand("xhq_%d" % g) for g in range(4)]
+        xh_q = [operand("xhq_%d" % i, 2 * P) for i in range(8)]
         d3_q = [[operand("d3q_%d%d" % (s, h)) for h in range(2)] for s in (X, H)]
         dx3t_q = [operand("dx3t_%d" % g) for g in range(2)]
         st_q = [[operand("st_%d%d" % (g, h)) for h in range(2)] for g in range(2)]
 
-        def new_group(columns=HALF):
-            group = groups.tile([P, columns, PACK], BF16, name="group", align_bytes=64)
-            return group
+        def pairs_of(text):
+            names = []
+            for name in text.split():
+                stem = name.replace("*", "")
+                names.extend([stem + "0", stem + "1"] if stem != name else [name])
+            return names
 
-        def quantiser(target, group, dtype, columns=slice(0, HALF)):
-            def quantise():
-                nc.vector.quantize_mx(
-                    out=target[0][:, columns].bitcast(dtype),
-                    scales=target[1][:, columns],
-                    in_=group[:].rearrange("p c j -> p (c j)"),
-                )
-
-            return quantise
+        vector_order = pairs_of(
+            "w3 q_w3 dpre0 dpre1 q_dpre0 q_dpre1 w4 dpre2 q_w4 dpre3 q_dpre2 q_dpre3 dpre4 dpre5 q_dpre4 dpre6 q_dpre5 dpre7 q_dpre6 dh0 q_dpre7 q_dh0 w0 st00_0 q_w0 st00_1 q_dxt0 q_st00 w1 q_st10 st01_* q_w1 w2 q_dxt1 q_w2 st11_1 q_st01 q_st11 dx0 xh0 q_dx0 dh1 q_xh0 dx1 q_dh1 xh1 q_dx1 q_xh1 xh2 xh3 q_xh2 xh4 q_xh3 xh5 q_xh4 xh6 q_xh5 xh7 q_xh6 q_xh7 shift3_01 shift3_11"
+        )
+        scalar_order = pairs_of(
+            "w4_a x3_0* h3_0* x3_1* h3_1* dxt0_* x3_2* h3_2* x3_3* h3_3* st10_* tap00_0* tap00_1* dxt1_* tap01_0* tap01_1* st11_0 tap10_0* tap10_1* tap11_0* tap11_1* tap20_0* tap20_1* tap21_0* tap21_1* shift0_0* shift0_1* shift1_0* shift1_1* shift2_0* shift2_1* shift3_00 shift3_10"
+        )
+        tensor_order = pairs_of(
+            "x3_0* h3_0* x3_1* h3_1* dxt0_* x3_2* h3_2* st00_* x3_3* h3_3* st10_* tap00_0* tap00_1* dxt1_* st01_* tap01_0* tap01_1* st11_* tap10_0* tap10_1* tap11_0* tap20_00 tap11_1* tap20_10 tap20_01 tap20_11 tap21_0* tap21_1* shift0_0* shift0_1* shift1_0* shift1_1* shift2_0* shift2_1* shift3_0* shift3_1*"
+        )
+        store_order = pairs_of("tap00 tap01_* tap10_* tap11_* tap20_* tap21_* shift0_* shift1_* shift2_* shift3_*")
+        spare_banks = pairs_of("tap20_00 tap20_10")
 
         def matmul(out, left, rows_out, left_dtype, right, columns, right_dtype, start=True, stop=True):
             nc.tensor.matmul_mx(
@@ -127,28 +137,43 @@ def tile_graphfilterrnnbatch_pb_v_kernel(
                 stop=stop,
             )
 
-        def new_bank(*shape):
-            bank = psum.tile([P, *shape], F32, name="bank")
-            return bank
+        def words_of(tile):
+            return tile[:].rearrange("p a b -> p (a b)").bitcast(F32)
 
-        def new_s_bank():
-            bank = psum_s.tile([P, 2, 2, P], F32, name="s_bank")
-            return bank
+        steps = {}
+        held = {}
 
-        def mix_dpre(i):
-            group = groups.tile([P, P, PACK], BF16, name="dpre_group", align_bytes=64, bufs=3)
-            nc.vector.scalar_tensor_tensor(
-                out=group[:],
-                in0=pre_sb[i // 2][:, :, block(i % 2)].rearrange("p j c -> p c j"),
-                scalar=0.0,
-                in1=grad_sb[i // 2][:, :, block(i % 2)].rearrange("p j c -> p c j"),
-                op0=IS_GT,
-                op1=MULT,
-            )
-            return quantiser(dpre_q, group, E5M2, block(i))
+        def step(name, needs, calls, **buffers):
+            steps[name] = (needs, buffers, calls)
 
-        def interleave(engine, group, source):
-            engine(group.rearrange("p (c i) j -> p c j i", i=2), source.rearrange("p j (c i) -> p c j i", i=2))
+        def group_of(name, columns, pool_name):
+            if name not in held:
+                held[name] = groups.tile([P, columns, PACK], BF16, name=pool_name, align_bytes=64, bufs=GROUP_BUFS[pool_name])
+            return held[name]
+
+        def quantise(name, needs, target, dtype, columns, pool_name):
+            def calls():
+                nc.vector.quantize_mx(
+                    out=target[0][:, columns].bitcast(dtype),
+                    scales=target[1][:, columns],
+                    in_=held[name][:].rearrange("p c j -> p (c j)"),
+                )
+
+            step("q_" + name, needs, calls, **{pool_name: -1})
+
+        def mask(i):
+            def calls():
+                nc.vector.scalar_tensor_tensor(
+                    out=group_of("dpre%d" % i, P, "dpre_group")[:],
+                    in0=pre_sb[i // 2][:, :, block(i % 2)].rearrange("p j c -> p c j"),
+                    scalar=0.0,
+                    in1=grad_sb[i // 2][:, :, block(i % 2)].rearrange("p j c -> p c j"),
+                    op0=IS_GT,
+                    op1=MULT,
+                )
+
+            step("dpre%d" % i, [], calls, dpre_group=1)
+            quantise("dpre%d" % i, ["dpre%d" % i], dpre_q, E5M2, block(i), "dpre_group")
 
         def interleave_by_four(engine, group, source, part):
             engine(
@@ -156,204 +181,224 @@ def tile_graphfilterrnnbatch_pb_v_kernel(
                 source.rearrange("p j (a b t) -> p a t j b", t=4, b=2)[:, part],
             )
 
-        def mix_w(k, on_scalar_eighths=0):
-            group = new_group()
-            cut = on_scalar_eighths * P // 16
-            if k < 2:
-                interleave(V, group[:], w_sb[k])
-            else:
-                if cut > 0:
-                    interleave_by_four(A, group[:], w_sb[k], slice(0, cut))
-                interleave_by_four(V, group[:], w_sb[k], slice(cut, P // 2))
-            return quantiser(w_q[k], group, E4M3)
+        def weight(k):
+            name = "w%d" % k
+            cut = SCALAR_EIGHTHS.get(k, 0) * P // 16
+            pool_name = "a_group" if cut else "group"
 
-        def mix_xh(g):
-            group = new_group()
-            V(
-                group[:].rearrange("p (s c i) j -> p s c j i", s=2, i=2),
-                xh_sb[:, :, :, quarter(g)].rearrange("p s j (c i) -> p s c j i", i=2),
-            )
-            return quantiser(xh_q[g], group, E4M3)
+            def on_vector_part():
+                group = group_of(name, HALF, pool_name)
+                interleave_by_four(V, group[:], w_sb[k], slice(cut, P // 2))
+
+            if cut:
+                step(
+                    name + "_a",
+                    [],
+                    lambda: interleave_by_four(A, group_of(name, HALF, pool_name)[:], w_sb[k], slice(0, cut)),
+                    a_group=1,
+                )
+                step(name, [name + "_a"], on_vector_part)
+            else:
+                step(name, [], on_vector_part, group=1)
+            quantise(name, [name], w_q[k], E4M3, half(0), pool_name)
+
+        def nodes(i):
+            def calls():
+                (V if "xh%d" % i in vector_order else A)(
+                    group_of("xh%d" % i, 2 * P, "xh_group")[:].rearrange("p (s c e) j -> p s c j e", s=2, e=2),
+                    xh_sb[:, :, :, block(i)].rearrange("p s j (c e) -> p s c j e", e=2),
+                )
+
+            step("xh%d" % i, [], calls, xh_group=1)
+            quantise("xh%d" % i, ["xh%d" % i], xh_q[i], E4M3, slice(0, 2 * P), "xh_group")
+
+        def bank_steps(name, needs, shape, fill, empty, pool_name="bank"):
+            def calls():
+                held[name] = (psum if pool_name == "bank" else psum_s).tile([P, *shape], F32, name=pool_name)
+                fill(held[name])
+
+            step("fill_" + name, needs, calls, **{pool_name: 1})
+            step(name, ["fill_" + name], lambda: empty(V if name in vector_order else A, held[name]), **{pool_name: -1})
 
         dx3_sb = [keep.tile([P, PACK, HALF], BF16, name="dx3_%d" % h, align_bytes=64) for h in range(2)]
         dh3_sb = [keep.tile([P, 2, HALF, 2], BF16, name="dh3_%d" % h, align_bytes=64) for h in range(2)]
 
-        def make_d3(s, q):
-            for u in range(2):
-                bank = new_bank(2, QUARTER)
+        def d3(s, q, u):
+            def fill(bank):
                 for e in range(2):
                     matmul(bank[:, e, :], w_q[LAST_TAP + s], block(2 * u + e), E4M3, dpre_q, quarter(q), E5M2)
+
+            def empty(engine, bank):
                 if s == X:
-                    A(
-                        dx3_sb[q // 2][:, 2 * u : 2 * u + 2, :].rearrange("p t (v r q e) -> p r t v q e", v=2, r=2, e=2)[
-                            :, q % 2
-                        ],
+                    target = dx3_sb[q // 2][:, 2 * u : 2 * u + 2, :]
+                    engine(
+                        target.rearrange("p t (v r q e) -> p r t v q e", v=2, r=2, e=2)[:, q % 2],
                         bank[:].rearrange("p t (q v e) -> p t v q e", v=2, e=2),
                     )
                 else:
-                    A(dh3_sb[q // 2][:, u, quarter(q % 2), :], bank[:].rearrange("p e n -> p n e"))
+                    engine(dh3_sb[q // 2][:, u, quarter(q % 2), :], bank[:].rearrange("p e n -> p n e"))
 
-        def mix_dh3(h):
-            group = new_group()
-            V(
-                words_of(group).rearrange("p (n u) -> p n u", u=2),
-                dh3_sb[h][:].rearrange("p u n e -> p (u n e)").bitcast(F32).rearrange("p (u n) -> p n u", u=2),
-            )
-            return quantiser(d3_q[H][h], group, E5M2)
+            needs = ["q_w%d" % (LAST_TAP + s), "q_dpre%d" % (2 * q), "q_dpre%d" % (2 * q + 1)]
+            bank_steps("xh"[s] + "3_%d%d" % (q, u), needs, (2, QUARTER), fill, empty)
 
-        def mix_dx3(h):
-            group = new_group()
-            V(
-                group[:].rearrange("p (q u e) t -> p u q t e", u=2, e=2),
-                dx3_sb[h][:].rearrange("p t (u q e) -> p u q t e", u=2, e=2),
-            )
-            return quantiser(d3_q[X][h], group, E5M2)
+        def d3_banks(s, h):
+            return ["xh"[s] + "3_%d%d" % (q, u) for q in (2 * h, 2 * h + 1) for u in range(2)]
 
-        def words_of(tile):
-            return tile[:].rearrange("p a b -> p (a b)").bitcast(F32)
+        def d3_group(s, h):
+            name = "d" + "xh"[s] + "%d" % h
+            engine, pool_name = (V, "group") if name in vector_order else (A, "a_group")
 
-        def transpose_dx3(h, engine=A):
-            words = words_of(dx3_sb[h])
-            group = new_group()
-            pairs = words_of(group).rearrange("p (c u) -> p c u", u=2)
+            def calls():
+                group = group_of(name, HALF, pool_name)
+                if s == X:
+                    engine(
+                        group[:].rearrange("p (q u e) t -> p u q t e", u=2, e=2),
+                        dx3_sb[h][:].rearrange("p t (u q e) -> p u q t e", u=2, e=2),
+                    )
+                else:
+                    engine(
+                        words_of(group).rearrange("p (n u) -> p n u", u=2),
+                        dh3_sb[h][:].rearrange("p u n e -> p (u n e)").bitcast(F32).rearrange("p (u n) -> p n u", u=2),
+                    )
+
+            step(name, d3_banks(s, h), calls, **{pool_name: 1})
+            quantise(name, [name], d3_q[s][h], E5M2, half(0), pool_name)
+
+        def dx3_transposed(h):
+            name = "dxt%d" % h
+
+            def bank(b):
+                def fill(bank):
+                    for i in range(2):
+                        for u in range(2):
+                            nc.tensor.transpose(
+                                bank[:, i, u, :], words_of(dx3_sb[h])[:, block(4 * b + 2 * i + u)], identity[:]
+                            )
+
+                def empty(engine, bank):
+                    pairs = words_of(group_of(name, HALF, "a_group")).rearrange("p (c u) -> p c u", u=2)
+                    engine(
+                        pairs[:, 2 * P * b : 2 * P * (b + 1), :].rearrange("p (i c) u -> p i c u", i=2),
+                        bank[:].rearrange("p i u c -> p i c u"),
+                    )
+
+                bank_steps(name + "_%d" % b, d3_banks(X, h), (2, 2, P), fill, empty)
+
             for b in range(2):
-                bank = new_bank(2, 2, P)
-                for i in range(2):
-                    for u in range(2):
-                        nc.tensor.transpose(bank[:, i, u, :], words[:, block(4 * b + 2 * i + u)], identity[:])
-                engine(
-                    pairs[:, 2 * P * b : 2 * P * (b + 1), :].rearrange("p (i c) u -> p i c u", i=2),
-                    bank[:].rearrange("p i u c -> p i c u"),
-                )
-            return quantiser(dx3t_q[h], group, E5M2)
+                bank(b)
+            steps[name + "_0"][1]["a_group"] = 1
+            quantise(name, [name + "_0", name + "_1"], dx3t_q[h], E5M2, half(0), "a_group")
 
-        def transpose_s(g, h):
-            words = words_of(s_sb[h])
-            banks = []
+        def s_transposed(g, h):
+            name = "st%d%d" % (g, h)
+            pool_name = "group" if name + "_0" in vector_order else "a_group"
+
+            def bank(b):
+                def fill(bank):
+                    for i in range(2):
+                        for u in range(2):
+                            low = ((2 * b + i) * NODES + g * HALF) // 2
+                            nc.tensor.transpose(
+                                bank[:, i, u, :], words_of(s_sb[h])[:, low + u : low + 2 * P : 2], identity[:]
+                            )
+
+                def empty(engine, bank):
+                    pairs = words_of(group_of(name, HALF, pool_name)).rearrange("p (c r u) -> p c r u", r=PACK, u=2)
+                    engine(pairs[:, :, 2 * b : 2 * b + 2, :], bank[:].rearrange("p i u c -> p c i u"))
+
+                bank_pool = "s_bank" if name + "_%d" % b in vector_order else "bank"
+                bank_steps(name + "_%d" % b, [], (2, 2, P), fill, empty, bank_pool)
+
             for b in range(2):
-                bank = new_s_bank()
-                banks.append(bank)
-                for i in range(2):
-                    for u in range(2):
-                        low = ((2 * b + i) * NODES + g * HALF) // 2
-                        nc.tensor.transpose(bank[:, i, u, :], words[:, low + u : low + 2 * P : 2], identity[:])
+                bank(b)
+            steps[name + "_0"][1][pool_name] = 1
+            steps[name + "_1"][0].append(name + "_0")
+            quantise(name, [name + "_0", name + "_1"], st_q[g][h], E4M3, half(0), pool_name)
 
-            def empty(engine):
-                group = new_group()
-                pairs = words_of(group).rearrange("p (c r u) -> p c r u", r=PACK, u=2)
-                for b in range(2):
-                    engine(pairs[:, :, 2 * b : 2 * b + 2, :], banks[b][:].rearrange("p i u c -> p c i u"))
-                return quantiser(st_q[g][h], group, E4M3)
+        def row_pair(name, target, needs, passes):
+            def bank(i, h):
+                def fill(bank):
+                    for n, one in enumerate(passes(i, h)):
+                        matmul(bank[:], *one, n == 0, n == len(passes(i, h)) - 1)
 
-            return empty
+                def empty(engine, bank):
+                    if name not in held:
+                        held[name] = rows.tile([P, 2, NODES], F32, name="row", align_bytes=64)
+                    engine(held[name][:, i, half(h)], bank[:])
 
-        def row_tile(target, passes):
-            row = rows.tile([P, NODES], F32, name="row", align_bytes=64)
+                spare = name + "_%d%d" % (i, h) in spare_banks
+                bank_steps(name + "_%d%d" % (i, h), needs(i, h), (HALF,), fill, empty, "s_bank" if spare else "bank")
+                if i + h > 0:
+                    steps[name + "_%d%d" % (i, h)][0].append(name + "_00")
 
-            def make(h, engine=A):
-                bank = new_bank(HALF)
-                steps = passes(h)
-                for n, step in enumerate(steps):
-                    matmul(bank[:], *step, n == 0, n == len(steps) - 1)
-                engine(row[:, half(h)], bank[:])
-                if h == 1:
-                    nc.sync.dma_start(out=target, in_=row[:])
+            def store(part):
+                return lambda: nc.sync.dma_start(out=target[:, part], in_=held[name][:, part])
 
-            return make
+            for i in range(2):
+                for h in range(2):
+                    bank(i, h)
+            steps[name + "_00"][1]["row"] = 1
+            if name in store_order:
+                step(name, pairs_of("%s_0* %s_1*" % (name, name)), store(slice(0, 2)), row=-1)
+            else:
+                step(name + "_0", pairs_of(name + "_0*"), store(0))
+                step(name + "_1", pairs_of(name + "_1*") + [name + "_0"], store(1), row=-1)
 
-        def both(make, second=A):
-            make(0)
-            make(1, second)
+        def dpre_half(h):
+            return ["q_dpre%d" % i for i in range(4 * h, 4 * h + 4)]
 
-        def direct(tap, i):
-            both(row_tile(out_0[0, tap, block(i), :], lambda h: [(w_q[tap], block(i), E4M3, dpre_q, half(h), E5M2)]))
+        def tap(k, a):
+            def needs(i, h):
+                back = ["q_dxt0", "q_dxt1", "q_st0%d" % h, "q_st1%d" % h] if k == 2 else []
+                return ["q_w%d" % k] + dpre_half(h) + back
 
-        def tap2(t):
-            return row_tile(
-                by_four(out_0[0, 2, :, :])[:, t, :],
-                lambda h: [(w_q[2], block(t), E4M3, dpre_q, half(h), E5M2)]
-                + [(dx3t_q[g], block(t), E5M2, st_q[g][h], half(0), E4M3) for g in range(2)],
+            def passes(i, h):
+                features = block(2 * a + i)
+                back = [(dx3t_q[g], features, E5M2, st_q[g][h], half(0), E4M3) for g in range(2)] if k == 2 else []
+                return [(w_q[k], features, E4M3, dpre_q, half(h), E5M2)] + back
+
+            row_pair("tap%d%d" % (k, a), by_four(out_0[0, k, :, :])[:, 2 * a : 2 * a + 2, :], needs, passes)
+
+        def shift(g):
+            row_pair(
+                "shift%d" % g,
+                out_1[0, quarter(g), :].rearrange("(i p) n -> p i n", i=2),
+                lambda i, h: ["q_xh%d" % (2 * g + i), "q_dx%d" % h, "q_dh%d" % h],
+                lambda i, h: [(xh_q[2 * g + i], block(s), E4M3, d3_q[s][h], half(0), E5M2) for s in (X, H)],
             )
 
-        def shift(i):
-            return row_tile(
-                out_1[0, block(i), :],
-                lambda h: [(xh_q[i // 2], block(2 * s + i % 2), E4M3, d3_q[s][h], half(0), E5M2) for s in (X, H)],
-            )
+        for i in range(8):
+            mask(i)
+            nodes(i)
+        for k in range(TAPS + 1):
+            weight(k)
+        for h in range(2):
+            dx3_transposed(h)
+            for k in range(LAST_TAP):
+                tap(k, h)
+            for s in (X, H):
+                d3_group(s, h)
+                s_transposed(s, h)
+        for q in range(4):
+            shift(q)
+            for s in (X, H):
+                for u in range(2):
+                    d3(s, q, u)
 
+
+        queues = [vector_order, scalar_order, ["fill_" + name for name in tensor_order], store_order]
+        free = dict(bank=BANKS, s_bank=S_BANKS, row=ROW_BUFS, **GROUP_BUFS)
+        done = set()
+        heads = [0] * len(queues)
         with tc.manual_schedule():
-            q_0 = mix_dpre(0)
-            q_1 = mix_dpre(1)
-            q_x = mix_w(LAST_TAP, 3)
-            q_0()
-            q_1()
-            q_x()
-            q_h = mix_w(TAPS, 4)
-            make_d3(X, 0)
-            q_h()
-            q_s00 = transpose_s(0, 0)(A)
-            make_d3(H, 0)
-            q_2 = mix_dpre(2)
-            q_3 = mix_dpre(3)
-            q_s10 = transpose_s(1, 0)(A)
-            q_2()
-            q_s00()
-            q_3()
-            make_d3(X, 1)
-            make_d3(H, 1)
-            q_4 = mix_dpre(4)
-            q_5 = mix_dpre(5)
-            q_4()
-            q_6 = mix_dpre(6)
-            q_5()
-            q_dx3t0 = transpose_dx3(0)
-            make_d3(X, 2)
-            make_d3(H, 2)
-            q_7 = mix_dpre(7)
-            q_6()
-            q_s10()
-            q_7()
-            make_d3(X, 3)
-            make_d3(H, 3)
-            q_w0 = mix_w(0)
-            q_dx3t0()
-            q_w0()
-            e_s = transpose_s(0, 1)
-            q_w1 = mix_w(1)
-            direct(0, 0)
-            q_s01 = e_s(V)
-            q_w1()
-            direct(0, 1)
-            q_dx3t1 = transpose_dx3(1)
-            e_s = transpose_s(1, 1)
-            q_w2 = mix_w(2)
-            q_s11 = e_s(V)
-            q_w2()
-            q_dx3t1()
-            q_s01()
-            q_s11()
-            direct(0, 2)
-            direct(0, 3)
-            tiles = [tap2(t) for t in range(PACK)]
-            direct(1, 0)
-            direct(1, 1)
-            for t in range(2):
-                both(tiles[t])
-                direct(1, 2 + t)
-            for t in range(2, 4):
-                both(tiles[t])
-            q_a = mix_dx3(0)
-            q_h = mix_dh3(0)
-            q_a()
-            q_x = mix_xh(0)
-            q_h()
-            q_h = mix_dh3(1)
-            q_x()
-            q_b = mix_dx3(1)
-            q_h()
-            q_b()
-            for g in range(4):
-                if g > 0:
-                    mix_xh(g)()
-                for i in (2 * g, 2 * g + 1):
-                    both(shift(i), A if i < 6 else V)
+            for turn in range(len(steps)):
+                for n, queue in enumerate(queues):
+                    if heads[n] < len(queue):
+                        needs, buffers, calls = steps[queue[heads[n]]]
+                        if all(need in done for need in needs) and all(free[b] >= c for b, c in buffers.items()):
+                            calls()
+                            for b, c in buffers.items():
+                                free[b] = free[b] - c
+                            done.add(queue[heads[n]])
+                            heads[n] = heads[n] + 1
+        assert len(done) == len(steps), [queue[n:] for queue, n in zip(queues, heads)]

@@ -20,11 +20,6 @@ HALF = 512
 QUARTER = 256
 TAPS = 4
 LAST_TAP = 3
-ROW_BUFS = 6
-BANKS = 6
-S_BANKS = 2
-SCALAR_EIGHTHS = {4: 4}
-GROUP_BUFS = dict(group=4, a_group=3, dpre_group=3, xh_group=3)
 X, H = 0, 1
 
 FLOPS = 2 * ((TAPS + 1) * FEATURES * FEATURES * NODES + FEATURES * NODES * NODES + 2 * FEATURES * NODES * NODES)
@@ -33,6 +28,9 @@ BYTES = (
     + 4 * FEATURES * NODES
     + 4 * (3 * FEATURES * NODES + NODES * NODES)
 )
+
+BUFFERS = dict(group=6, small=3, pairs=3, rows=6)
+SCALAR_SIXTEENTHS = {4: 8}
 
 
 def tile_graphfilterrnnbatch_pb_v_kernel(
@@ -46,14 +44,10 @@ def tile_graphfilterrnnbatch_pb_v_kernel(
     def on_scalar(out, in_):
         nc.scalar.copy(out=out, in_=in_)
 
-    V, A = on_vector, on_scalar
-
     with ExitStack() as ctx:
         keep = ctx.enter_context(tc.tile_pool(name="keep", bufs=1))
-        groups = ctx.enter_context(tc.tile_pool(name="groups", bufs=3))
-        rows = ctx.enter_context(tc.tile_pool(name="rows", bufs=ROW_BUFS))
-        psum = ctx.enter_context(tc.psum_pool(name="psum", bufs=BANKS))
-        psum_s = ctx.enter_context(tc.psum_pool(name="psum_s", bufs=S_BANKS))
+        rings = ctx.enter_context(tc.tile_pool(name="rings", bufs=2))
+        psum = ctx.enter_context(tc.psum_pool(name="psum", bufs=1))
 
         def half(h):
             return slice(h * HALF, (h + 1) * HALF)
@@ -64,33 +58,47 @@ def tile_graphfilterrnnbatch_pb_v_kernel(
         def block(i):
             return slice(i * P, (i + 1) * P)
 
+        def two(u):
+            return slice(2 * u, 2 * u + 2)
+
         def by_four(source):
             return source.rearrange("(p j) n -> p j n", j=PACK)
 
         def load(name, source, dtype):
-            tile = keep.tile([P, PACK, source.shape[-1]], dtype, name=name, align_bytes=64)
-            nc.sync.dma_start(out=tile[:], in_=by_four(source))
+            tile = keep.tile([P, *source.shape[1:]], dtype, name=name, align_bytes=64)
+            nc.sync.dma_start(out=tile[:], in_=source)
             return tile
 
+        def words_of(tile):
+            return tile[:].rearrange("p a b -> p (a b)").bitcast(F32)
+
         xh_sb = keep.tile([P, 2, PACK, NODES], BF16, name="xh", align_bytes=64)
-        w_last = load("w_last", weight_A[:, LAST_TAP, :], BF16)
-        grad_0 = load("grad_0", grad_out[0, :, half(0)], BF16)
-        pre_0 = load("pre_0", pre[0, :, quarter(0)], F32)
-        w_b = load("w_b", weight_B[:, LAST_TAP, :], BF16)
-        pre_1 = load("pre_1", pre[0, :, quarter(1)], F32)
-        grad_1 = load("grad_1", grad_out[0, :, half(1)], BF16)
-        pre_2 = load("pre_2", pre[0, :, quarter(2)], F32)
-        pre_3 = load("pre_3", pre[0, :, quarter(3)], F32)
-        s_0 = load("s_0", S[0, half(0), :], BF16)
-        w_0 = load("w_0", weight_A[:, 0, :], BF16)
-        w_12 = load("w_12", weight_A.rearrange("k t c -> k (t c)")[:, FEATURES : 3 * FEATURES], BF16)
-        s_1 = load("s_1", S[0, half(1), :], BF16)
+        w_rows = by_four(weight_A.rearrange("k t c -> k (t c)"))
+        pre_rows = by_four(pre[0])
+        grad_rows = by_four(grad_out[0])
+        w_last = load("w_last", w_rows[:, :, LAST_TAP * FEATURES :], BF16)
+        grad_0 = load("grad_0", grad_rows[:, :, half(0)], BF16)
+        pre_00 = load("pre_00", pre_rows[:, two(0), half(0)], F32)
+        pre_01a = load("pre_01a", pre_rows[:, two(1), quarter(0)], F32)
+        pre_01b = load("pre_01b", pre_rows[:, two(1), quarter(1)], F32)
+        w_b = load("w_b", by_four(weight_B[:, LAST_TAP, :]), BF16)
+        grad_1 = load("grad_1", grad_rows[:, :, half(1)], BF16)
+        pre_10 = load("pre_10", pre_rows[:, two(0), half(1)], F32)
+        pre_11 = load("pre_11", pre_rows[:, two(1), half(1)], F32)
+        s_0 = load("s_0", by_four(S[0, half(0), :]), BF16)
+        w_012 = load("w_012", w_rows[:, :, : 3 * FEATURES], BF16)
+        s_1 = load("s_1", by_four(S[0, half(1), :]), BF16)
         nc.sync.dma_start(out=xh_sb[:, X], in_=by_four(x_taps[0, 2, :, :]))
         nc.sync.dma_start(out=xh_sb[:, H], in_=by_four(h_taps[0, 2, :, :]))
-        pre_sb = [pre_0[:], pre_1[:], pre_2[:], pre_3[:]]
-        grad_sb = [(grad_0, grad_1)[q // 2][:, :, quarter(q % 2)] for q in range(4)]
+        pre_sb = [
+            [pre_00[:, :, quarter(0)], pre_01a[:]],
+            [pre_00[:, :, quarter(1)], pre_01b[:]],
+            [pre_10[:, :, quarter(0)], pre_11[:, :, quarter(0)]],
+            [pre_10[:, :, quarter(1)], pre_11[:, :, quarter(1)]],
+        ]
+        grad_sb = [grad_0, grad_1]
         s_sb = [s_0, s_1]
-        w_sb = [w_0[:], w_12[:, :, 0:FEATURES], w_12[:, :, FEATURES:], w_last[:], w_b[:]]
+        w_sb = [w_012[:, :, half(0)], w_012[:, :, half(1)], w_012[:, :, half(2)], w_last[:], w_b[:]]
 
         identity = keep.tile([P, P], F32, name="identity", align_bytes=64)
         make_identity(nc, identity[:])
@@ -106,25 +114,29 @@ def tile_graphfilterrnnbatch_pb_v_kernel(
         d3_q = [[operand("d3q_%d%d" % (s, h)) for h in range(2)] for s in (X, H)]
         dx3t_q = [operand("dx3t_%d" % g) for g in range(2)]
         st_q = [[operand("st_%d%d" % (g, h)) for h in range(2)] for g in range(2)]
+        dx3_sb = [keep.tile([P, PACK, HALF], BF16, name="dx3_%d" % h, align_bytes=64) for h in range(2)]
 
-        def pairs_of(text):
-            names = []
+        def names(text):
+            found = []
             for name in text.split():
                 stem = name.replace("*", "")
-                names.extend([stem + "0", stem + "1"] if stem != name else [name])
-            return names
+                found.extend([stem + "0", stem + "1"] if stem != name else [name])
+            return found
 
-        vector_order = pairs_of(
-            "w3 q_w3 dpre0 dpre1 q_dpre0 q_dpre1 w4 dpre2 q_w4 dpre3 q_dpre2 q_dpre3 dpre4 dpre5 q_dpre4 dpre6 q_dpre5 dpre7 q_dpre6 dh0 q_dpre7 q_dh0 w0 st00_0 q_w0 st00_1 q_dxt0 q_st00 w1 q_st10 st01_* q_w1 w2 q_dxt1 q_w2 st11_1 q_st01 q_st11 dx0 xh0 q_dx0 dh1 q_xh0 dx1 q_dh1 xh1 q_dx1 q_xh1 xh2 xh3 q_xh2 xh4 q_xh3 xh5 q_xh4 xh6 q_xh5 xh7 q_xh6 q_xh7 shift3_01 shift3_11"
+        vector_order = names(
+            "w3 q_w3 mask00 mask01 mask10 dpre0 mask11 q_dpre0 dpre1 w4 q_dpre1 q_w4 mask20 mask30 mask21 mask31 dpre2 dpre3 q_dpre2 q_dpre3 q_dxt0 x3_20 dh0 st00_0 q_dh0 w0 st00_1 q_w0 q_st00 w1 q_st10 st01_* q_w1 w2 q_dxt1 q_w2 st11_1 q_st01 q_st11 dx0 xh0 q_dx0 dh1 q_xh0 dx1 q_dh1 xh1 q_dx1 q_xh1 xh2 xh3 q_xh2 xh4 q_xh3 xh5 q_xh4 xh6 q_xh5 xh7 q_xh6 q_xh7 shift3_01 shift3_11"
         )
-        scalar_order = pairs_of(
-            "w4_a x3_0* h3_0* x3_1* h3_1* dxt0_* x3_2* h3_2* x3_3* h3_3* st10_* tap00_0* tap00_1* dxt1_* tap01_0* tap01_1* st11_0 tap10_0* tap10_1* tap11_0* tap11_1* tap20_0* tap20_1* tap21_0* tap21_1* shift0_0* shift0_1* shift1_0* shift1_1* shift2_0* shift2_1* shift3_00 shift3_10"
+        bank_order = names(
+            "x3_0* x3_1* h3_0* dxt0_* h3_10 h3_11 x3_2* x3_30 st00_0 x3_31 h3_2* st10_0 st00_1 st10_1 h3_3* tap00_0* tap00_10 st01_0 tap00_11 st01_1 dxt1_* tap01_0* tap01_1* st11_* tap10_0* tap10_1* tap11_0* tap11_1* tap20_0* tap20_1* tap21_0* tap21_1* shift0_0* shift0_1* shift1_0* shift1_1* shift2_0* shift2_1* shift3_0* shift3_1*"
         )
-        tensor_order = pairs_of(
-            "x3_0* h3_0* x3_1* h3_1* dxt0_* x3_2* h3_2* st00_* x3_3* h3_3* st10_* tap00_0* tap00_1* dxt1_* st01_* tap01_0* tap01_1* st11_* tap10_0* tap10_1* tap11_0* tap20_00 tap11_1* tap20_10 tap20_01 tap20_11 tap21_0* tap21_1* shift0_0* shift0_1* shift1_0* shift1_1* shift2_0* shift2_1* shift3_0* shift3_1*"
+        scalar_order = names("w4_a") + [name for name in bank_order if name not in vector_order]
+        tensor_order = names(
+            "x3_0* x3_1* h3_0* dxt0_* h3_1* x3_2* x3_3* st00_* h3_2* st10_* h3_3* dxt1_* tap00_0* tap00_1* st01_* tap01_0* tap01_1* st11_* tap10_0* tap10_1* tap11_0* tap20_00 tap11_1* tap20_10 tap20_01 tap20_11 tap21_0* tap21_1* shift0_0* shift0_1* shift1_0* shift1_1* shift2_0* shift2_1* shift3_0* shift3_1*"
         )
-        store_order = pairs_of("tap00 tap01_* tap10_* tap11_* tap20_* tap21_* shift0_* shift1_* shift2_* shift3_*")
-        spare_banks = pairs_of("tap20_00 tap20_10")
+        store_order = names("tap00_* tap01_* tap10_* tap11_* tap20_* tap21_* shift0_* shift1_* shift2_* shift3_0 shift3_1*")
+
+        def engine_of(name):
+            return on_vector if name in vector_order else on_scalar
 
         def matmul(out, left, rows_out, left_dtype, right, columns, right_dtype, start=True, stop=True):
             nc.tensor.matmul_mx(
@@ -137,91 +149,102 @@ def tile_graphfilterrnnbatch_pb_v_kernel(
                 stop=stop,
             )
 
-        def words_of(tile):
-            return tile[:].rearrange("p a b -> p (a b)").bitcast(F32)
-
         steps = {}
+        takes = {}
+        frees = {}
         held = {}
 
-        def step(name, needs, calls, **buffers):
-            steps[name] = (needs, buffers, calls)
+        def step(name, needs, calls):
+            steps[name] = (needs, calls)
 
-        def group_of(name, columns, pool_name):
-            if name not in held:
-                held[name] = groups.tile([P, columns, PACK], BF16, name=pool_name, align_bytes=64, bufs=GROUP_BUFS[pool_name])
-            return held[name]
+        def ring_tile(name, ring, shape, dtype, first, last):
+            for one in first:
+                takes[one] = (name, ring, shape, dtype)
+            frees.setdefault(last, []).append(ring)
 
-        def quantise(name, needs, target, dtype, columns, pool_name):
+        def quantise(name, needs, target, dtype, columns, writers, ring, width):
             def calls():
                 nc.vector.quantize_mx(
                     out=target[0][:, columns].bitcast(dtype),
                     scales=target[1][:, columns],
-                    in_=held[name][:].rearrange("p c j -> p (c j)"),
+                    in_=held["group_" + name][:].rearrange("p c j -> p (c j)"),
                 )
 
-            step("q_" + name, needs, calls, **{pool_name: -1})
+            step("q_" + name, needs, calls)
+            ring_tile("group_" + name, ring, [P, width, PACK], BF16, writers, "q_" + name)
 
-        def mask(i):
+        def join_pairs(engine, group, pairs):
+            engine(words_of(group).rearrange("p (n u) -> p n u", u=2), pairs.rearrange("p u n -> p n u"))
+
+        def pair_words(name):
+            return held[name][:].rearrange("p u n e -> p (u n e)").bitcast(F32).rearrange("p (u n) -> p u n", u=2)
+
+        def mask(q, u):
             def calls():
                 nc.vector.scalar_tensor_tensor(
-                    out=group_of("dpre%d" % i, P, "dpre_group")[:],
-                    in0=pre_sb[i // 2][:, :, block(i % 2)].rearrange("p j c -> p c j"),
+                    out=held["dpre_pairs%d" % (q // 2)][:, u, quarter(q % 2), :],
+                    in0=pre_sb[q][u].rearrange("p e c -> p c e"),
                     scalar=0.0,
-                    in1=grad_sb[i // 2][:, :, block(i % 2)].rearrange("p j c -> p c j"),
+                    in1=grad_sb[q // 2][:, two(u), quarter(q % 2)].rearrange("p e c -> p c e"),
                     op0=IS_GT,
                     op1=MULT,
                 )
 
-            step("dpre%d" % i, [], calls, dpre_group=1)
-            quantise("dpre%d" % i, ["dpre%d" % i], dpre_q, E5M2, block(i), "dpre_group")
+            step("mask%d%d" % (q, u), [], calls)
 
-        def interleave_by_four(engine, group, source, part):
-            engine(
-                group.rearrange("p (t a b) j -> p a t j b", t=4, b=2)[:, part],
-                source.rearrange("p j (a b t) -> p a t j b", t=4, b=2)[:, part],
+        def dpre(q):
+            name = "dpre%d" % q
+            mask(q, 0)
+            mask(q, 1)
+            step(
+                name,
+                ["mask%d0" % q, "mask%d1" % q],
+                lambda: join_pairs(
+                    engine_of(name), held["group_" + name], pair_words("dpre_pairs%d" % (q // 2))[:, :, quarter(q % 2)]
+                ),
             )
+            quantise(name, [name], dpre_q, E5M2, quarter(q), [name], "small", QUARTER)
 
         def weight(k):
             name = "w%d" % k
-            cut = SCALAR_EIGHTHS.get(k, 0) * P // 16
-            pool_name = "a_group" if cut else "group"
+            cut = SCALAR_SIXTEENTHS.get(k, 0) * P // 32
 
-            def on_vector_part():
-                group = group_of(name, HALF, pool_name)
-                interleave_by_four(V, group[:], w_sb[k], slice(cut, P // 2))
+            def part(engine, columns):
+                def calls():
+                    engine(
+                        held["group_" + name][:].rearrange("p (t a b) j -> p a t j b", t=4, b=2)[:, columns],
+                        w_sb[k].rearrange("p j (a b t) -> p a t j b", t=4, b=2)[:, columns],
+                    )
 
-            if cut:
-                step(
-                    name + "_a",
-                    [],
-                    lambda: interleave_by_four(A, group_of(name, HALF, pool_name)[:], w_sb[k], slice(0, cut)),
-                    a_group=1,
-                )
-                step(name, [name + "_a"], on_vector_part)
-            else:
-                step(name, [], on_vector_part, group=1)
-            quantise(name, [name], w_q[k], E4M3, half(0), pool_name)
+                return calls
+
+            parts = []
+            if cut > 0:
+                parts.append(name + "_a")
+                step(name + "_a", [], part(on_scalar, slice(0, cut)))
+            if cut < P // 2:
+                parts.append(name)
+                step(name, [], part(on_vector, slice(cut, P // 2)))
+            quantise(name, parts, w_q[k], E4M3, half(0), parts, "group", HALF)
 
         def nodes(i):
+            name = "xh%d" % i
+
             def calls():
-                (V if "xh%d" % i in vector_order else A)(
-                    group_of("xh%d" % i, 2 * P, "xh_group")[:].rearrange("p (s c e) j -> p s c j e", s=2, e=2),
+                engine_of(name)(
+                    held["group_" + name][:].rearrange("p (s c e) j -> p s c j e", s=2, e=2),
                     xh_sb[:, :, :, block(i)].rearrange("p s j (c e) -> p s c j e", e=2),
                 )
 
-            step("xh%d" % i, [], calls, xh_group=1)
-            quantise("xh%d" % i, ["xh%d" % i], xh_q[i], E4M3, slice(0, 2 * P), "xh_group")
+            step(name, [], calls)
+            quantise(name, [name], xh_q[i], E4M3, slice(0, 2 * P), [name], "small", 2 * P)
 
-        def bank_steps(name, needs, shape, fill, empty, pool_name="bank"):
-            def calls():
-                held[name] = (psum if pool_name == "bank" else psum_s).tile([P, *shape], F32, name=pool_name)
-                fill(held[name])
+        banks = {}
 
-            step("fill_" + name, needs, calls, **{pool_name: 1})
-            step(name, ["fill_" + name], lambda: empty(V if name in vector_order else A, held[name]), **{pool_name: -1})
-
-        dx3_sb = [keep.tile([P, PACK, HALF], BF16, name="dx3_%d" % h, align_bytes=64) for h in range(2)]
-        dh3_sb = [keep.tile([P, 2, HALF, 2], BF16, name="dh3_%d" % h, align_bytes=64) for h in range(2)]
+        def bank_steps(name, needs, shape, fill, empty):
+            banks[name] = shape
+            step("fill_" + name, needs, lambda: fill(held["bank_" + name]))
+            step(name, ["fill_" + name], lambda: empty(engine_of(name), held["bank_" + name]))
 
         def d3(s, q, u):
             def fill(bank):
@@ -230,39 +253,34 @@ def tile_graphfilterrnnbatch_pb_v_kernel(
 
             def empty(engine, bank):
                 if s == X:
-                    target = dx3_sb[q // 2][:, 2 * u : 2 * u + 2, :]
+                    target = dx3_sb[q // 2][:, two(u), :]
                     engine(
                         target.rearrange("p t (v r q e) -> p r t v q e", v=2, r=2, e=2)[:, q % 2],
                         bank[:].rearrange("p t (q v e) -> p t v q e", v=2, e=2),
                     )
                 else:
-                    engine(dh3_sb[q // 2][:, u, quarter(q % 2), :], bank[:].rearrange("p e n -> p n e"))
+                    engine(held["dh3_pairs%d" % (q // 2)][:, u, quarter(q % 2), :], bank[:].rearrange("p e n -> p n e"))
 
-            needs = ["q_w%d" % (LAST_TAP + s), "q_dpre%d" % (2 * q), "q_dpre%d" % (2 * q + 1)]
-            bank_steps("xh"[s] + "3_%d%d" % (q, u), needs, (2, QUARTER), fill, empty)
+            bank_steps("xh"[s] + "3_%d%d" % (q, u), ["q_w%d" % (LAST_TAP + s), "q_dpre%d" % q], (2, QUARTER), fill, empty)
 
         def d3_banks(s, h):
             return ["xh"[s] + "3_%d%d" % (q, u) for q in (2 * h, 2 * h + 1) for u in range(2)]
 
         def d3_group(s, h):
             name = "d" + "xh"[s] + "%d" % h
-            engine, pool_name = (V, "group") if name in vector_order else (A, "a_group")
 
             def calls():
-                group = group_of(name, HALF, pool_name)
+                group = held["group_" + name]
                 if s == X:
-                    engine(
+                    engine_of(name)(
                         group[:].rearrange("p (q u e) t -> p u q t e", u=2, e=2),
                         dx3_sb[h][:].rearrange("p t (u q e) -> p u q t e", u=2, e=2),
                     )
                 else:
-                    engine(
-                        words_of(group).rearrange("p (n u) -> p n u", u=2),
-                        dh3_sb[h][:].rearrange("p u n e -> p (u n e)").bitcast(F32).rearrange("p (u n) -> p n u", u=2),
-                    )
+                    join_pairs(engine_of(name), group, pair_words("dh3_pairs%d" % h))
 
-            step(name, d3_banks(s, h), calls, **{pool_name: 1})
-            quantise(name, [name], d3_q[s][h], E5M2, half(0), pool_name)
+            step(name, d3_banks(s, h), calls)
+            quantise(name, [name], d3_q[s][h], E5M2, half(0), [name], "group", HALF)
 
         def dx3_transposed(h):
             name = "dxt%d" % h
@@ -276,9 +294,9 @@ def tile_graphfilterrnnbatch_pb_v_kernel(
                             )
 
                 def empty(engine, bank):
-                    pairs = words_of(group_of(name, HALF, "a_group")).rearrange("p (c u) -> p c u", u=2)
+                    pairs = words_of(held["group_" + name]).rearrange("p (c u) -> p c u", u=2)
                     engine(
-                        pairs[:, 2 * P * b : 2 * P * (b + 1), :].rearrange("p (i c) u -> p i c u", i=2),
+                        pairs[:, quarter(b), :].rearrange("p (i c) u -> p i c u", i=2),
                         bank[:].rearrange("p i u c -> p i c u"),
                     )
 
@@ -286,12 +304,10 @@ def tile_graphfilterrnnbatch_pb_v_kernel(
 
             for b in range(2):
                 bank(b)
-            steps[name + "_0"][1]["a_group"] = 1
-            quantise(name, [name + "_0", name + "_1"], dx3t_q[h], E5M2, half(0), "a_group")
+            quantise(name, names(name + "_*"), dx3t_q[h], E5M2, half(0), names(name + "_*"), "group", HALF)
 
         def s_transposed(g, h):
             name = "st%d%d" % (g, h)
-            pool_name = "group" if name + "_0" in vector_order else "a_group"
 
             def bank(b):
                 def fill(bank):
@@ -303,17 +319,14 @@ def tile_graphfilterrnnbatch_pb_v_kernel(
                             )
 
                 def empty(engine, bank):
-                    pairs = words_of(group_of(name, HALF, pool_name)).rearrange("p (c r u) -> p c r u", r=PACK, u=2)
-                    engine(pairs[:, :, 2 * b : 2 * b + 2, :], bank[:].rearrange("p i u c -> p c i u"))
+                    pairs = words_of(held["group_" + name]).rearrange("p (c r u) -> p c r u", r=PACK, u=2)
+                    engine(pairs[:, :, two(b), :], bank[:].rearrange("p i u c -> p c i u"))
 
-                bank_pool = "s_bank" if name + "_%d" % b in vector_order else "bank"
-                bank_steps(name + "_%d" % b, [], (2, 2, P), fill, empty, bank_pool)
+                bank_steps(name + "_%d" % b, [], (2, 2, P), fill, empty)
 
             for b in range(2):
                 bank(b)
-            steps[name + "_0"][1][pool_name] = 1
-            steps[name + "_1"][0].append(name + "_0")
-            quantise(name, [name + "_0", name + "_1"], st_q[g][h], E4M3, half(0), pool_name)
+            quantise(name, names(name + "_*"), st_q[g][h], E4M3, half(0), names(name + "_*"), "group", HALF)
 
         def row_pair(name, target, needs, passes):
             def bank(i, h):
@@ -322,42 +335,43 @@ def tile_graphfilterrnnbatch_pb_v_kernel(
                         matmul(bank[:], *one, n == 0, n == len(passes(i, h)) - 1)
 
                 def empty(engine, bank):
-                    if name not in held:
-                        held[name] = rows.tile([P, 2, NODES], F32, name="row", align_bytes=64)
-                    engine(held[name][:, i, half(h)], bank[:])
+                    engine(held["rows_" + name][:, i, half(h)], bank[:])
 
-                spare = name + "_%d%d" % (i, h) in spare_banks
-                bank_steps(name + "_%d%d" % (i, h), needs(i, h), (HALF,), fill, empty, "s_bank" if spare else "bank")
-                if i + h > 0:
-                    steps[name + "_%d%d" % (i, h)][0].append(name + "_00")
+                bank_steps(name + "_%d%d" % (i, h), needs(i, h), (HALF,), fill, empty)
 
-            def store(part):
-                return lambda: nc.sync.dma_start(out=target[:, part], in_=held[name][:, part])
+            def store(part, columns=slice(0, NODES)):
+                return lambda: nc.sync.dma_start(
+                    out=target[:, part, columns], in_=held["rows_" + name][:, part, columns]
+                )
 
             for i in range(2):
                 for h in range(2):
                     bank(i, h)
-            steps[name + "_00"][1]["row"] = 1
+            all_banks = names("%s_0* %s_1*" % (name, name))
             if name in store_order:
-                step(name, pairs_of("%s_0* %s_1*" % (name, name)), store(slice(0, 2)), row=-1)
+                step("store_" + name, all_banks, store(slice(0, 2)))
+                ring_tile("rows_" + name, "rows", [P, 2, NODES], F32, all_banks, "store_" + name)
             else:
-                step(name + "_0", pairs_of(name + "_0*"), store(0))
-                step(name + "_1", pairs_of(name + "_1*") + [name + "_0"], store(1), row=-1)
-
-        def dpre_half(h):
-            return ["q_dpre%d" % i for i in range(4 * h, 4 * h + 4)]
+                step("store_" + name + "_0", names(name + "_0*"), store(0))
+                if name + "_1" in store_order:
+                    step("store_" + name + "_1", names(name + "_1*"), store(1))
+                else:
+                    for h in range(2):
+                        step("store_" + name + "_1%d" % h, [name + "_1%d" % h], store(1, half(h)))
+                later = [one for one in store_order if one.startswith(name)][-1]
+                ring_tile("rows_" + name, "rows", [P, 2, NODES], F32, all_banks, "store_" + later)
 
         def tap(k, a):
             def needs(i, h):
                 back = ["q_dxt0", "q_dxt1", "q_st0%d" % h, "q_st1%d" % h] if k == 2 else []
-                return ["q_w%d" % k] + dpre_half(h) + back
+                return ["q_w%d" % k, "q_dpre%d" % (2 * h), "q_dpre%d" % (2 * h + 1)] + back
 
             def passes(i, h):
                 features = block(2 * a + i)
                 back = [(dx3t_q[g], features, E5M2, st_q[g][h], half(0), E4M3) for g in range(2)] if k == 2 else []
                 return [(w_q[k], features, E4M3, dpre_q, half(h), E5M2)] + back
 
-            row_pair("tap%d%d" % (k, a), by_four(out_0[0, k, :, :])[:, 2 * a : 2 * a + 2, :], needs, passes)
+            row_pair("tap%d%d" % (k, a), by_four(out_0[0, k, :, :])[:, two(a), :], needs, passes)
 
         def shift(g):
             row_pair(
@@ -368,37 +382,62 @@ def tile_graphfilterrnnbatch_pb_v_kernel(
             )
 
         for i in range(8):
-            mask(i)
             nodes(i)
         for k in range(TAPS + 1):
             weight(k)
         for h in range(2):
             dx3_transposed(h)
+            first_mask = ["mask%d%d" % (q, u) for q in (2 * h, 2 * h + 1) for u in range(2)]
+            ring_tile("dpre_pairs%d" % h, "pairs", [P, 2, HALF, 2], BF16, first_mask, "dpre%d" % (2 * h + 1))
+            ring_tile("dh3_pairs%d" % h, "pairs", [P, 2, HALF, 2], BF16, d3_banks(H, h), "dh%d" % h)
             for k in range(LAST_TAP):
                 tap(k, h)
             for s in (X, H):
                 d3_group(s, h)
                 s_transposed(s, h)
         for q in range(4):
+            dpre(q)
             shift(q)
             for s in (X, H):
                 for u in range(2):
                     d3(s, q, u)
 
-
-        queues = [vector_order, scalar_order, ["fill_" + name for name in tensor_order], store_order]
-        free = dict(bank=BANKS, s_bank=S_BANKS, row=ROW_BUFS, **GROUP_BUFS)
+        queues = [
+            vector_order,
+            scalar_order,
+            ["fill_" + name for name in tensor_order],
+            ["store_" + name for name in store_order],
+        ]
+        free = dict(BUFFERS)
+        bank_of = {}
         done = set()
         heads = [0] * len(queues)
+
+        def ready(name):
+            if not all(need in done for need in steps[name][0]):
+                return False
+            if name in takes and takes[name][0] not in held and free[takes[name][1]] == 0:
+                return False
+            return name not in follows or follows[name] in done
+
+        def run(name):
+            if name in takes and takes[name][0] not in held:
+                tile_name, ring, shape, dtype = takes[name]
+                free[ring] = free[ring] - 1
+                held[tile_name] = rings.tile(shape, dtype, name=ring, align_bytes=64, bufs=BUFFERS[ring])
+            if name.startswith("fill_"):
+                bank_of[name[5:]] = bank_of[follows[name]] if name in follows else len(bank_of)
+                held["bank_" + name[5:]] = psum.tile([P, *banks[name[5:]]], F32, name="bank%d" % bank_of[name[5:]])
+            steps[name][1]()
+            for ring in frees.get(name, []):
+                free[ring] = free[ring] + 1
+            done.add(name)
+
+        follows = dict(zip(queues[2][8:], bank_order))
         with tc.manual_schedule():
             for turn in range(len(steps)):
                 for n, queue in enumerate(queues):
-                    if heads[n] < len(queue):
-                        needs, buffers, calls = steps[queue[heads[n]]]
-                        if all(need in done for need in needs) and all(free[b] >= c for b, c in buffers.items()):
-                            calls()
-                            for b, c in buffers.items():
-                                free[b] = free[b] - c
-                            done.add(queue[heads[n]])
-                            heads[n] = heads[n] + 1
+                    if heads[n] < len(queue) and ready(queue[heads[n]]):
+                        run(queue[heads[n]])
+                        heads[n] = heads[n] + 1
         assert len(done) == len(steps), [queue[n:] for queue, n in zip(queues, heads)]

@@ -124,16 +124,16 @@ def tile_graphfilterrnnbatch_pb_v_kernel(
             return found
 
         vector_order = names(
-            "w3 q_w3 mask00 mask01 mask10 dpre0 mask11 q_dpre0 dpre1 w4 q_dpre1 q_w4 mask20 mask30 mask21 mask31 dpre2 dpre3 q_dpre2 q_dpre3 q_dxt0 x3_20 dh0 st00_0 q_dh0 w0 st00_1 q_w0 q_st00 w1 q_st10 st01_* q_w1 w2 q_dxt1 q_w2 st11_1 q_st01 q_st11 dx0 xh0 q_dx0 dh1 q_xh0 dx1 q_dh1 xh1 q_dx1 q_xh1 xh2 xh3 q_xh2 xh4 q_xh3 xh5 q_xh4 xh6 q_xh5 xh7 q_xh6 q_xh7 shift3_01 shift3_11"
+            "w3 q_w3 mask00 mask01 mask10 dpre0 mask11 q_dpre0 dpre1 w4 q_dpre1 q_w4 mask20 mask30 mask21 mask31 dpre2 dpre3 q_dpre2 q_dpre3 dx0 q_dxt0 dh0 st00_0 q_dh0 w0 st00_1 q_w0 q_st00 dxt1_1 w1 q_st10 st01_* q_w1 w2 q_dxt1 q_w2 st11_1 q_st01 q_dx0 q_st11 xh0 dh1 q_xh0 dx1 q_dh1 xh1 q_dx1 xh2 q_xh1 xh3 q_xh2 xh4 q_xh3 xh5 q_xh4 xh6 q_xh5 xh7 q_xh6 q_xh7 shift3_01 shift3_11"
         )
         bank_order = names(
-            "x3_0* x3_1* h3_0* dxt0_* h3_10 h3_11 x3_2* x3_30 st00_0 x3_31 h3_2* st10_0 st00_1 st10_1 h3_3* tap00_0* tap00_10 st01_0 tap00_11 st01_1 dxt1_* tap01_0* tap01_1* st11_* tap10_0* tap10_1* tap11_0* tap11_1* tap20_0* tap20_1* tap21_0* tap21_1* shift0_0* shift0_1* shift1_0* shift1_1* shift2_0* shift2_1* shift3_0* shift3_1*"
+            "x3_0* x3_1* h3_0* dxt0_* h3_1* x3_2* x3_30 st00_0 x3_31 h3_2* st10_0 st00_1 st10_1 h3_3* dxt1_* tap00_0* tap00_1* st01_0 tap01_00 st01_1 tap01_01 tap01_1* st11_0 tap10_0* tap10_10 st11_1 tap10_11 tap11_0* tap11_1* tap20_0* tap20_1* tap21_0* tap21_1* shift0_0* shift0_1* shift1_0* shift1_1* shift2_0* shift2_1* shift3_0* shift3_1*"
         )
         scalar_order = names("w4_a") + [name for name in bank_order if name not in vector_order]
         tensor_order = names(
             "x3_0* x3_1* h3_0* dxt0_* h3_1* x3_2* x3_3* st00_* h3_2* st10_* h3_3* dxt1_* tap00_0* tap00_1* st01_* tap01_0* tap01_1* st11_* tap10_0* tap10_1* tap11_0* tap20_00 tap11_1* tap20_10 tap20_01 tap20_11 tap21_0* tap21_1* shift0_0* shift0_1* shift1_0* shift1_1* shift2_0* shift2_1* shift3_0* shift3_1*"
         )
-        store_order = names("tap00_* tap01_* tap10_* tap11_* tap20_* tap21_* shift0_* shift1_* shift2_* shift3_0 shift3_1*")
+        store_order = names("tap00_* tap01_* tap10_* tap11_* tap20_* tap21_* shift0_* shift1_* shift2_* shift3_*")
 
         def engine_of(name):
             return on_vector if name in vector_order else on_scalar
@@ -339,10 +339,8 @@ def tile_graphfilterrnnbatch_pb_v_kernel(
 
                 bank_steps(name + "_%d%d" % (i, h), needs(i, h), (HALF,), fill, empty)
 
-            def store(part, columns=slice(0, NODES)):
-                return lambda: nc.sync.dma_start(
-                    out=target[:, part, columns], in_=held["rows_" + name][:, part, columns]
-                )
+            def store(part):
+                return lambda: nc.sync.dma_start(out=target[:, part], in_=held["rows_" + name][:, part])
 
             for i in range(2):
                 for h in range(2):
@@ -353,12 +351,8 @@ def tile_graphfilterrnnbatch_pb_v_kernel(
                 ring_tile("rows_" + name, "rows", [P, 2, NODES], F32, all_banks, "store_" + name)
             else:
                 step("store_" + name + "_0", names(name + "_0*"), store(0))
-                if name + "_1" in store_order:
-                    step("store_" + name + "_1", names(name + "_1*"), store(1))
-                else:
-                    for h in range(2):
-                        step("store_" + name + "_1%d" % h, [name + "_1%d" % h], store(1, half(h)))
-                later = [one for one in store_order if one.startswith(name)][-1]
+                step("store_" + name + "_1", names(name + "_1*"), store(1))
+                later = max(names(name + "_*"), key=store_order.index)
                 ring_tile("rows_" + name, "rows", [P, 2, NODES], F32, all_banks, "store_" + later)
 
         def tap(k, a):

@@ -30,7 +30,7 @@ BYTES = (
 )
 
 BUFFERS = dict(group=6, small=3, pairs=3, rows=6)
-SCALAR_SIXTEENTHS = {4: 8}
+SCALAR_SIXTEENTHS = {4: 9}
 
 
 def tile_graphfilterrnnbatch_pb_v_kernel(
@@ -86,7 +86,8 @@ def tile_graphfilterrnnbatch_pb_v_kernel(
         pre_10 = load("pre_10", pre_rows[:, two(0), half(1)], F32)
         pre_11 = load("pre_11", pre_rows[:, two(1), half(1)], F32)
         s_0 = load("s_0", by_four(S[0, half(0), :]), BF16)
-        w_012 = load("w_012", w_rows[:, :, : 3 * FEATURES], BF16)
+        w_0 = load("w_0", w_rows[:, :, :FEATURES], BF16)
+        w_12 = load("w_12", w_rows[:, :, FEATURES : 3 * FEATURES], BF16)
         s_1 = load("s_1", by_four(S[0, half(1), :]), BF16)
         nc.sync.dma_start(out=xh_sb[:, X], in_=by_four(x_taps[0, 2, :, :]))
         nc.sync.dma_start(out=xh_sb[:, H], in_=by_four(h_taps[0, 2, :, :]))
@@ -98,7 +99,7 @@ def tile_graphfilterrnnbatch_pb_v_kernel(
         ]
         grad_sb = [grad_0, grad_1]
         s_sb = [s_0, s_1]
-        w_sb = [w_012[:, :, half(0)], w_012[:, :, half(1)], w_012[:, :, half(2)], w_last[:], w_b[:]]
+        w_sb = [w_0[:], w_12[:, :, half(0)], w_12[:, :, half(1)], w_last[:], w_b[:]]
 
         identity = keep.tile([P, P], F32, name="identity", align_bytes=64)
         make_identity(nc, identity[:])
@@ -124,16 +125,16 @@ def tile_graphfilterrnnbatch_pb_v_kernel(
             return found
 
         vector_order = names(
-            "w3 q_w3 mask00 mask01 mask10 dpre0 mask11 q_dpre0 dpre1 w4 q_dpre1 q_w4 mask20 mask30 mask21 mask31 dpre2 dpre3 q_dpre2 q_dpre3 dx0 q_dxt0 dh0 st00_0 q_dh0 w0 st00_1 q_w0 q_st00 dxt1_1 w1 q_st10 st01_* q_w1 w2 q_dxt1 q_w2 st11_1 q_st01 q_dx0 q_st11 xh0 dh1 q_xh0 dx1 q_dh1 xh1 q_dx1 xh2 q_xh1 xh3 q_xh2 xh4 q_xh3 xh5 q_xh4 xh6 q_xh5 xh7 q_xh6 q_xh7 shift3_01 shift3_11"
+            "w3 q_w3 mask00 mask01 mask10 dpre0 mask11 q_dpre0 dpre1 w4 q_dpre1 q_w4 mask20 mask30 mask21 mask31 dpre2 dpre3 q_dpre2 q_dpre3 dx0 w0 q_dxt0 q_w0 st00_* w1 q_st00 q_w1 w2 st01_* q_st10 q_w2 q_dxt1 st11_* q_st01 dh0 q_st11 xh0 q_dx0 dh1 q_dh0 q_xh0 dx1 q_dh1 xh1 q_dx1 xh2 q_xh1 xh3 q_xh2 xh4 q_xh3 xh5 q_xh4 xh6 q_xh5 xh7 q_xh6 q_xh7 shift3_01 shift3_11"
         )
         bank_order = names(
-            "x3_0* x3_1* h3_0* dxt0_* h3_1* x3_2* x3_30 st00_0 x3_31 h3_2* st10_0 st00_1 st10_1 h3_3* dxt1_* tap00_0* tap00_1* st01_0 tap01_00 st01_1 tap01_01 tap01_1* st11_0 tap10_0* tap10_10 st11_1 tap10_11 tap11_0* tap11_1* tap20_0* tap20_1* tap21_0* tap21_1* shift0_0* shift0_1* shift1_0* shift1_1* shift2_0* shift2_1* shift3_0* shift3_1*"
+            "x3_0* x3_1* h3_0* dxt0_* h3_1* x3_2* x3_3* h3_2* h3_30 st00_0 h3_31 st00_1 st10_0 tap00_0* tap00_1* st10_1 dxt1_0 st01_0 dxt1_1 st01_1 tap01_0* tap01_1* st11_0 tap10_00 st11_1 tap10_01 tap10_1* tap11_0* tap11_1* tap20_0* tap20_1* tap21_0* tap21_1* shift0_0* shift0_1* shift1_0* shift1_1* shift2_0* shift2_1* shift3_0* shift3_1*"
         )
         scalar_order = names("w4_a") + [name for name in bank_order if name not in vector_order]
         tensor_order = names(
-            "x3_0* x3_1* h3_0* dxt0_* h3_1* x3_2* x3_3* st00_* h3_2* st10_* h3_3* dxt1_* tap00_0* tap00_1* st01_* tap01_0* tap01_1* st11_* tap10_0* tap10_1* tap11_0* tap20_00 tap11_1* tap20_10 tap20_01 tap20_11 tap21_0* tap21_1* shift0_0* shift0_1* shift1_0* shift1_1* shift2_0* shift2_1* shift3_0* shift3_1*"
+            "x3_0* x3_1* h3_0* dxt0_* h3_1* x3_2* x3_3* st00_* h3_2* h3_3* st10_* tap00_0* tap00_1* dxt1_* st01_* tap01_0* tap01_1* st11_* tap10_0* tap10_1* tap11_0* tap20_00 tap11_1* tap20_10 tap20_01 tap20_11 tap21_0* tap21_1* shift0_0* shift0_1* shift1_0* shift1_1* shift2_0* shift2_1* shift3_0* shift3_1*"
         )
-        store_order = names("tap00_* tap01_* tap10_* tap11_* tap20_* tap21_* shift0_* shift1_* shift2_* shift3_*")
+        store_order = names("tap00 tap01_* tap10_* tap11_* tap20_* tap21_* shift0_* shift1_* shift2_* shift3_*")
 
         def engine_of(name):
             return on_vector if name in vector_order else on_scalar

@@ -29,7 +29,9 @@ BYTES = (
     + 4 * (3 * FEATURES * NODES + NODES * NODES)
 )
 
-BUFFERS = dict(group=6, small=3, pairs=3, rows=6)
+BUFFERS = dict(group=5, small=3, pairs=3, rows=6, taps=1)
+GPSIMD_PAIRS = 160
+ADD = mybir.AluOpType.add
 SCALAR_SIXTEENTHS = {4: 9}
 
 
@@ -43,6 +45,9 @@ def tile_graphfilterrnnbatch_pb_v_kernel(
 
     def on_scalar(out, in_):
         nc.scalar.copy(out=out, in_=in_)
+
+    def on_gpsimd(out, in_):
+        nc.gpsimd.tensor_scalar(out=out, in0=in_, scalar1=1.0, scalar2=0.0, op0=MULT, op1=ADD)
 
     with ExitStack() as ctx:
         keep = ctx.enter_context(tc.tile_pool(name="keep", bufs=1))
@@ -125,16 +130,18 @@ def tile_graphfilterrnnbatch_pb_v_kernel(
             return found
 
         vector_order = names(
-            "w3 q_w3 mask00 mask01 mask10 dpre0 mask11 q_dpre0 dpre1 w4 q_dpre1 q_w4 mask20 mask30 mask21 mask31 dpre2 dpre3 q_dpre2 q_dpre3 dx0 w0 q_dxt0 q_w0 st00_* w1 q_st00 q_w1 w2 st01_* q_st10 q_w2 q_dxt1 st11_* q_st01 dh0 q_st11 xh0 q_dx0 dh1 q_dh0 q_xh0 dx1 q_dh1 xh1 q_dx1 xh2 q_xh1 xh3 q_xh2 xh4 q_xh3 xh5 q_xh4 xh6 q_xh5 xh7 q_xh6 q_xh7 shift3_01 shift3_11"
+            "w3 q_w3 mask00 mask01 mask10 dpre0 mask11 q_dpre0 dpre1 w4 q_dpre1 q_w4 mask20 mask30 mask21 mask31 dpre2 dpre3 q_dpre2 q_dpre3 dx0 w0 q_dxt0 q_w0 st00_* st10_* w1 q_st00 q_w1 q_st10 w2 q_dxt1 q_w2 st01_* st11_* q_st01 dh0 q_st11 q_xh0 q_dx0 dh1 q_dh0 dx1 q_dh1 xh1 q_dx1 xh2 q_xh1 xh3 q_xh2 xh4 q_xh3 xh5 q_xh4 xh6 q_xh5 xh7 q_xh6 q_xh7 shift3_01 shift3_11"
         )
         bank_order = names(
-            "x3_0* x3_1* h3_0* dxt0_* h3_1* x3_2* x3_3* h3_2* h3_30 st00_0 h3_31 st00_1 st10_0 tap00_0* tap00_1* st10_1 dxt1_0 st01_0 dxt1_1 st01_1 tap01_0* tap01_1* st11_0 tap10_00 st11_1 tap10_01 tap10_1* tap11_0* tap11_1* tap20_0* tap20_1* tap21_0* tap21_1* shift0_0* shift0_1* shift1_0* shift1_1* shift2_0* shift2_1* shift3_0* shift3_1*"
+            "x3_0* x3_1* h3_0* dxt0_* h3_1* x3_2* x3_3* h3_2* h3_30 st00_0 h3_31 st00_1 tap00_00 st10_0 tap00_01 st10_1 tap00_1* dxt1_* tap01_0* tap01_1* tap10_00 st01_0 tap10_01 st01_1 tap10_10 st11_0 tap10_11 st11_1 tap11_0* tap11_1* tap20_0* tap20_1* tap21_0* tap21_1* shift0_0* shift0_1* shift1_0* shift1_1* shift2_0* shift2_1* shift3_0* shift3_1*"
         )
         scalar_order = names("w4_a") + [name for name in bank_order if name not in vector_order]
         tensor_order = names(
-            "x3_0* x3_1* h3_0* dxt0_* h3_1* x3_2* x3_3* st00_* h3_2* h3_3* st10_* tap00_0* tap00_1* dxt1_* st01_* tap01_0* tap01_1* st11_* tap10_0* tap10_1* tap11_0* tap20_00 tap11_1* tap20_10 tap20_01 tap20_11 tap21_0* tap21_1* shift0_0* shift0_1* shift1_0* shift1_1* shift2_0* shift2_1* shift3_0* shift3_1*"
+            "x3_0* x3_1* h3_0* dxt0_* h3_1* x3_2* x3_3* st00_* h3_2* h3_3* st10_* tap00_0* tap00_1* dxt1_* tap01_0* tap01_1* st01_* tap10_0* st11_* tap10_1* tap11_0* tap20_00 tap11_1* tap20_10 tap20_01 tap20_11 tap21_0* tap21_1* shift0_0* shift0_1* shift1_0* shift1_1* shift2_0* shift2_1* shift3_0* shift3_1*"
         )
-        store_order = names("tap00 tap01_* tap10_* tap11_* tap20_* tap21_* shift0_* shift1_* shift2_* shift3_*")
+        store_order = names("tap00 tap01 tap10 tap11 tap20 tap21_* shift0_* shift1_* shift2_* shift3_*")
+
+        gpsimd_order = names("w1_g xh0")
 
         def engine_of(name):
             return on_vector if name in vector_order else on_scalar
@@ -219,6 +226,17 @@ def tile_graphfilterrnnbatch_pb_v_kernel(
 
                 return calls
 
+            def pair_part(engine, columns):
+                return lambda: engine(
+                    held["group_" + name][:].rearrange("p (i m) j -> p m i j", i=2)[:, columns],
+                    w_sb[k].rearrange("p j (m i) -> p m i j", i=2)[:, columns],
+                )
+
+            if k == 1:
+                step(name + "_g", ["q_w0"], pair_part(on_gpsimd, slice(0, GPSIMD_PAIRS)))
+                step(name, [], pair_part(on_vector, slice(GPSIMD_PAIRS, QUARTER)))
+                quantise(name, [name + "_g", name], w_q[k], E4M3, half(0), [name + "_g", name], "taps", HALF)
+                return
             parts = []
             if cut > 0:
                 parts.append(name + "_a")
@@ -226,19 +244,26 @@ def tile_graphfilterrnnbatch_pb_v_kernel(
             if cut < P // 2:
                 parts.append(name)
                 step(name, [], part(on_vector, slice(cut, P // 2)))
-            quantise(name, parts, w_q[k], E4M3, half(0), parts, "group", HALF)
+            quantise(name, parts, w_q[k], E4M3, half(0), parts, "taps" if k < LAST_TAP else "group", HALF)
 
         def nodes(i):
             name = "xh%d" % i
 
             def calls():
-                engine_of(name)(
-                    held["group_" + name][:].rearrange("p (s c e) j -> p s c j e", s=2, e=2),
-                    xh_sb[:, :, :, block(i)].rearrange("p s j (c e) -> p s c j e", e=2),
-                )
+                if name in gpsimd_order:
+                    on_gpsimd(
+                        held["group_" + name][:].rearrange("p (s c) j -> p s c j", s=2),
+                        xh_sb[:, :, :, block(i)].rearrange("p s j c -> p s c j"),
+                    )
+                else:
+                    on_vector(
+                        held["group_" + name][:].rearrange("p (s c e) j -> p s c j e", s=2, e=2),
+                        xh_sb[:, :, :, block(i)].rearrange("p s j (c e) -> p s c j e", e=2),
+                    )
 
-            step(name, [], calls)
-            quantise(name, [name], xh_q[i], E4M3, slice(0, 2 * P), [name], "small", 2 * P)
+            step(name, ["q_w2"] if name in gpsimd_order else [], calls)
+            ring = "taps" if name in gpsimd_order else "small"
+            quantise(name, [name], xh_q[i], E4M3, slice(0, 2 * P), [name], ring, 2 * P)
 
         banks = {}
 
@@ -362,11 +387,15 @@ def tile_graphfilterrnnbatch_pb_v_kernel(
                 return ["q_w%d" % k, "q_dpre%d" % (2 * h), "q_dpre%d" % (2 * h + 1)] + back
 
             def passes(i, h):
-                features = block(2 * a + i)
+                features = block(2 * i + a if k == 1 else 2 * a + i)
                 back = [(dx3t_q[g], features, E5M2, st_q[g][h], half(0), E4M3) for g in range(2)] if k == 2 else []
                 return [(w_q[k], features, E4M3, dpre_q, half(h), E5M2)] + back
 
-            row_pair("tap%d%d" % (k, a), by_four(out_0[0, k, :, :])[:, two(a), :], needs, passes)
+            if k == 1:
+                target = out_0[0, k, quarter(a), :].rearrange("(p i) n -> p i n", i=2)
+            else:
+                target = by_four(out_0[0, k, :, :])[:, two(a), :]
+            row_pair("tap%d%d" % (k, a), target, needs, passes)
 
         def shift(g):
             row_pair(
@@ -402,6 +431,7 @@ def tile_graphfilterrnnbatch_pb_v_kernel(
             scalar_order,
             ["fill_" + name for name in tensor_order],
             ["store_" + name for name in store_order],
+            gpsimd_order,
         ]
         free = dict(BUFFERS)
         bank_of = {}

@@ -29,10 +29,10 @@ BYTES = (
     + 4 * (3 * FEATURES * NODES + NODES * NODES)
 )
 
-BUFFERS = dict(group=5, small=3, pairs=3, rows=6, taps=1)
-GPSIMD_PAIRS = 160
+BUFFERS = dict(group=6, small=3, pairs=3, rows=6, taps=1)
+GPSIMD_PAIRS = 208
 ADD = mybir.AluOpType.add
-SCALAR_SIXTEENTHS = {4: 9}
+SCALAR_SIXTEENTHS = {4: 7}
 
 
 def tile_graphfilterrnnbatch_pb_v_kernel(
@@ -51,7 +51,7 @@ def tile_graphfilterrnnbatch_pb_v_kernel(
 
     with ExitStack() as ctx:
         keep = ctx.enter_context(tc.tile_pool(name="keep", bufs=1))
-        rings = ctx.enter_context(tc.tile_pool(name="rings", bufs=2))
+        rings = ctx.enter_context(tc.tile_pool(name="rings", bufs=1))
         psum = ctx.enter_context(tc.psum_pool(name="psum", bufs=1))
 
         def half(h):
@@ -84,8 +84,7 @@ def tile_graphfilterrnnbatch_pb_v_kernel(
         w_last = load("w_last", w_rows[:, :, LAST_TAP * FEATURES :], BF16)
         grad_0 = load("grad_0", grad_rows[:, :, half(0)], BF16)
         pre_00 = load("pre_00", pre_rows[:, two(0), half(0)], F32)
-        pre_01a = load("pre_01a", pre_rows[:, two(1), quarter(0)], F32)
-        pre_01b = load("pre_01b", pre_rows[:, two(1), quarter(1)], F32)
+        pre_01 = load("pre_01", pre_rows[:, two(1), half(0)], F32)
         w_b = load("w_b", by_four(weight_B[:, LAST_TAP, :]), BF16)
         grad_1 = load("grad_1", grad_rows[:, :, half(1)], BF16)
         pre_10 = load("pre_10", pre_rows[:, two(0), half(1)], F32)
@@ -97,8 +96,8 @@ def tile_graphfilterrnnbatch_pb_v_kernel(
         nc.sync.dma_start(out=xh_sb[:, X], in_=by_four(x_taps[0, 2, :, :]))
         nc.sync.dma_start(out=xh_sb[:, H], in_=by_four(h_taps[0, 2, :, :]))
         pre_sb = [
-            [pre_00[:, :, quarter(0)], pre_01a[:]],
-            [pre_00[:, :, quarter(1)], pre_01b[:]],
+            [pre_00[:, :, quarter(0)], pre_01[:, :, quarter(0)]],
+            [pre_00[:, :, quarter(1)], pre_01[:, :, quarter(1)]],
             [pre_10[:, :, quarter(0)], pre_11[:, :, quarter(0)]],
             [pre_10[:, :, quarter(1)], pre_11[:, :, quarter(1)]],
         ]
@@ -130,14 +129,14 @@ def tile_graphfilterrnnbatch_pb_v_kernel(
             return found
 
         vector_order = names(
-            "w3 q_w3 mask00 mask01 mask10 dpre0 mask11 q_dpre0 dpre1 w4 q_dpre1 q_w4 mask20 mask30 mask21 mask31 dpre2 dpre3 q_dpre2 q_dpre3 dx0 w0 q_dxt0 q_w0 st00_* st10_* w1 q_st00 q_w1 q_st10 w2 q_dxt1 q_w2 st01_* st11_* q_st01 dh0 q_st11 q_xh0 q_dx0 dh1 q_dh0 dx1 q_dh1 xh1 q_dx1 xh2 q_xh1 xh3 q_xh2 xh4 q_xh3 xh5 q_xh4 xh6 q_xh5 xh7 q_xh6 q_xh7 shift3_01 shift3_11"
+            "w3 q_w3 mask00 mask10 mask01 mask11 q_dpre0 w4 q_dpre1 q_w4 mask20 mask30 mask21 mask31_0 dpre2 mask31_1 q_dpre2 dpre3 dx0_0 q_dpre3 w0 q_dxt0 q_w0 x3_31 st00_* st10_* w1 q_st00 q_w1 q_st10 w2 q_dxt1 q_w2 st01_* st11_* q_st01 q_st11 dx0_1 q_xh0 dh0 q_dx0 dx1_0 q_dh0 dx1_1 xh1 q_dx1 q_xh1 q_dh1 xh2 xh3 q_xh2 xh4 q_xh3 xh5 q_xh4 xh6 q_xh5 xh7 q_xh6 q_xh7 shift3_01 shift3_11"
         )
         bank_order = names(
-            "x3_0* x3_1* h3_0* dxt0_* h3_1* x3_2* x3_3* h3_2* h3_30 st00_0 h3_31 st00_1 tap00_00 st10_0 tap00_01 st10_1 tap00_1* dxt1_* tap01_0* tap01_1* tap10_00 st01_0 tap10_01 st01_1 tap10_10 st11_0 tap10_11 st11_1 tap11_0* tap11_1* tap20_0* tap20_1* tap21_0* tap21_1* shift0_0* shift0_1* shift1_0* shift1_1* shift2_0* shift2_1* shift3_0* shift3_1*"
+            "x3_0* x3_1* h3_0* dxt0_* h3_1* x3_2* h3_2* x3_3* h3_30 st00_0 h3_31 st00_1 tap00_00 st10_0 tap00_01 st10_1 tap00_1* dxt1_* tap01_0* tap01_1* tap10_00 st01_0 tap10_01 st01_1 tap10_10 st11_0 tap10_11 st11_1 tap11_0* tap11_1* tap20_0* tap20_1* dh1 tap21_0* tap21_1* shift0_0* shift0_1* shift1_0* shift1_1* shift2_0* shift2_1* shift3_0* shift3_1*"
         )
-        scalar_order = names("w4_a") + [name for name in bank_order if name not in vector_order]
+        scalar_order = names("dpre0 dpre1 w4_a") + [name for name in bank_order if name not in vector_order]
         tensor_order = names(
-            "x3_0* x3_1* h3_0* dxt0_* h3_1* x3_2* x3_3* st00_* h3_2* h3_3* st10_* tap00_0* tap00_1* dxt1_* tap01_0* tap01_1* st01_* tap10_0* st11_* tap10_1* tap11_0* tap20_00 tap11_1* tap20_10 tap20_01 tap20_11 tap21_0* tap21_1* shift0_0* shift0_1* shift1_0* shift1_1* shift2_0* shift2_1* shift3_0* shift3_1*"
+            "x3_0* x3_1* h3_0* dxt0_* h3_1* x3_2* h3_2* st00_* x3_3* h3_3* st10_* tap00_0* tap00_1* dxt1_* tap01_0* tap01_1* st01_* tap10_0* st11_* tap10_1* tap11_0* tap20_00 tap11_1* tap20_10 tap20_01 tap20_11 tap21_0* tap21_1* shift0_0* shift0_1* shift1_0* shift1_1* shift2_0* shift2_1* shift3_0* shift3_1*"
         )
         store_order = names("tap00 tap01 tap10 tap11 tap20 tap21_* shift0_* shift1_* shift2_* shift3_*")
 
@@ -168,7 +167,7 @@ def tile_graphfilterrnnbatch_pb_v_kernel(
         def ring_tile(name, ring, shape, dtype, first, last):
             for one in first:
                 takes[one] = (name, ring, shape, dtype)
-            frees.setdefault(last, []).append(ring)
+            frees.setdefault(last, []).append((name, ring))
 
         def quantise(name, needs, target, dtype, columns, writers, ring, width):
             def calls():
@@ -187,26 +186,30 @@ def tile_graphfilterrnnbatch_pb_v_kernel(
         def pair_words(name):
             return held[name][:].rearrange("p u n e -> p (u n e)").bitcast(F32).rearrange("p (u n) -> p u n", u=2)
 
-        def mask(q, u):
+        def mask(q, u, part, columns):
             def calls():
                 nc.vector.scalar_tensor_tensor(
-                    out=held["dpre_pairs%d" % (q // 2)][:, u, quarter(q % 2), :],
-                    in0=pre_sb[q][u].rearrange("p e c -> p c e"),
+                    out=held["dpre_pairs%d" % (q // 2)][:, u, quarter(q % 2), :][:, columns],
+                    in0=pre_sb[q][u].rearrange("p e c -> p c e")[:, columns],
                     scalar=0.0,
-                    in1=grad_sb[q // 2][:, two(u), quarter(q % 2)].rearrange("p e c -> p c e"),
+                    in1=grad_sb[q // 2][:, two(u), quarter(q % 2)].rearrange("p e c -> p c e")[:, columns],
                     op0=IS_GT,
                     op1=MULT,
                 )
 
-            step("mask%d%d" % (q, u), [], calls)
+            step("mask%d%d" % (q, u) + part, [], calls)
 
         def dpre(q):
             name = "dpre%d" % q
-            mask(q, 0)
-            mask(q, 1)
+            parts = []
+            for u in range(2):
+                whole = "mask%d%d" % (q, u) in vector_order
+                for part, columns in [("", quarter(0))] if whole else [("_0", block(0)), ("_1", block(1))]:
+                    mask(q, u, part, columns)
+                    parts.append("mask%d%d" % (q, u) + part)
             step(
                 name,
-                ["mask%d0" % q, "mask%d1" % q],
+                parts,
                 lambda: join_pairs(
                     engine_of(name), held["group_" + name], pair_words("dpre_pairs%d" % (q // 2))[:, :, quarter(q % 2)]
                 ),
@@ -295,18 +298,24 @@ def tile_graphfilterrnnbatch_pb_v_kernel(
         def d3_group(s, h):
             name = "d" + "xh"[s] + "%d" % h
 
-            def calls():
-                group = held["group_" + name]
-                if s == X:
-                    engine_of(name)(
-                        group[:].rearrange("p (q u e) t -> p u q t e", u=2, e=2),
-                        dx3_sb[h][:].rearrange("p t (u q e) -> p u q t e", u=2, e=2),
-                    )
-                else:
-                    join_pairs(engine_of(name), group, pair_words("dh3_pairs%d" % h))
+            def node_pairs(u):
+                return lambda: on_vector(
+                    held["group_" + name][:].rearrange("p (q u e) t -> p u q t e", u=2, e=2)[:, u],
+                    dx3_sb[h][:].rearrange("p t (u q e) -> p u q t e", u=2, e=2)[:, u],
+                )
 
-            step(name, d3_banks(s, h), calls)
-            quantise(name, [name], d3_q[s][h], E5M2, half(0), [name], "group", HALF)
+            if s == X:
+                parts = names(name + "_*")
+                for u in range(2):
+                    step(parts[u], d3_banks(s, h), node_pairs(u))
+            else:
+                parts = [name]
+                step(
+                    name,
+                    d3_banks(s, h),
+                    lambda: join_pairs(engine_of(name), held["group_" + name], pair_words("dh3_pairs%d" % h)),
+                )
+            quantise(name, parts, d3_q[s][h], E5M2, half(0), parts, "group", HALF)
 
         def dx3_transposed(h):
             name = "dxt%d" % h
@@ -433,7 +442,8 @@ def tile_graphfilterrnnbatch_pb_v_kernel(
             ["store_" + name for name in store_order],
             gpsimd_order,
         ]
-        free = dict(BUFFERS)
+        free = {ring: list(range(count)) for ring, count in BUFFERS.items()}
+        slot_of = {}
         bank_of = {}
         done = set()
         heads = [0] * len(queues)
@@ -441,24 +451,24 @@ def tile_graphfilterrnnbatch_pb_v_kernel(
         def ready(name):
             if not all(need in done for need in steps[name][0]):
                 return False
-            if name in takes and takes[name][0] not in held and free[takes[name][1]] == 0:
+            if name in takes and takes[name][0] not in held and len(free[takes[name][1]]) == 0:
                 return False
             return name not in follows or follows[name] in done
 
         def run(name):
             if name in takes and takes[name][0] not in held:
                 tile_name, ring, shape, dtype = takes[name]
-                free[ring] = free[ring] - 1
-                held[tile_name] = rings.tile(shape, dtype, name=ring, align_bytes=64, bufs=BUFFERS[ring])
+                slot_of[tile_name] = free[ring].pop(0)
+                held[tile_name] = rings.tile(shape, dtype, name=ring + str(slot_of[tile_name]), align_bytes=64)
             if name.startswith("fill_"):
                 bank_of[name[5:]] = bank_of[follows[name]] if name in follows else len(bank_of)
                 held["bank_" + name[5:]] = psum.tile([P, *banks[name[5:]]], F32, name="bank%d" % bank_of[name[5:]])
             steps[name][1]()
-            for ring in frees.get(name, []):
-                free[ring] = free[ring] + 1
+            for tile_name, ring in frees.get(name, []):
+                free[ring].append(slot_of[tile_name])
             done.add(name)
 
-        follows = dict(zip(queues[2][8:], bank_order))
+        follows = dict(zip(queues[2][8:], [name for name in bank_order if name in banks]))
         with tc.manual_schedule():
             for turn in range(len(steps)):
                 for n, queue in enumerate(queues):

@@ -32,7 +32,7 @@ BYTES = (
 BUFFERS = dict(group=6, small=3, pairs=3, rows=6, taps=1)
 GPSIMD_PAIRS = 208
 ADD = mybir.AluOpType.add
-SCALAR_SIXTEENTHS = {4: 7}
+WEIGHT_CUTS = {0: (4,), 4: (3, 5)}
 
 
 def tile_graphfilterrnnbatch_pb_v_kernel(
@@ -89,8 +89,8 @@ def tile_graphfilterrnnbatch_pb_v_kernel(
         grad_1 = load("grad_1", grad_rows[:, :, half(1)], BF16)
         pre_10 = load("pre_10", pre_rows[:, two(0), half(1)], F32)
         pre_11 = load("pre_11", pre_rows[:, two(1), half(1)], F32)
-        s_0 = load("s_0", by_four(S[0, half(0), :]), BF16)
         w_0 = load("w_0", w_rows[:, :, :FEATURES], BF16)
+        s_0 = load("s_0", by_four(S[0, half(0), :]), BF16)
         w_12 = load("w_12", w_rows[:, :, FEATURES : 3 * FEATURES], BF16)
         s_1 = load("s_1", by_four(S[0, half(1), :]), BF16)
         nc.sync.dma_start(out=xh_sb[:, X], in_=by_four(x_taps[0, 2, :, :]))
@@ -129,14 +129,14 @@ def tile_graphfilterrnnbatch_pb_v_kernel(
             return found
 
         vector_order = names(
-            "w3 q_w3 mask00 mask10 mask01 mask11 q_dpre0 w4 q_dpre1 q_w4 mask20 mask30 mask21 mask31_0 dpre2 mask31_1 q_dpre2 dpre3 dx0_0 q_dpre3 w0 q_dxt0 q_w0 x3_31 st00_* st10_* w1 q_st00 q_w1 q_st10 w2 q_dxt1 q_w2 st01_* st11_* q_st01 q_st11 dx0_1 q_xh0 dh0 q_dx0 dx1_0 q_dh0 dx1_1 xh1 q_dx1 q_xh1 q_dh1 xh2 xh3 q_xh2 xh4 q_xh3 xh5 q_xh4 xh6 q_xh5 xh7 q_xh6 q_xh7 shift3_01 shift3_11"
+            "w3 q_w3 mask00 mask10 mask01 mask11_0 dpre0 mask11_1 q_dpre0 w4_2 q_dpre1 q_w4 mask20 mask30 mask21 mask31_0 dpre2 mask31_1 q_dpre2 dpre3 w0_0 q_dpre3 w0_1 q_dxt0 q_w0 dx0_0 x3_31 st00_* st10_* w1 q_st00 q_w1 q_st10 w2 q_dxt1 q_w2 st01_* st11_* q_st01 q_st11 dx0_1 q_xh0 dh0 q_dx0 dx1_0 q_dh0 dx1_1 xh1 q_dx1 q_xh1 q_dh1 xh2 xh3 q_xh2 xh4 q_xh3 xh5 q_xh4 xh6 q_xh5 xh7 q_xh6 q_xh7 shift3_01 shift3_11"
         )
         bank_order = names(
-            "x3_0* x3_1* h3_0* dxt0_* h3_1* x3_2* h3_2* x3_3* h3_30 st00_0 h3_31 st00_1 tap00_00 st10_0 tap00_01 st10_1 tap00_1* dxt1_* tap01_0* tap01_1* tap10_00 st01_0 tap10_01 st01_1 tap10_10 st11_0 tap10_11 st11_1 tap11_0* tap11_1* tap20_0* tap20_1* dh1 tap21_0* tap21_1* shift0_0* shift0_1* shift1_0* shift1_1* shift2_0* shift2_1* shift3_0* shift3_1*"
+            "x3_0* x3_1* h3_0* dxt0_* h3_1* x3_2* h3_2* x3_31 x3_30 st00_0 h3_30 st00_1 h3_31 st10_0 tap00_00 st10_1 tap00_01 tap00_1* dxt1_* tap01_0* tap01_1* tap10_00 st01_0 tap10_01 st01_1 tap10_10 st11_0 tap10_11 st11_1 tap11_0* tap11_1* tap20_00 tap20_10 tap20_01 tap20_11 dh1 tap21_0* tap21_1* shift0_0* shift0_1* shift1_0* shift1_1* shift2_0* shift2_1* shift3_0* shift3_1*"
         )
-        scalar_order = names("dpre0 dpre1 w4_a") + [name for name in bank_order if name not in vector_order]
+        scalar_order = names("w4_0 dpre1 w4_1") + [name for name in bank_order if name not in vector_order]
         tensor_order = names(
-            "x3_0* x3_1* h3_0* dxt0_* h3_1* x3_2* h3_2* st00_* x3_3* h3_3* st10_* tap00_0* tap00_1* dxt1_* tap01_0* tap01_1* st01_* tap10_0* st11_* tap10_1* tap11_0* tap20_00 tap11_1* tap20_10 tap20_01 tap20_11 tap21_0* tap21_1* shift0_0* shift0_1* shift1_0* shift1_1* shift2_0* shift2_1* shift3_0* shift3_1*"
+            "x3_0* x3_1* h3_0* dxt0_* h3_1* x3_2* h3_2* x3_3* st00_* h3_3* tap00_0* st10_* tap00_1* dxt1_* tap01_0* tap01_1* st01_* tap10_0* tap10_1* st11_* tap11_0* tap11_1* tap20_00 tap20_10 tap20_01 tap20_11 tap21_0* tap21_1* shift0_0* shift0_1* shift1_0* shift1_1* shift2_0* shift2_1* shift3_0* shift3_1*"
         )
         store_order = names("tap00 tap01 tap10 tap11 tap20 tap21_* shift0_* shift1_* shift2_* shift3_*")
 
@@ -218,7 +218,7 @@ def tile_graphfilterrnnbatch_pb_v_kernel(
 
         def weight(k):
             name = "w%d" % k
-            cut = SCALAR_SIXTEENTHS.get(k, 0) * P // 32
+            cuts = [0] + [cut * P // 32 for cut in WEIGHT_CUTS.get(k, ())] + [P // 2]
 
             def part(engine, columns):
                 def calls():
@@ -240,13 +240,9 @@ def tile_graphfilterrnnbatch_pb_v_kernel(
                 step(name, [], pair_part(on_vector, slice(GPSIMD_PAIRS, QUARTER)))
                 quantise(name, [name + "_g", name], w_q[k], E4M3, half(0), [name + "_g", name], "taps", HALF)
                 return
-            parts = []
-            if cut > 0:
-                parts.append(name + "_a")
-                step(name + "_a", [], part(on_scalar, slice(0, cut)))
-            if cut < P // 2:
-                parts.append(name)
-                step(name, [], part(on_vector, slice(cut, P // 2)))
+            parts = [name + "_%d" % n for n in range(len(cuts) - 1)] if k in WEIGHT_CUTS else [name]
+            for n, one in enumerate(parts):
+                step(one, [], part(engine_of(one), slice(cuts[n], cuts[n + 1])))
             quantise(name, parts, w_q[k], E4M3, half(0), parts, "taps" if k < LAST_TAP else "group", HALF)
 
         def nodes(i):

@@ -82,12 +82,13 @@ def tile_graphfilterrnnbatch_pb_v_kernel(
         pre_rows = by_four(pre[0])
         grad_rows = by_four(grad_out[0])
         w_last = load("w_last", w_rows[:, :, LAST_TAP * FEATURES :], BF16)
-        grad_0 = load("grad_0", grad_rows[:, :, half(0)], BF16)
+        grad_0 = load("grad_0", grad_rows[:, two(0), :], BF16)
         pre_00 = load("pre_00", pre_rows[:, two(0), half(0)], F32)
+        grad_10 = load("grad_10", grad_rows[:, two(1), half(0)], BF16)
         pre_01 = load("pre_01", pre_rows[:, two(1), half(0)], F32)
         w_b = load("w_b", by_four(weight_B[:, LAST_TAP, :]), BF16)
-        grad_1 = load("grad_1", grad_rows[:, :, half(1)], BF16)
         pre_10 = load("pre_10", pre_rows[:, two(0), half(1)], F32)
+        grad_11 = load("grad_11", grad_rows[:, two(1), half(1)], BF16)
         pre_11 = load("pre_11", pre_rows[:, two(1), half(1)], F32)
         w_0 = load("w_0", w_rows[:, :, :FEATURES], BF16)
         s_0 = load("s_0", by_four(S[0, half(0), :]), BF16)
@@ -101,7 +102,7 @@ def tile_graphfilterrnnbatch_pb_v_kernel(
             [pre_10[:, :, quarter(0)], pre_11[:, :, quarter(0)]],
             [pre_10[:, :, quarter(1)], pre_11[:, :, quarter(1)]],
         ]
-        grad_sb = [grad_0, grad_1]
+        grad_sb = [[grad_0[:, :, quarter(q)], (grad_10, grad_11)[q // 2][:, :, quarter(q % 2)]] for q in range(4)]
         s_sb = [s_0, s_1]
         w_sb = [w_0[:], w_12[:, :, half(0)], w_12[:, :, half(1)], w_last[:], w_b[:]]
 
@@ -192,7 +193,7 @@ def tile_graphfilterrnnbatch_pb_v_kernel(
                     out=held["dpre_pairs%d" % (q // 2)][:, u, quarter(q % 2), :][:, columns],
                     in0=pre_sb[q][u].rearrange("p e c -> p c e")[:, columns],
                     scalar=0.0,
-                    in1=grad_sb[q // 2][:, two(u), quarter(q % 2)].rearrange("p e c -> p c e")[:, columns],
+                    in1=grad_sb[q][u].rearrange("p e c -> p c e")[:, columns],
                     op0=IS_GT,
                     op1=MULT,
                 )

from contextlib import ExitStack

import concourse.mybir as mybir
from concourse.masks import make_identity

F32 = mybir.dt.float32
BF16 = mybir.dt.bfloat16
U32 = mybir.dt.uint32
U8 = mybir.dt.uint8
E4M3 = mybir.dt.float8_e4m3fn_x4
E5M2 = mybir.dt.float8_e5m2_x4
IS_GT = mybir.AluOpType.is_gt
MULT = mybir.AluOpType.mult

P = 128
PACK = 4
FEATURES = 512
NODES = 1024
HALF = 512
QUARTER = 256
TAPS = 4
LAST_TAP = 3
X, H = 0, 1

FLOPS = 2 * ((TAPS + 1) * FEATURES * FEATURES * NODES + FEATURES * NODES * NODES + 2 * FEATURES * NODES * NODES)
BYTES = (
    2 * (2 * FEATURES * NODES + NODES * NODES + (TAPS + 1) * FEATURES * FEATURES + FEATURES * NODES)
    + 4 * FEATURES * NODES
    + 4 * (3 * FEATURES * NODES + NODES * NODES)
)

BUFFERS = dict(group=6, small=3, pairs=3, rows=6, taps=1)
GPSIMD_PAIRS = 208
ADD = mybir.AluOpType.add
WEIGHT_CUTS = {0: (4,), 4: (3, 5)}


def tile_graphfilterrnnbatch_pb_v_kernel(
    tc, x_taps, h_taps, S, weight_A, weight_B, bias_A, bias_B, pre, grad_out, out_0, out_1
):
    nc = tc.nc

    def on_vector(out, in_):
        nc.vector.tensor_copy(out=out, in_=in_)

    def on_scalar(out, in_):
        nc.scalar.copy(out=out, in_=in_)

    def on_gpsimd(out, in_):
        nc.gpsimd.tensor_scalar(out=out, in0=in_, scalar1=1.0, scalar2=0.0, op0=MULT, op1=ADD)

    with ExitStack() as ctx:
        keep = ctx.enter_context(tc.tile_pool(name="keep", bufs=1))
        rings = ctx.enter_context(tc.tile_pool(name="rings", bufs=1))
        psum = ctx.enter_context(tc.psum_pool(name="psum", bufs=1))

        def half(h):
            return slice(h * HALF, (h + 1) * HALF)

        def quarter(q):
            return slice(q * QUARTER, (q + 1) * QUARTER)

        def block(i):
            return slice(i * P, (i + 1) * P)

        def two(u):
            return slice(2 * u, 2 * u + 2)

        def by_four(source):
            return source.rearrange("(p j) n -> p j n", j=PACK)

        def load(name, source, dtype):
            tile = keep.tile([P, *source.shape[1:]], dtype, name=name, align_bytes=64)
            nc.sync.dma_start(out=tile[:], in_=source)
            return tile

        def words_of(tile):
            return tile[:].rearrange("p a b -> p (a b)").bitcast(F32)

        xh_sb = keep.tile([P, 2, PACK, NODES], BF16, name="xh", align_bytes=64)
        w_rows = by_four(weight_A.rearrange("k t c -> k (t c)"))
        pre_rows = by_four(pre[0])
        grad_rows = by_four(grad_out[0])
        w_last = load("w_last", w_rows[:, :, LAST_TAP * FEATURES :], BF16)
        grad_0 = load("grad_0", grad_rows[:, two(0), :], BF16)
        pre_00 = load("pre_00", pre_rows[:, two(0), half(0)], F32)
        grad_10 = load("grad_10", grad_rows[:, two(1), half(0)], BF16)
        pre_01 = load("pre_01", pre_rows[:, two(1), half(0)], F32)
        w_b = load("w_b", by_four(weight_B[:, LAST_TAP, :]), BF16)
        pre_10 = load("pre_10", pre_rows[:, two(0), half(1)], F32)
        grad_11 = load("grad_11", grad_rows[:, two(1), half(1)], BF16)
        pre_11 = load("pre_11", pre_rows[:, two(1), half(1)], F32)
        w_0 = load("w_0", w_rows[:, :, :FEATURES], BF16)
        s_0 = load("s_0", by_four(S[0, half(0), :]), BF16)
        w_12 = load("w_12", w_rows[:, :, FEATURES : 3 * FEATURES], BF16)
        s_1 = load("s_1", by_four(S[0, half(1), :]), BF16)
        nc.sync.dma_start(out=xh_sb[:, X], in_=by_four(x_taps[0, 2, :, :]))
        nc.sync.dma_start(out=xh_sb[:, H], in_=by_four(h_taps[0, 2, :, :]))
        pre_sb = [
            [pre_00[:, :, quarter(0)], pre_01[:, :, quarter(0)]],
            [pre_00[:, :, quarter(1)], pre_01[:, :, quarter(1)]],
            [pre_10[:, :, quarter(0)], pre_11[:, :, quarter(0)]],
            [pre_10[:, :, quarter(1)], pre_11[:, :, quarter(1)]],
        ]
        grad_sb = [[grad_0[:, :, quarter(q)], (grad_10, grad_11)[q // 2][:, :, quarter(q % 2)]] for q in range(4)]
        s_sb = [s_0, s_1]
        w_sb = [w_0[:], w_12[:, :, half(0)], w_12[:, :, half(1)], w_last[:], w_b[:]]

        identity = keep.tile([P, P], F32, name="identity", align_bytes=64)
        make_identity(nc, identity[:])

        def operand(name, columns=HALF):
            codes = keep.tile([P, columns], U32, name=name + "_codes", align_bytes=64)
            scales = keep.tile([P, columns], U8, name=name + "_scales", align_bytes=64)
            return codes, scales

        w_q = [operand("wq_%d" % k) for k in range(TAPS + 1)]
        dpre_q = operand("dpre", NODES)
        xh_q = [operand("xhq_%d" % i, 2 * P) for i in range(8)]
        d3_q = [[operand("d3q_%d%d" % (s, h)) for h in range(2)] for s in (X, H)]
        dx3t_q = [operand("dx3t_%d" % g) for g in range(2)]
        st_q = [[operand("st_%d%d" % (g, h)) for h in range(2)] for g in range(2)]
        dx3_sb = [keep.tile([P, PACK, HALF], BF16, name="dx3_%d" % h, align_bytes=64) for h in range(2)]

        def names(text):
            found = []
            for name in text.split():
                stem = name.replace("*", "")
                found.extend([stem + "0", stem + "1"] if stem != name else [name])
            return found

        vector_order = names(
            "w3 q_w3 mask00 mask10 mask01 mask11_0 dpre0 mask11_1 q_dpre0 w4_2 q_dpre1 q_w4 mask20 mask30 mask21 mask31_0 dpre2 mask31_1 q_dpre2 dpre3 w0_0 q_dpre3 w0_1 q_dxt0 q_w0 dx0_0 x3_31 st00_* st10_* w1 q_st00 q_w1 q_st10 w2 q_dxt1 q_w2 st01_* st11_* q_st01 q_st11 dx0_1 q_xh0 dh0 q_dx0 dx1_0 q_dh0 dx1_1 xh1 q_dx1 q_xh1 q_dh1 xh2 xh3 q_xh2 xh4 q_xh3 xh5 q_xh4 xh6 q_xh5 xh7 q_xh6 q_xh7 shift3_01 shift3_11"
        )
        bank_order = names(
            "x3_0* x3_1* h3_0* dxt0_* h3_1* x3_2* h3_2* x3_31 x3_30 st00_0 h3_30 st00_1 h3_31 st10_0 tap00_00 st10_1 tap00_01 tap00_1* dxt1_* tap01_0* tap01_1* tap10_00 st01_0 tap10_01 st01_1 tap10_10 st11_0 tap10_11 st11_1 tap11_0* tap11_1* tap20_00 tap20_10 tap20_01 tap20_11 dh1 tap21_0* tap21_1* shift0_0* shift0_1* shift1_0* shift1_1* shift2_0* shift2_1* shift3_0* shift3_1*"
        )
        scalar_order = names("w4_0 dpre1 w4_1") + [name for name in bank_order if name not in vector_order]
        tensor_order = names(
            "x3_0* x3_1* h3_0* dxt0_* h3_1* x3_2* h3_2* x3_3* st00_* h3_3* tap00_0* st10_* tap00_1* dxt1_* tap01_0* tap01_1* st01_* tap10_0* tap10_1* st11_* tap11_0* tap11_1* tap20_00 tap20_10 tap20_01 tap20_11 tap21_0* tap21_1* shift0_0* shift0_1* shift1_0* shift1_1* shift2_0* shift2_1* shift3_0* shift3_1*"
        )
        store_order = names("tap00 tap01 tap10 tap11 tap20 tap21_* shift0_* shift1_* shift2_* shift3_*")

        gpsimd_order = names("w1_g xh0")

        def engine_of(name):
            return on_vector if name in vector_order else on_scalar

        def matmul(out, left, rows_out, left_dtype, right, columns, right_dtype, start=True, stop=True):
            nc.tensor.matmul_mx(
                out=out,
                lhsT=left[0][:, rows_out].bitcast(left_dtype),
                lhsT_scale=left[1][:, rows_out],
                rhs=right[0][:, columns].bitcast(right_dtype),
                rhs_scale=right[1][:, columns],
                start=start,
                stop=stop,
            )

        steps = {}
        takes = {}
        frees = {}
        held = {}

        def step(name, needs, calls):
            steps[name] = (needs, calls)

        def ring_tile(name, ring, shape, dtype, first, last):
            for one in first:
                takes[one] = (name, ring, shape, dtype)
            frees.setdefault(last, []).append((name, ring))

        def quantise(name, needs, target, dtype, columns, writers, ring, width):
            def calls():
                nc.vector.quantize_mx(
                    out=target[0][:, columns].bitcast(dtype),
                    scales=target[1][:, columns],
                    in_=held["group_" + name][:].rearrange("p c j -> p (c j)"),
                )

            step("q_" + name, needs, calls)
            ring_tile("group_" + name, ring, [P, width, PACK], BF16, writers, "q_" + name)

        def join_pairs(engine, group, pairs):
            engine(words_of(group).rearrange("p (n u) -> p n u", u=2), pairs.rearrange("p u n -> p n u"))

        def pair_words(name):
            return held[name][:].rearrange("p u n e -> p (u n e)").bitcast(F32).rearrange("p (u n) -> p u n", u=2)

        def mask(q, u, part, columns):
            def calls():
                nc.vector.scalar_tensor_tensor(
                    out=held["dpre_pairs%d" % (q // 2)][:, u, quarter(q % 2), :][:, columns],
                    in0=pre_sb[q][u].rearrange("p e c -> p c e")[:, columns],
                    scalar=0.0,
                    in1=grad_sb[q][u].rearrange("p e c -> p c e")[:, columns],
                    op0=IS_GT,
                    op1=MULT,
                )

            step("mask%d%d" % (q, u) + part, [], calls)

        def dpre(q):
            name = "dpre%d" % q
            parts = []
            for u in range(2):
                whole = "mask%d%d" % (q, u) in vector_order
                for part, columns in [("", quarter(0))] if whole else [("_0", block(0)), ("_1", block(1))]:
                    mask(q, u, part, columns)
                    parts.append("mask%d%d" % (q, u) + part)
            step(
                name,
                parts,
                lambda: join_pairs(
                    engine_of(name), held["group_" + name], pair_words("dpre_pairs%d" % (q // 2))[:, :, quarter(q % 2)]
                ),
            )
            quantise(name, [name], dpre_q, E5M2, quarter(q), [name], "small", QUARTER)

        def weight(k):
            name = "w%d" % k
            cuts = [0] + [cut * P // 32 for cut in WEIGHT_CUTS.get(k, ())] + [P // 2]

            def part(engine, columns):
                def calls():
                    engine(
                        held["group_" + name][:].rearrange("p (t a b) j -> p a t j b", t=4, b=2)[:, columns],
                        w_sb[k].rearrange("p j (a b t) -> p a t j b", t=4, b=2)[:, columns],
                    )

                return calls

            def pair_part(engine, columns):
                return lambda: engine(
                    held["group_" + name][:].rearrange("p (i m) j -> p m i j", i=2)[:, columns],
                    w_sb[k].rearrange("p j (m i) -> p m i j", i=2)[:, columns],
                )

            if k == 1:
                step(name + "_g", ["q_w0"], pair_part(on_gpsimd, slice(0, GPSIMD_PAIRS)))
                step(name, [], pair_part(on_vector, slice(GPSIMD_PAIRS, QUARTER)))
                quantise(name, [name + "_g", name], w_q[k], E4M3, half(0), [name + "_g", name], "taps", HALF)
                return
            parts = [name + "_%d" % n for n in range(len(cuts) - 1)] if k in WEIGHT_CUTS else [name]
            for n, one in enumerate(parts):
                step(one, [], part(engine_of(one), slice(cuts[n], cuts[n + 1])))
            quantise(name, parts, w_q[k], E4M3, half(0), parts, "taps" if k < LAST_TAP else "group", HALF)

        def nodes(i):
            name = "xh%d" % i

            def calls():
                if name in gpsimd_order:
                    on_gpsimd(
                        held["group_" + name][:].rearrange("p (s c) j -> p s c j", s=2),
                        xh_sb[:, :, :, block(i)].rearrange("p s j c -> p s c j"),
                    )
                else:
                    on_vector(
                        held["group_" + name][:].rearrange("p (s c e) j -> p s c j e", s=2, e=2),
                        xh_sb[:, :, :, block(i)].rearrange("p s j (c e) -> p s c j e", e=2),
                    )

            step(name, ["q_w2"] if name in gpsimd_order else [], calls)
            ring = "taps" if name in gpsimd_order else "small"
            quantise(name, [name], xh_q[i], E4M3, slice(0, 2 * P), [name], ring, 2 * P)

        banks = {}

        def bank_steps(name, needs, shape, fill, empty):
            banks[name] = shape
            step("fill_" + name, needs, lambda: fill(held["bank_" + name]))
            step(name, ["fill_" + name], lambda: empty(engine_of(name), held["bank_" + name]))

        def d3(s, q, u):
            def fill(bank):
                for e in range(2):
                    matmul(bank[:, e, :], w_q[LAST_TAP + s], block(2 * u + e), E4M3, dpre_q, quarter(q), E5M2)

            def empty(engine, bank):
                if s == X:
                    target = dx3_sb[q // 2][:, two(u), :]
                    engine(
                        target.rearrange("p t (v r q e) -> p r t v q e", v=2, r=2, e=2)[:, q % 2],
                        bank[:].rearrange("p t (q v e) -> p t v q e", v=2, e=2),
                    )
                else:
                    engine(held["dh3_pairs%d" % (q // 2)][:, u, quarter(q % 2), :], bank[:].rearrange("p e n -> p n e"))

            bank_steps("xh"[s] + "3_%d%d" % (q, u), ["q_w%d" % (LAST_TAP + s), "q_dpre%d" % q], (2, QUARTER), fill, empty)

        def d3_banks(s, h):
            return ["xh"[s] + "3_%d%d" % (q, u) for q in (2 * h, 2 * h + 1) for u in range(2)]

        def d3_group(s, h):
            name = "d" + "xh"[s] + "%d" % h

            def node_pairs(u):
                return lambda: on_vector(
                    held["group_" + name][:].rearrange("p (q u e) t -> p u q t e", u=2, e=2)[:, u],
                    dx3_sb[h][:].rearrange("p t (u q e) -> p u q t e", u=2, e=2)[:, u],
                )

            if s == X:
                parts = names(name + "_*")
                for u in range(2):
                    step(parts[u], d3_banks(s, h), node_pairs(u))
            else:
                parts = [name]
                step(
                    name,
                    d3_banks(s, h),
                    lambda: join_pairs(engine_of(name), held["group_" + name], pair_words("dh3_pairs%d" % h)),
                )
            quantise(name, parts, d3_q[s][h], E5M2, half(0), parts, "group", HALF)

        def dx3_transposed(h):
            name = "dxt%d" % h

            def bank(b):
                def fill(bank):
                    for i in range(2):
                        for u in range(2):
                            nc.tensor.transpose(
                                bank[:, i, u, :], words_of(dx3_sb[h])[:, block(4 * b + 2 * i + u)], identity[:]
                            )

                def empty(engine, bank):
                    pairs = words_of(held["group_" + name]).rearrange("p (c u) -> p c u", u=2)
                    engine(
                        pairs[:, quarter(b), :].rearrange("p (i c) u -> p i c u", i=2),
                        bank[:].rearrange("p i u c -> p i c u"),
                    )

                bank_steps(name + "_%d" % b, d3_banks(X, h), (2, 2, P), fill, empty)

            for b in range(2):
                bank(b)
            quantise(name, names(name + "_*"), dx3t_q[h], E5M2, half(0), names(name + "_*"), "group", HALF)

        def s_transposed(g, h):
            name = "st%d%d" % (g, h)

            def bank(b):
                def fill(bank):
                    for i in range(2):
                        for u in range(2):
                            low = ((2 * b + i) * NODES + g * HALF) // 2
                            nc.tensor.transpose(
                                bank[:, i, u, :], words_of(s_sb[h])[:, low + u : low + 2 * P : 2], identity[:]
                            )

                def empty(engine, bank):
                    pairs = words_of(held["group_" + name]).rearrange("p (c r u) -> p c r u", r=PACK, u=2)
                    engine(pairs[:, :, two(b), :], bank[:].rearrange("p i u c -> p c i u"))

                bank_steps(name + "_%d" % b, [], (2, 2, P), fill, empty)

            for b in range(2):
                bank(b)
            quantise(name, names(name + "_*"), st_q[g][h], E4M3, half(0), names(name + "_*"), "group", HALF)

        def row_pair(name, target, needs, passes):
            def bank(i, h):
                def fill(bank):
                    for n, one in enumerate(passes(i, h)):
                        matmul(bank[:], *one, n == 0, n == len(passes(i, h)) - 1)

                def empty(engine, bank):
                    engine(held["rows_" + name][:, i, half(h)], bank[:])

                bank_steps(name + "_%d%d" % (i, h), needs(i, h), (HALF,), fill, empty)

            def store(part):
                return lambda: nc.sync.dma_start(out=target[:, part], in_=held["rows_" + name][:, part])

            for i in range(2):
                for h in range(2):
                    bank(i, h)
            all_banks = names("%s_0* %s_1*" % (name, name))
            if name in store_order:
                step("store_" + name, all_banks, store(slice(0, 2)))
                ring_tile("rows_" + name, "rows", [P, 2, NODES], F32, all_banks, "store_" + name)
            else:
                step("store_" + name + "_0", names(name + "_0*"), store(0))
                step("store_" + name + "_1", names(name + "_1*"), store(1))
                later = max(names(name + "_*"), key=store_order.index)
                ring_tile("rows_" + name, "rows", [P, 2, NODES], F32, all_banks, "store_" + later)

        def tap(k, a):
            def needs(i, h):
                back = ["q_dxt0", "q_dxt1", "q_st0%d" % h, "q_st1%d" % h] if k == 2 else []
                return ["q_w%d" % k, "q_dpre%d" % (2 * h), "q_dpre%d" % (2 * h + 1)] + back

            def passes(i, h):
                features = block(2 * i + a if k == 1 else 2 * a + i)
                back = [(dx3t_q[g], features, E5M2, st_q[g][h], half(0), E4M3) for g in range(2)] if k == 2 else []
                return [(w_q[k], features, E4M3, dpre_q, half(h), E5M2)] + back

            if k == 1:
                target = out_0[0, k, quarter(a), :].rearrange("(p i) n -> p i n", i=2)
            else:
                target = by_four(out_0[0, k, :, :])[:, two(a), :]
            row_pair("tap%d%d" % (k, a), target, needs, passes)

        def shift(g):
            row_pair(
                "shift%d" % g,
                out_1[0, quarter(g), :].rearrange("(i p) n -> p i n", i=2),
                lambda i, h: ["q_xh%d" % (2 * g + i), "q_dx%d" % h, "q_dh%d" % h],
                lambda i, h: [(xh_q[2 * g + i], block(s), E4M3, d3_q[s][h], half(0), E5M2) for s in (X, H)],
            )

        for i in range(8):
            nodes(i)
        for k in range(TAPS + 1):
            weight(k)
        for h in range(2):
            dx3_transposed(h)
            first_mask = ["mask%d%d" % (q, u) for q in (2 * h, 2 * h + 1) for u in range(2)]
            ring_tile("dpre_pairs%d" % h, "pairs", [P, 2, HALF, 2], BF16, first_mask, "dpre%d" % (2 * h + 1))
            ring_tile("dh3_pairs%d" % h, "pairs", [P, 2, HALF, 2], BF16, d3_banks(H, h), "dh%d" % h)
            for k in range(LAST_TAP):
                tap(k, h)
            for s in (X, H):
                d3_group(s, h)
                s_transposed(s, h)
        for q in range(4):
            dpre(q)
            shift(q)
            for s in (X, H):
                for u in range(2):
                    d3(s, q, u)

        queues = [
            vector_order,
            scalar_order,
            ["fill_" + name for name in tensor_order],
            ["store_" + name for name in store_order],
            gpsimd_order,
        ]
        free = {ring: list(range(count)) for ring, count in BUFFERS.items()}
        slot_of = {}
        bank_of = {}
        done = set()
        heads = [0] * len(queues)

        def ready(name):
            if not all(need in done for need in steps[name][0]):
                return False
            if name in takes and takes[name][0] not in held and len(free[takes[name][1]]) == 0:
                return False
            return name not in follows or follows[name] in done

        def run(name):
            if name in takes and takes[name][0] not in held:
                tile_name, ring, shape, dtype = takes[name]
                slot_of[tile_name] = free[ring].pop(0)
                held[tile_name] = rings.tile(shape, dtype, name=ring + str(slot_of[tile_name]), align_bytes=64)
            if name.startswith("fill_"):
                bank_of[name[5:]] = bank_of[follows[name]] if name in follows else len(bank_of)
                held["bank_" + name[5:]] = psum.tile([P, *banks[name[5:]]], F32, name="bank%d" % bank_of[name[5:]])
            steps[name][1]()
            for tile_name, ring in frees.get(name, []):
                free[ring].append(slot_of[tile_name])
            done.add(name)

        follows = dict(zip(queues[2][8:], [name for name in bank_order if name in banks]))
        with tc.manual_schedule():
            for turn in range(len(steps)):
                for n, queue in enumerate(queues):
                    if heads[n] < len(queue) and ready(queue[heads[n]]):
                        run(queue[heads[n]])
                        heads[n] = heads[n] + 1
        assert len(done) == len(steps), [queue[n:] for queue, n in zip(queues, heads)]
